import numpy as np
import ml_dtypes


def mxq(x, axis, fmt="e4m3"):
    dtype, down = {"e4m3": (ml_dtypes.float8_e4m3fn, 7), "e5m2": (ml_dtypes.float8_e5m2, 14)}[fmt]
    v = np.moveaxis(np.asarray(x, np.float32).astype(ml_dtypes.bfloat16).astype(np.float64), axis, -1)
    blocks = v.reshape(v.shape[:-1] + (-1, 32))
    amax = np.abs(blocks).max(-1, keepdims=True)
    byte = np.maximum(np.where(amax > 0, np.frexp(amax)[1] - 1 + 127, 0) - down, 1)
    scale = np.exp2(byte - 127.0)
    codes = (blocks / scale).astype(np.float32).astype(dtype).astype(np.float64)
    return np.moveaxis((codes * scale).reshape(v.shape), -1, axis)


WIDE = False


def mx_kscale(k):
    if not WIDE:
        return np.ones(k)
    levels = np.array([10, -10, 5, -5, 0])
    a = np.random.permutation(np.resize(levels, k // 512 * 4)).reshape(k // 512, 4)
    idx = np.arange(k)
    return np.exp2(a[idx // 512, idx % 128 // 32])


BF16 = ml_dtypes.bfloat16


def bf(x):
    return np.asarray(x, np.float32).astype(BF16)


def f64(x):
    return np.asarray(x).astype(np.float64)


E2M1 = np.array([0.0, 0.5, 1.0, 1.5, 2.0, 3.0, 4.0, 6.0, -0.0, -0.5, -1.0, -1.5, -2.0, -3.0, -4.0, -6.0])


def pack_weight(w, fmt):
    k, n = w.shape
    w = f64(bf(w)).reshape(k // 32, 32, n)
    amax = np.abs(w).max(1)
    if fmt == "e4m3":
        byte = np.frexp(amax)[1] - 1 + 127 - 7
    else:
        mant, ex = np.frexp(amax / 6.0)
        byte = np.where(mant > 0.5, ex, ex - 1) + 127
    byte = np.clip(np.where(amax > 0, byte, 1), 1, 254)
    scaled = (w * np.exp2(127.0 - byte)[:, None, :]).reshape(k, n).astype(np.float32)
    by_word = np.ascontiguousarray(scaled.reshape(k // 512, 128, 4, n).transpose(0, 1, 3, 2))
    if fmt == "e4m3":
        words = by_word.astype(ml_dtypes.float8_e4m3fn).view(np.uint8)
    else:
        c = by_word.astype(ml_dtypes.float4_e2m1fn).view(np.uint8) & 0xF
        words = c[..., 0::2] | (c[..., 1::2] << 4)
    return np.ascontiguousarray(words), np.ascontiguousarray(byte.astype(np.uint8).reshape(k // 512, 16, n))


def unpack_weight(words, scales, fmt):
    g, p, n, _ = words.shape
    if fmt == "e4m3":
        vals = np.ascontiguousarray(words).view(ml_dtypes.float8_e4m3fn).astype(np.float64)
    else:
        nib = np.empty((g, p, n, 4), np.uint8)
        nib[..., 0::2] = words & 0xF
        nib[..., 1::2] = words >> 4
        vals = E2M1[nib]
    vals = vals * np.repeat(np.exp2(scales.astype(np.float64) - 127.0), 8, axis=1)[..., None]
    return vals.transpose(0, 1, 3, 2).reshape(g * 512, n)


B, D, H, NH, P, KC = 256, 2048, 2048, 4, 2560, 4
DI = D // NH
DH = H // NH
FMT = "e4m3"


def silu(v):
    return v / (1.0 + np.exp(-v))


def sigmoid(v):
    return 1.0 / (1.0 + np.exp(-v))


def layer_norm(v, g, b):
    mu = v.mean(-1, keepdims=True)
    var = ((v - mu) ** 2).mean(-1, keepdims=True)
    return (v - mu) / np.sqrt(var + 1e-5) * g + b


def heads(v):
    return v.reshape(v.shape[0], NH, -1).transpose(1, 0, 2)


def block_linear(vq, words, scales, b):
    y = vq @ unpack_weight(words, scales, FMT).reshape(NH, vq.shape[2], DH)
    return y.transpose(1, 0, 2).reshape(y.shape[1], H) + f64(b)


def setup_inputs():
    rn = np.random.standard_normal
    s = mx_kscale(DH)
    sw, sr = 0.7 / np.sqrt(DI), 0.7 / np.sqrt(DH)
    inp = {
        "x": bf(rn((B, D)) * (0.7 + 0.6 * np.random.random((B, 1))) + 0.3 * rn((B, 1))),
        "h_prev": bf(rn((B, H)) * np.tile(s, NH)),
        "c_prev": bf(rn((B, H))),
        "n_prev": bf(0.5 + np.random.random((B, H))),
        "m_prev": bf(rn((B, H)) * 0.5),
        "ln_g": bf(1.0 + 0.1 * rn(D)),
        "ln_b": bf(0.3 * rn(D)),
        "conv_w": bf((0.35 + 0.3 * np.random.random(KC)) * np.sign(rn(KC))),
        "conv_b": bf(0.3 + 0.05 * rn(1)),
    }
    for nm in ("wz", "wi", "wf", "wo"):
        stack = rn((NH, DI, DH)) * sw
        words, scales = pack_weight(stack.reshape(-1, DH), FMT)
        inp[nm + "_w_words"] = words
        inp[nm + "_w_scales"] = scales
        inp[nm + "_b"] = bf(rn(H) * 0.2)
    for nm in ("rz", "ri", "rf", "ro"):
        stack = rn((NH, DH, DH)) * sr / s[None, :, None]
        words, scales = pack_weight(stack.reshape(-1, DH), FMT)
        inp[nm + "_w_words"] = words
        inp[nm + "_w_scales"] = scales
        inp[nm + "_b"] = bf(rn(H) * 0.2)
    return inp


def reference(x, h_prev, c_prev, n_prev, m_prev, ln_g, ln_b, conv_w, conv_b,
              wz_w_words, wz_w_scales, wz_b, wi_w_words, wi_w_scales, wi_b,
              wf_w_words, wf_w_scales, wf_b, wo_w_words, wo_w_scales, wo_b,
              rz_w_words, rz_w_scales, rz_b, ri_w_words, ri_w_scales, ri_b,
              rf_w_words, rf_w_scales, rf_b, ro_w_words, ro_w_scales, ro_b):
    x, cw = f64(x), f64(conv_w)
    x_norm = layer_norm(x, f64(ln_g), f64(ln_b))
    xp = np.pad(x_norm, ((0, 0), (KC - 1, 0)))
    xc = f64(conv_b) + sum(cw[k] * xp[:, k:k + D] for k in range(KC))
    x_conv = silu(xc)

    xq = mxq(heads(x), 2, "e4m3")
    cq = mxq(heads(x_conv), 2, "e4m3")
    hq = mxq(heads(f64(h_prev)), 2, "e4m3")

    z = np.tanh(block_linear(xq, wz_w_words, wz_w_scales, wz_b) + block_linear(hq, rz_w_words, rz_w_scales, rz_b))
    o = sigmoid(block_linear(xq, wo_w_words, wo_w_scales, wo_b) + block_linear(hq, ro_w_words, ro_w_scales, ro_b))
    i_tilde = block_linear(cq, wi_w_words, wi_w_scales, wi_b) + block_linear(hq, ri_w_words, ri_w_scales, ri_b)
    f_tilde = block_linear(cq, wf_w_words, wf_w_scales, wf_b) + block_linear(hq, rf_w_words, rf_w_scales, rf_b)

    m_t = np.maximum(f_tilde + f64(m_prev), i_tilde)
    i_g = np.exp(i_tilde - m_t)
    f_g = np.exp(f_tilde + f64(m_prev) - m_t)
    c_t = f_g * f64(c_prev) + i_g * z
    n_t = f_g * f64(n_prev) + i_g
    h_t = o * c_t / (n_t + 1e-6)
    return (h_t, c_t, n_t, m_t)

@@ -1,0 +1,396 @@
+from contextlib import ExitStack
+
+import concourse.mybir as mybir
+from concourse.masks import make_identity
+
+F32 = mybir.dt.float32
+BF16 = mybir.dt.bfloat16
+I32 = mybir.dt.int32
+U32 = mybir.dt.uint32
+U8 = mybir.dt.uint8
+FP8X4 = mybir.dt.float8_e4m3fn_x4
+ACT = mybir.ActivationFunctionType
+ALU = mybir.AluOpType
+
+P = 128
+PACK = 4
+ROWS = 256
+ROW_TILES = ROWS // P
+FEATURES = 2048
+HEADS = 4
+HEAD = FEATURES // HEADS
+BLOCKS = HEAD // P
+CHUNKS = HEADS * ROW_TILES
+TAPS = 4
+PAD = 4
+AHEAD = 2
+
+WEIGHTS = ("wz", "wi", "wf", "wo", "rz", "ri", "rf", "ro")
+GATES = ("z", "i", "f", "o")
+GATE_FUNC = {"z": ACT.Tanh, "i": ACT.Identity, "f": ACT.Identity, "o": ACT.Tanh}
+GATE_SCALE = {"z": 1.0, "i": 1.0, "f": -1.0, "o": 0.5}
+
+FLOPS = 2 * len(WEIGHTS) * ROWS * FEATURES * HEAD
+
+
+def tile_slstmblock_pa_e_kernel(
+    tc, x, h_prev, c_prev, n_prev, m_prev, ln_g, ln_b, conv_w, conv_b,
+    wz_w_words, wz_w_scales, wz_b, wi_w_words, wi_w_scales, wi_b,
+    wf_w_words, wf_w_scales, wf_b, wo_w_words, wo_w_scales, wo_b,
+    rz_w_words, rz_w_scales, rz_b, ri_w_words, ri_w_scales, ri_b,
+    rf_w_words, rf_w_scales, rf_b, ro_w_words, ro_w_scales, ro_b,
+    out_0, out_1, out_2, out_3,
+):
+    nc = tc.nc
+    word_bytes = {"wz": wz_w_words, "wi": wi_w_words, "wf": wf_w_words, "wo": wo_w_words,
+                  "rz": rz_w_words, "ri": ri_w_words, "rf": rf_w_words, "ro": ro_w_words}
+    scale_bytes = {"wz": wz_w_scales, "wi": wi_w_scales, "wf": wf_w_scales, "wo": wo_w_scales,
+                   "rz": rz_w_scales, "ri": ri_w_scales, "rf": rf_w_scales, "ro": ro_w_scales}
+    biases = {"wz": wz_b, "wi": wi_b, "wf": wf_b, "wo": wo_b,
+              "rz": rz_b, "ri": ri_b, "rf": rf_b, "ro": ro_b}
+
+    with ExitStack() as ctx:
+        ctx.enter_context(tc.manual_schedule())
+        keep = ctx.enter_context(tc.tile_pool(name="keep", bufs=1))
+        ring = ctx.enter_context(tc.tile_pool(name="ring", bufs=2))
+        psum = ctx.enter_context(tc.psum_pool(name="psum", bufs=1))
+
+        planes = keep.tile([P, len(WEIGHTS), HEAD], U8, name="planes", align_bytes=64)
+        words_sb = {}
+        for name in WEIGHTS:
+            words_sb[name] = keep.tile([P, HEADS, HEAD], U32, name="words_" + name, align_bytes=64)
+        codes = {}
+        scales = {}
+        for name in ("x", "h", "c"):
+            codes[name] = keep.tile([P, HEADS * ROWS], U32, name="codes_" + name, align_bytes=64)
+            scales[name] = keep.tile([P, HEADS * ROWS], U8, name="scales_" + name, align_bytes=64)
+        m_sb = keep.tile([P, ROW_TILES, FEATURES], BF16, name="m_sb")
+        cn_sb = keep.tile([P, ROW_TILES, HEADS, 2, HEAD], BF16, name="cn_sb")
+        ident_f32 = keep.tile([P, P], F32, name="ident_f32")
+        ident_bf16 = keep.tile([P, P], BF16, name="ident_bf16")
+        minus_ident = keep.tile([P, P], BF16, name="minus_ident")
+        bias_rows = keep.tile([P, P], BF16, name="bias_rows")
+        bias_t = keep.tile([P, 2, len(GATES), HEADS * BLOCKS], F32, name="bias_t")
+        bias_cols = keep.tile([P, len(GATES), HEADS * BLOCKS], F32, name="bias_cols")
+        tap_coef = keep.tile([P, 1], BF16, name="tap_coef")
+        gain_pick = keep.tile([P, 1], BF16, name="gain_pick")
+        taps_bf16 = keep.tile([P, TAPS], BF16, name="taps_bf16")
+        stats = keep.tile([P, ROW_TILES, HEADS, 6], F32, name="stats")
+        mean_var = keep.tile([P, ROW_TILES, 2], F32, name="mean_var")
+        var_eps = keep.tile([P, ROW_TILES], F32, name="var_eps")
+        std = keep.tile([P, ROW_TILES], F32, name="std")
+        rstd = keep.tile([P, ROW_TILES], F32, name="rstd")
+        taps_rstd = keep.tile([P, ROW_TILES, TAPS], F32, name="taps_rstd")
+        two_eps = keep.tile([P, 1], F32, name="two_eps")
+        warm_in = keep.tile([P, 1], F32, name="warm_in")
+        warm_sqrt = keep.tile([P, 1], F32, name="warm_sqrt")
+        warm_silu = keep.tile([P, 1], F32, name="warm_silu")
+
+        def chunk_rows_cols(c):
+            g, r = divmod(c, ROW_TILES)
+            return g, r, slice(r * P, (r + 1) * P), slice(g * HEAD, (g + 1) * HEAD)
+
+        def mx_pass(acc, name, operand, g, j, start, stop):
+            cols = slice(j * P, (j + 1) * P)
+            batch = slice(g * ROWS, (g + 1) * ROWS)
+            nc.tensor.matmul_mx(
+                out=acc,
+                lhsT=words_sb[name][:, g, cols].bitcast(FP8X4),
+                lhsT_scale=planes[PACK * g:P, WEIGHTS.index(name), cols],
+                rhs=codes[operand][:, batch].bitcast(FP8X4),
+                rhs_scale=scales[operand][:, batch],
+                start=start,
+                stop=stop,
+            )
+
+        gate_t = {}
+
+        def gates(g, names):
+            for gate in names:
+                operand = "x" if gate in ("z", "o") else "c"
+                out_t = ring.tile([P, BLOCKS, ROWS], F32, name="gate_t_" + gate, tag="gate_t_" + gate)
+                gate_t[(gate, g)] = out_t
+                for pair in range(BLOCKS // 2):
+                    acc = psum.tile([P, 2, ROWS], F32, name="acc", tag="acc", bufs=2)
+                    for s in range(2):
+                        j = 2 * pair + s
+                        mx_pass(acc[:, s, :], "w" + gate, operand, g, j, True, False)
+                        mx_pass(acc[:, s, :], "r" + gate, "h", g, j, False, True)
+                    for s in range(2):
+                        j = 2 * pair + s
+                        col = g * BLOCKS + j
+                        nc.scalar.activation(
+                            out=out_t[:, j, :], in_=acc[:, s, :], func=GATE_FUNC[gate],
+                            bias=bias_cols[:, GATES.index(gate), col:col + 1], scale=GATE_SCALE[gate],
+                        )
+
+        def quantise(grouped, name, g):
+            batch = slice(g * ROWS, (g + 1) * ROWS)
+            nc.vector.quantize_mx(
+                out=codes[name][:, batch].bitcast(FP8X4),
+                scales=scales[name][:, batch],
+                in_=grouped[:].rearrange("p b t -> p (b t)"),
+            )
+
+        with tc.tile_pool(name="pre", bufs=1) as pre:
+            x_sb = pre.tile([P, ROW_TILES, FEATURES], BF16, name="x_sb")
+            h_sb = pre.tile([P, ROW_TILES, FEATURES], BF16, name="h_sb")
+            vec_rows = pre.tile([P, FEATURES], BF16, name="vec_rows")
+            centred = pre.tile([P, ROW_TILES, PAD + FEATURES], F32, name="centred")
+
+            nc.vector.memset(vec_rows[:], 0.0)
+            nc.vector.memset(vec_rows[32:33, :], 1.0)
+            nc.vector.memset(tap_coef[:], 0.0)
+            nc.vector.memset(gain_pick[:], 0.0)
+            nc.vector.memset(gain_pick[64:65, :], 1.0)
+            nc.vector.memset(warm_in[:], 1.0)
+            nc.vector.memset(planes[:].rearrange("p w n -> p (w n)").bitcast(I32), 0)
+            nc.vector.memset(centred[:, :, 0:PAD], 0.0)
+            nc.vector.memset(two_eps[:], 2.0e-6)
+
+            make_identity(nc, ident_f32[:])
+            make_identity(nc, ident_bf16[:])
+
+            for r in range(ROW_TILES):
+                nc.sync.dma_start(out=x_sb[:, r, :], in_=x[r * P:(r + 1) * P, :])
+            nc.scalar.dma_start(out=vec_rows[64:65, :], in_=ln_g.rearrange("(o d) -> o d", o=1))
+            nc.scalar.dma_start(out=taps_bf16[:], in_=conv_w.partition_broadcast(P))
+            nc.scalar.dma_start(out=tap_coef[0:TAPS, :], in_=conv_w.rearrange("(k o) -> k o", o=1))
+            nc.scalar.dma_start(out=tap_coef[32:33, :], in_=conv_b.rearrange("(k o) -> k o", o=1))
+            for j in range(TAPS):
+                shift = TAPS - 1 - j
+                nc.scalar.dma_start(
+                    out=vec_rows[j:j + 1, shift:FEATURES],
+                    in_=ln_b.rearrange("(o d) -> o d", o=1)[:, 0:FEATURES - shift],
+                )
+            for i, name in enumerate(WEIGHTS):
+                nc.gpsimd.dma_start(
+                    out=bias_rows[16 * i:16 * (i + 1), :],
+                    in_=biases[name].rearrange("(c f) -> c f", f=P),
+                )
+            for r in range(ROW_TILES):
+                nc.sync.dma_start(out=h_sb[:, r, :], in_=h_prev[r * P:(r + 1) * P, :])
+
+            def load_planes(name):
+                w = WEIGHTS.index(name)
+                for quad in range(4):
+                    nc.sync.dma_start(
+                        out=planes[32 * quad:32 * quad + 16, w, :].bitcast(I32),
+                        in_=scale_bytes[name][:, PACK * quad:PACK * (quad + 1), :].bitcast(I32),
+                    )
+
+            def load_words(name, g):
+                nc.sync.dma_start(
+                    out=words_sb[name][:, g, :].bitcast(I32),
+                    in_=word_bytes[name][g].rearrange("p n t -> p (n t)").bitcast(I32),
+                )
+
+            for name in WEIGHTS:
+                load_planes(name)
+            for name in WEIGHTS:
+                load_words(name, 0)
+            for r in range(ROW_TILES):
+                nc.sync.dma_start(out=m_sb[:, r, :], in_=m_prev[r * P:(r + 1) * P, :])
+            for name in WEIGHTS:
+                load_words(name, 1)
+            for r in range(ROW_TILES):
+                for s, state in enumerate((c_prev, n_prev)):
+                    nc.sync.dma_start(
+                        out=cn_sb[:, r, :, s, :],
+                        in_=state[r * P:(r + 1) * P, :].rearrange("p (g f) -> p g f", g=HEADS),
+                    )
+            for g in range(2, HEADS):
+                for name in WEIGHTS:
+                    load_words(name, g)
+
+            nc.scalar.activation(out=warm_sqrt[:], in_=warm_in[:], func=ACT.Sqrt)
+
+            gain_bank = {}
+            shift_bank = {}
+
+            def spread_vectors(g):
+                cols = slice(g * HEAD, (g + 1) * HEAD)
+                gain_bank[g] = psum.tile([P, HEAD], F32, name="gain_bank", tag="z" if g % 2 == 0 else "d")
+                shift_bank[g] = psum.tile([P, HEAD], F32, name="shift_bank", tag="o" if g % 2 == 0 else "a")
+                nc.tensor.matmul(out=gain_bank[g][:], lhsT=gain_pick[:].to_broadcast([P, P]),
+                                 rhs=vec_rows[:, cols], start=True, stop=True)
+                nc.tensor.matmul(out=shift_bank[g][:], lhsT=tap_coef[:].to_broadcast([P, P]),
+                                 rhs=vec_rows[:, cols], start=True, stop=True)
+
+            spread_vectors(0)
+            spread_vectors(1)
+
+            def words_to_partitions(src, g):
+                bank = psum.tile([P, 2, ROWS], F32, name="word_bank", tag="turn", bufs=2)
+                for r in range(ROW_TILES):
+                    src_words = src[:, r, :].bitcast(F32)
+                    for u in range(2):
+                        nc.tensor.transpose(
+                            out=bank[:, u, r * P:(r + 1) * P],
+                            in_=src_words[:, (HEAD // 2) * g + u:(HEAD // 2) * (g + 1):2],
+                            identity=ident_f32[:],
+                        )
+                grouped = pre.tile([P, ROWS, PACK], BF16, name="grouped", tag="grouped", bufs=4,
+                                   align_bytes=64)
+                nc.scalar.copy(out=grouped[:].bitcast(F32), in_=bank[:].rearrange("p u b -> p b u"))
+                return grouped
+
+            grouped_x = [words_to_partitions(x_sb, g) for g in range(HEADS)]
+
+            for r in range(ROW_TILES):
+                for g in range(HEADS):
+                    nc.vector.bn_stats(out=stats[:, r, g, :], in_=x_sb[:, r, g * HEAD:(g + 1) * HEAD])
+            for r in range(ROW_TILES):
+                nc.vector.bn_aggr(out=mean_var[:, r, :], in_=stats[:, r, :, :].rearrange("p g s -> p (g s)"))
+            nc.vector.tensor_scalar_add(out=var_eps[:], in0=mean_var[:, :, 1], scalar1=1.0e-5)
+            nc.scalar.activation(out=std[:], in_=var_eps[:], func=ACT.Sqrt)
+            nc.scalar.activation(out=warm_silu[:], in_=warm_in[:], func=ACT.Silu)
+            for g in range(HEADS):
+                quantise(grouped_x[g], "x", g)
+            nc.vector.reciprocal(out=rstd[:], in_=std[:])
+            for r in range(ROW_TILES):
+                nc.vector.tensor_scalar_mul(out=taps_rstd[:, r, :], in0=taps_bf16[:], scalar1=rstd[:, r:r + 1])
+
+            grouped_h = [words_to_partitions(h_sb, g) for g in range(HEADS)]
+
+            bias_bank = psum.tile([P, P], BF16, name="bias_bank", tag="turn", bufs=2)
+            nc.tensor.transpose(out=bias_bank[:], in_=bias_rows[:], identity=ident_bf16[:])
+
+            def conv_head(g):
+                cols = slice(g * HEAD, (g + 1) * HEAD)
+                for r in range(ROW_TILES):
+                    nc.vector.scalar_tensor_tensor(
+                        out=centred[:, r, PAD + g * HEAD:PAD + (g + 1) * HEAD],
+                        in0=x_sb[:, r, cols], scalar=mean_var[:, r, 0:1], in1=gain_bank[g][:],
+                        op0=ALU.subtract, op1=ALU.mult,
+                    )
+                sums = [pre.tile([P, HEAD], F32, name="conv_sum", tag="conv_sum", bufs=2)
+                        for r in range(ROW_TILES)]
+                planes_t = [pre.tile([P, PACK, P], F32, name="conv_planes", tag="conv_planes", bufs=2)
+                            for r in range(ROW_TILES)]
+                for j in range(TAPS):
+                    first = PAD + g * HEAD + j - (TAPS - 1)
+                    for r in range(ROW_TILES):
+                        moved = centred[:, r, first:first + HEAD]
+                        coef = taps_rstd[:, r, j:j + 1]
+                        if j == 0:
+                            nc.vector.scalar_tensor_tensor(
+                                out=sums[r][:], in0=moved, scalar=coef, in1=shift_bank[g][:],
+                                op0=ALU.mult, op1=ALU.add)
+                        elif j < TAPS - 1:
+                            nc.vector.scalar_tensor_tensor(
+                                out=sums[r][:], in0=moved, scalar=coef, in1=sums[r][:],
+                                op0=ALU.mult, op1=ALU.add)
+                        else:
+                            nc.vector.scalar_tensor_tensor(
+                                out=planes_t[r][:].rearrange("p t q -> p q t"),
+                                in0=moved.rearrange("p (q t) -> p q t", t=PACK), scalar=coef,
+                                in1=sums[r][:].rearrange("p (q t) -> p q t", t=PACK),
+                                op0=ALU.mult, op1=ALU.add)
+                    if j == 0 and g + 2 < HEADS:
+                        spread_vectors(g + 2)
+                grouped = pre.tile([P, ROWS, PACK], BF16, name="grouped_c", tag="grouped_c", bufs=2,
+                                   align_bytes=64)
+                for r in range(ROW_TILES):
+                    bank = psum.tile([P, PACK, P], F32, name="conv_bank", tag="turn", bufs=2)
+                    for t in range(PACK):
+                        nc.tensor.transpose(out=bank[:, t, :], in_=planes_t[r][:, t, :], identity=ident_f32[:])
+                    nc.scalar.activation(out=grouped[:, r * P:(r + 1) * P, :],
+                                         in_=bank[:].rearrange("p t b -> p b t"), func=ACT.Silu)
+                return grouped
+
+            grouped_c = {0: conv_head(0)}
+            nc.vector.tensor_copy(out=bias_t[:].rearrange("p s q c -> p (s q c)"), in_=bias_bank[:])
+            nc.vector.tensor_tensor(out=bias_cols[:], in0=bias_t[:, 0, :, :], in1=bias_t[:, 1, :, :], op=ALU.add)
+            for gate in ("f", "o"):
+                q = GATES.index(gate)
+                nc.vector.tensor_scalar_mul(out=bias_cols[:, q, :], in0=bias_cols[:, q, :],
+                                            scalar1=GATE_SCALE[gate])
+            nc.vector.tensor_scalar_mul(out=minus_ident[:], in0=ident_bf16[:], scalar1=-1.0)
+            for g in range(HEADS):
+                quantise(grouped_h[g], "h", g)
+            for g in range(1, HEADS):
+                grouped_c[g] = conv_head(g)
+                quantise(grouped_c[g - 1], "c", g - 1)
+                if g - 1 < AHEAD:
+                    gates(g - 1, ("i", "f", "z", "o"))
+            quantise(grouped_c[HEADS - 1], "c", HEADS - 1)
+
+        with tc.tile_pool(name="late", bufs=1, reuse_waits="tile") as late:
+            n_all = late.tile([P, CHUNKS, HEAD], F32, name="n_all")
+            oc_all = late.tile([P, CHUNKS, HEAD], F32, name="oc_all")
+            recip_all = late.tile([P, CHUNKS, HEAD], F32, name="recip_all")
+            relus = {}
+            exps = {}
+
+            def back_to_rows(bank, gate, g, r, start, stop):
+                for j in range(BLOCKS):
+                    nc.tensor.matmul(
+                        out=bank[:, j * P:(j + 1) * P], lhsT=gate_t[(gate, g)][:, j, r * P:(r + 1) * P],
+                        rhs=ident_f32[:], is_transpose=True, start=start, stop=stop and j == BLOCKS - 1,
+                    )
+
+            def difference(c):
+                g, r, rows, cols = chunk_rows_cols(c)
+                d_bank = psum.tile([P, HEAD], F32, name="d_bank", tag="d")
+                nc.tensor.matmul(out=d_bank[:], lhsT=minus_ident[:], rhs=m_sb[:, r, cols], start=True, stop=False)
+                back_to_rows(d_bank, "i", g, r, False, False)
+                back_to_rows(d_bank, "f", g, r, False, True)
+                relus[c] = ring.tile([P, 2, HEAD], F32, name="relus", tag="relus")
+                nc.scalar.activation(out=relus[c][:, 0, :], in_=d_bank[:], func=ACT.Relu, scale=-1.0)
+                nc.scalar.activation(out=relus[c][:, 1, :], in_=d_bank[:], func=ACT.Relu, scale=1.0)
+
+            def gate_exps(c):
+                exps[c] = ring.tile([P, 2, HEAD], F32, name="exps", tag="exps")
+                nc.scalar.activation(out=exps[c][:], in_=relus[c][:], func=ACT.Exp, scale=-1.0)
+
+            def update(c):
+                g, r, rows, cols = chunk_rows_cols(c)
+                banks = {}
+                for gate, tag in (("i", "a"), ("z", "z"), ("o", "o")):
+                    banks[gate] = psum.tile([P, HEAD], F32, name="bank_" + gate, tag=tag)
+                    for j in range(BLOCKS):
+                        nc.tensor.transpose(out=banks[gate][:, j * P:(j + 1) * P],
+                                            in_=gate_t[(gate, g)][:, j, r * P:(r + 1) * P],
+                                            identity=ident_f32[:])
+                ig = exps[c][:, 0, :]
+                kept = ring.tile([P, 2, HEAD], F32, name="kept", tag="kept", bufs=1)
+                nc.vector.tensor_tensor(out=kept[:], in0=exps[c][:, 1:2, :].to_broadcast([P, 2, HEAD]),
+                                        in1=cn_sb[:, r, g, :, :], op=ALU.mult)
+                fresh = ring.tile([P, HEAD], F32, name="fresh", tag="fresh", bufs=1)
+                nc.vector.tensor_tensor(out=fresh[:], in0=banks["z"][:], in1=ig, op=ALU.mult)
+                nc.vector.tensor_tensor(out=n_all[:, c, :], in0=kept[:, 1, :], in1=ig, op=ALU.add)
+                nc.sync.dma_start(out=out_2[rows, cols], in_=n_all[:, c, :])
+                c_t = ring.tile([P, HEAD], F32, name="c_t", tag="c_t")
+                nc.vector.tensor_tensor(out=c_t[:], in0=kept[:, 0, :], in1=fresh[:], op=ALU.add)
+                nc.sync.dma_start(out=out_1[rows, cols], in_=c_t[:])
+                m_t = ring.tile([P, HEAD], F32, name="m_t", tag="m_t")
+                nc.vector.tensor_tensor(out=m_t[:], in0=banks["i"][:], in1=relus[c][:, 0, :], op=ALU.add)
+                nc.sync.dma_start(out=out_3[rows, cols], in_=m_t[:])
+                nc.vector.scalar_tensor_tensor(out=oc_all[:, c, :], in0=banks["o"][:], scalar=1.0, in1=c_t[:],
+                                               op0=ALU.add, op1=ALU.mult)
+
+            difference(0)
+            difference(1)
+            gate_exps(0)
+            for c in range(CHUNKS):
+                g, r = divmod(c, ROW_TILES)
+                if c + 1 < CHUNKS:
+                    gate_exps(c + 1)
+                update(c)
+                if r == 1 and g + AHEAD < HEADS:
+                    gates(g + AHEAD, ("i", "f"))
+                if r == 0 and AHEAD <= g + 1 < HEADS:
+                    gates(g + 1, ("z", "o"))
+                if c + 2 < CHUNKS:
+                    difference(c + 2)
+
+            for c in range(CHUNKS):
+                nc.scalar.activation(out=recip_all[:, c, :], in_=n_all[:, c, :], func=ACT.Ln,
+                                     bias=two_eps[:, 0:1], scale=2.0)
+            for c in range(CHUNKS):
+                g, r, rows, cols = chunk_rows_cols(c)
+                nc.scalar.activation(out=recip_all[:, c, :], in_=recip_all[:, c, :], func=ACT.Exp, scale=-1.0)
+                nc.vector.tensor_tensor(out=oc_all[:, c, :], in0=oc_all[:, c, :], in1=recip_all[:, c, :],
+                                        op=ALU.mult)
+                nc.sync.dma_start(out=out_0[rows, cols], in_=oc_all[:, c, :])

@@ -23,7 +23,6 @@ BLOCKS = HEAD // P
 CHUNKS = HEADS * ROW_TILES
 TAPS = 4
 PAD = 4
-AHEAD = 2
 
 WEIGHTS = ("wz", "wi", "wf", "wo", "rz", "ri", "rf", "ro")
 GATES = ("z", "i", "f", "o")
@@ -52,18 +51,19 @@ def tile_slstmblock_pa_e_kernel(
     with ExitStack() as ctx:
         ctx.enter_context(tc.manual_schedule())
         keep = ctx.enter_context(tc.tile_pool(name="keep", bufs=1))
+        stream = ctx.enter_context(tc.tile_pool(name="stream", bufs=2))
         ring = ctx.enter_context(tc.tile_pool(name="ring", bufs=2))
         psum = ctx.enter_context(tc.psum_pool(name="psum", bufs=1))
 
         planes = keep.tile([P, len(WEIGHTS), HEAD], U8, name="planes", align_bytes=64)
-        words_sb = {}
-        for name in WEIGHTS:
-            words_sb[name] = keep.tile([P, HEADS, HEAD], U32, name="words_" + name, align_bytes=64)
         codes = {}
         scales = {}
         for name in ("x", "h", "c"):
             codes[name] = keep.tile([P, HEADS * ROWS], U32, name="codes_" + name, align_bytes=64)
             scales[name] = keep.tile([P, HEADS * ROWS], U8, name="scales_" + name, align_bytes=64)
+        gate_t = {}
+        for gate in GATES:
+            gate_t[gate] = keep.tile([P, HEADS, BLOCKS, ROWS], F32, name="gate_t_" + gate)
         m_sb = keep.tile([P, ROW_TILES, FEATURES], BF16, name="m_sb")
         cn_sb = keep.tile([P, ROW_TILES, HEADS, 2, HEAD], BF16, name="cn_sb")
         ident_f32 = keep.tile([P, P], F32, name="ident_f32")
@@ -83,19 +83,36 @@ def tile_slstmblock_pa_e_kernel(
         taps_rstd = keep.tile([P, ROW_TILES, TAPS], F32, name="taps_rstd")
         two_eps = keep.tile([P, 1], F32, name="two_eps")
         warm_in = keep.tile([P, 1], F32, name="warm_in")
-        warm_sqrt = keep.tile([P, 1], F32, name="warm_sqrt")
-        warm_silu = keep.tile([P, 1], F32, name="warm_silu")
+        warm_out = keep.tile([P, 3, 8], F32, name="warm_out")
 
         def chunk_rows_cols(c):
             g, r = divmod(c, ROW_TILES)
             return g, r, slice(r * P, (r + 1) * P), slice(g * HEAD, (g + 1) * HEAD)
+
+        words_sb = {}
+
+        def load_words(name, g):
+            words_sb[(name, g)] = stream.tile([P, HEAD], U32, name="words_" + name, tag="words_" + name,
+                                              align_bytes=64)
+            nc.sync.dma_start(
+                out=words_sb[(name, g)][:].bitcast(I32),
+                in_=word_bytes[name][g].rearrange("p n t -> p (n t)").bitcast(I32),
+            )
+
+        def load_planes(name):
+            w = WEIGHTS.index(name)
+            for quad in range(4):
+                nc.sync.dma_start(
+                    out=planes[32 * quad:32 * quad + 16, w, :].bitcast(I32),
+                    in_=scale_bytes[name][:, PACK * quad:PACK * (quad + 1), :].bitcast(I32),
+                )
 
         def mx_pass(acc, name, operand, g, j, start, stop):
             cols = slice(j * P, (j + 1) * P)
             batch = slice(g * ROWS, (g + 1) * ROWS)
             nc.tensor.matmul_mx(
                 out=acc,
-                lhsT=words_sb[name][:, g, cols].bitcast(FP8X4),
+                lhsT=words_sb[(name, g)][:, cols].bitcast(FP8X4),
                 lhsT_scale=planes[PACK * g:P, WEIGHTS.index(name), cols],
                 rhs=codes[operand][:, batch].bitcast(FP8X4),
                 rhs_scale=scales[operand][:, batch],
@@ -103,13 +120,9 @@ def tile_slstmblock_pa_e_kernel(
                 stop=stop,
             )
 
-        gate_t = {}
-
         def gates(g, names):
             for gate in names:
                 operand = "x" if gate in ("z", "o") else "c"
-                out_t = ring.tile([P, BLOCKS, ROWS], F32, name="gate_t_" + gate, tag="gate_t_" + gate)
-                gate_t[(gate, g)] = out_t
                 for pair in range(BLOCKS // 2):
                     acc = psum.tile([P, 2, ROWS], F32, name="acc", tag="acc", bufs=2)
                     for s in range(2):
@@ -120,9 +133,12 @@ def tile_slstmblock_pa_e_kernel(
                         j = 2 * pair + s
                         col = g * BLOCKS + j
                         nc.scalar.activation(
-                            out=out_t[:, j, :], in_=acc[:, s, :], func=GATE_FUNC[gate],
+                            out=gate_t[gate][:, g, j, :], in_=acc[:, s, :], func=GATE_FUNC[gate],
                             bias=bias_cols[:, GATES.index(gate), col:col + 1], scale=GATE_SCALE[gate],
                         )
+                if g + 2 < HEADS:
+                    load_words("w" + gate, g + 2)
+                    load_words("r" + gate, g + 2)
 
         def quantise(grouped, name, g):
             batch = slice(g * ROWS, (g + 1) * ROWS)
@@ -132,13 +148,39 @@ def tile_slstmblock_pa_e_kernel(
                 in_=grouped[:].rearrange("p b t -> p (b t)"),
             )
 
+        relus = {}
+        exps = {}
+
+        def add_back_to_rows(bank, gate, g, r, stop):
+            for j in range(BLOCKS):
+                nc.tensor.matmul(
+                    out=bank[:, j * P:(j + 1) * P], lhsT=gate_t[gate][:, g, j, r * P:(r + 1) * P],
+                    rhs=ident_f32[:], is_transpose=True, start=False, stop=stop and j == BLOCKS - 1,
+                )
+
+        def difference(c):
+            g, r, rows, cols = chunk_rows_cols(c)
+            d_bank = psum.tile([P, HEAD], F32, name="d_bank", tag="d")
+            nc.tensor.matmul(out=d_bank[:], lhsT=minus_ident[:], rhs=m_sb[:, r, cols], start=True, stop=False)
+            add_back_to_rows(d_bank, "i", g, r, False)
+            add_back_to_rows(d_bank, "f", g, r, True)
+            relus[c] = ring.tile([P, 2, HEAD], F32, name="relus", tag="relus")
+            nc.scalar.activation(out=relus[c][:, 0, :], in_=d_bank[:], func=ACT.Relu, scale=-1.0)
+            nc.scalar.activation(out=relus[c][:, 1, :], in_=d_bank[:], func=ACT.Relu, scale=1.0)
+
+        def gate_exps(c):
+            exps[c] = ring.tile([P, 2, HEAD], F32, name="exps", tag="exps")
+            nc.scalar.activation(out=exps[c][:], in_=relus[c][:], func=ACT.Exp, scale=-1.0)
+
+        grouped_c = {}
+
         with tc.tile_pool(name="pre", bufs=1) as pre:
             x_sb = pre.tile([P, ROW_TILES, FEATURES], BF16, name="x_sb")
             h_sb = pre.tile([P, ROW_TILES, FEATURES], BF16, name="h_sb")
             vec_rows = pre.tile([P, FEATURES], BF16, name="vec_rows")
             centred = pre.tile([P, ROW_TILES, PAD + FEATURES], F32, name="centred")
 
-            nc.vector.memset(vec_rows[:], 0.0)
+            nc.vector.memset(vec_rows[:].bitcast(I32), 0)
             nc.vector.memset(vec_rows[32:33, :], 1.0)
             nc.vector.memset(tap_coef[:], 0.0)
             nc.vector.memset(gain_pick[:], 0.0)
@@ -153,72 +195,46 @@ def tile_slstmblock_pa_e_kernel(
 
             for r in range(ROW_TILES):
                 nc.sync.dma_start(out=x_sb[:, r, :], in_=x[r * P:(r + 1) * P, :])
-            nc.scalar.dma_start(out=vec_rows[64:65, :], in_=ln_g.rearrange("(o d) -> o d", o=1))
-            nc.scalar.dma_start(out=taps_bf16[:], in_=conv_w.partition_broadcast(P))
-            nc.scalar.dma_start(out=tap_coef[0:TAPS, :], in_=conv_w.rearrange("(k o) -> k o", o=1))
-            nc.scalar.dma_start(out=tap_coef[32:33, :], in_=conv_b.rearrange("(k o) -> k o", o=1))
+            nc.sync.dma_start(out=vec_rows[64:65, :], in_=ln_g.rearrange("(o d) -> o d", o=1))
+            nc.sync.dma_start(out=tap_coef[0:TAPS, :], in_=conv_w.rearrange("(k o) -> k o", o=1))
             for j in range(TAPS):
                 shift = TAPS - 1 - j
-                nc.scalar.dma_start(
+                nc.sync.dma_start(
                     out=vec_rows[j:j + 1, shift:FEATURES],
                     in_=ln_b.rearrange("(o d) -> o d", o=1)[:, 0:FEATURES - shift],
                 )
+            nc.sync.dma_start(out=tap_coef[32:33, :], in_=conv_b.rearrange("(k o) -> k o", o=1))
+            nc.sync.dma_start(out=taps_bf16[:], in_=conv_w.partition_broadcast(P))
+            for r in range(ROW_TILES):
+                nc.sync.dma_start(out=h_sb[:, r, :], in_=h_prev[r * P:(r + 1) * P, :])
             for i, name in enumerate(WEIGHTS):
-                nc.gpsimd.dma_start(
+                nc.sync.dma_start(
                     out=bias_rows[16 * i:16 * (i + 1), :],
                     in_=biases[name].rearrange("(c f) -> c f", f=P),
                 )
-            for r in range(ROW_TILES):
-                nc.sync.dma_start(out=h_sb[:, r, :], in_=h_prev[r * P:(r + 1) * P, :])
-
-            def load_planes(name):
-                w = WEIGHTS.index(name)
-                for quad in range(4):
-                    nc.sync.dma_start(
-                        out=planes[32 * quad:32 * quad + 16, w, :].bitcast(I32),
-                        in_=scale_bytes[name][:, PACK * quad:PACK * (quad + 1), :].bitcast(I32),
-                    )
-
-            def load_words(name, g):
-                nc.sync.dma_start(
-                    out=words_sb[name][:, g, :].bitcast(I32),
-                    in_=word_bytes[name][g].rearrange("p n t -> p (n t)").bitcast(I32),
-                )
-
-            for name in WEIGHTS:
+            for name in ("wz", "rz", "wo", "ro"):
                 load_planes(name)
-            for name in WEIGHTS:
-                load_words(name, 0)
-            for r in range(ROW_TILES):
-                nc.sync.dma_start(out=m_sb[:, r, :], in_=m_prev[r * P:(r + 1) * P, :])
-            for name in WEIGHTS:
-                load_words(name, 1)
-            for r in range(ROW_TILES):
-                for s, state in enumerate((c_prev, n_prev)):
-                    nc.sync.dma_start(
-                        out=cn_sb[:, r, :, s, :],
-                        in_=state[r * P:(r + 1) * P, :].rearrange("p (g f) -> p g f", g=HEADS),
-                    )
-            for g in range(2, HEADS):
-                for name in WEIGHTS:
+            for g in range(2):
+                for name in ("wz", "rz", "wo", "ro"):
                     load_words(name, g)
+            for name in ("wi", "ri", "wf", "rf"):
+                load_planes(name)
+            for name in ("wi", "ri", "wf", "rf"):
+                load_words(name, 0)
 
-            nc.scalar.activation(out=warm_sqrt[:], in_=warm_in[:], func=ACT.Sqrt)
+            nc.scalar.activation(out=warm_out[:, 0, 0:1], in_=warm_in[:], func=ACT.Sqrt)
 
             gain_bank = {}
             shift_bank = {}
 
             def spread_vectors(g):
                 cols = slice(g * HEAD, (g + 1) * HEAD)
-                gain_bank[g] = psum.tile([P, HEAD], F32, name="gain_bank", tag="z" if g % 2 == 0 else "d")
-                shift_bank[g] = psum.tile([P, HEAD], F32, name="shift_bank", tag="o" if g % 2 == 0 else "a")
+                gain_bank[g] = psum.tile([P, HEAD], F32, name="gain_bank", tag="d" if g % 2 == 0 else "z")
+                shift_bank[g] = psum.tile([P, HEAD], F32, name="shift_bank", tag="a" if g % 2 == 0 else "o")
                 nc.tensor.matmul(out=gain_bank[g][:], lhsT=gain_pick[:].to_broadcast([P, P]),
                                  rhs=vec_rows[:, cols], start=True, stop=True)
                 nc.tensor.matmul(out=shift_bank[g][:], lhsT=tap_coef[:].to_broadcast([P, P]),
                                  rhs=vec_rows[:, cols], start=True, stop=True)
-
-            spread_vectors(0)
-            spread_vectors(1)
 
             def words_to_partitions(src, g):
                 bank = psum.tile([P, 2, ROWS], F32, name="word_bank", tag="turn", bufs=2)
@@ -235,35 +251,59 @@ def tile_slstmblock_pa_e_kernel(
                 nc.scalar.copy(out=grouped[:].bitcast(F32), in_=bank[:].rearrange("p u b -> p b u"))
                 return grouped
 
-            grouped_x = [words_to_partitions(x_sb, g) for g in range(HEADS)]
-
-            for r in range(ROW_TILES):
+            def row_stats(r):
                 for g in range(HEADS):
                     nc.vector.bn_stats(out=stats[:, r, g, :], in_=x_sb[:, r, g * HEAD:(g + 1) * HEAD])
-            for r in range(ROW_TILES):
                 nc.vector.bn_aggr(out=mean_var[:, r, :], in_=stats[:, r, :, :].rearrange("p g s -> p (g s)"))
-            nc.vector.tensor_scalar_add(out=var_eps[:], in0=mean_var[:, :, 1], scalar1=1.0e-5)
-            nc.scalar.activation(out=std[:], in_=var_eps[:], func=ACT.Sqrt)
-            nc.scalar.activation(out=warm_silu[:], in_=warm_in[:], func=ACT.Silu)
+
+            grouped_x = [words_to_partitions(x_sb, g) for g in range(HEADS)]
+            row_stats(0)
             for g in range(HEADS):
                 quantise(grouped_x[g], "x", g)
+            grouped_h = [words_to_partitions(h_sb, g) for g in range(HEADS)]
+            spread_vectors(0)
+            spread_vectors(1)
+            bias_bank = psum.tile([P, P], BF16, name="bias_bank", tag="turn", bufs=2)
+            nc.tensor.transpose(out=bias_bank[:], in_=bias_rows[:], identity=ident_bf16[:])
+            row_stats(1)
+            nc.vector.tensor_scalar_add(out=var_eps[:], in0=mean_var[:, :, 1], scalar1=1.0e-5)
+            nc.scalar.activation(out=std[:], in_=var_eps[:], func=ACT.Sqrt)
+            nc.scalar.activation(out=warm_out[:, 1, 0:1], in_=warm_in[:], func=ACT.Silu)
+            for g in range(HEADS):
+                quantise(grouped_h[g], "h", g)
             nc.vector.reciprocal(out=rstd[:], in_=std[:])
             for r in range(ROW_TILES):
                 nc.vector.tensor_scalar_mul(out=taps_rstd[:, r, :], in0=taps_bf16[:], scalar1=rstd[:, r:r + 1])
+            nc.vector.tensor_copy(out=bias_t[:].rearrange("p s q c -> p (s q c)"), in_=bias_bank[:])
+            nc.vector.tensor_tensor(out=bias_cols[:], in0=bias_t[:, 0, :, :], in1=bias_t[:, 1, :, :], op=ALU.add)
+            for gate in ("f", "o"):
+                q = GATES.index(gate)
+                nc.vector.tensor_scalar_mul(out=bias_cols[:, q, :], in0=bias_cols[:, q, :],
+                                            scalar1=GATE_SCALE[gate])
+            nc.vector.tensor_scalar_mul(out=minus_ident[:], in0=ident_bf16[:], scalar1=-1.0)
 
-            grouped_h = [words_to_partitions(h_sb, g) for g in range(HEADS)]
+            gates(0, ("z", "o"))
+            for r in range(ROW_TILES):
+                nc.sync.dma_start(out=m_sb[:, r, :], in_=m_prev[r * P:(r + 1) * P, :])
+            for name in ("wi", "ri", "wf", "rf"):
+                load_words(name, 1)
+            for r in range(ROW_TILES):
+                for s, state in enumerate((c_prev, n_prev)):
+                    nc.sync.dma_start(
+                        out=cn_sb[:, r, :, s, :],
+                        in_=state[r * P:(r + 1) * P, :].rearrange("p (g f) -> p g f", g=HEADS),
+                    )
+            gates(1, ("z", "o"))
 
-            bias_bank = psum.tile([P, P], BF16, name="bias_bank", tag="turn", bufs=2)
-            nc.tensor.transpose(out=bias_bank[:], in_=bias_rows[:], identity=ident_bf16[:])
-
-            def conv_head(g):
-                cols = slice(g * HEAD, (g + 1) * HEAD)
+            def centre(g):
                 for r in range(ROW_TILES):
                     nc.vector.scalar_tensor_tensor(
                         out=centred[:, r, PAD + g * HEAD:PAD + (g + 1) * HEAD],
-                        in0=x_sb[:, r, cols], scalar=mean_var[:, r, 0:1], in1=gain_bank[g][:],
-                        op0=ALU.subtract, op1=ALU.mult,
+                        in0=x_sb[:, r, g * HEAD:(g + 1) * HEAD], scalar=mean_var[:, r, 0:1],
+                        in1=gain_bank[g][:], op0=ALU.subtract, op1=ALU.mult,
                     )
+
+            def conv_head(g):
                 sums = [pre.tile([P, HEAD], F32, name="conv_sum", tag="conv_sum", bufs=2)
                         for r in range(ROW_TILES)]
                 planes_t = [pre.tile([P, PACK, P], F32, name="conv_planes", tag="conv_planes", bufs=2)
@@ -289,69 +329,45 @@ def tile_slstmblock_pa_e_kernel(
                                 op0=ALU.mult, op1=ALU.add)
                     if j == 0 and g + 2 < HEADS:
                         spread_vectors(g + 2)
-                grouped = pre.tile([P, ROWS, PACK], BF16, name="grouped_c", tag="grouped_c", bufs=2,
-                                   align_bytes=64)
+                grouped_c[g] = ring.tile([P, ROWS, PACK], BF16, name="grouped_c", tag="grouped_c",
+                                         align_bytes=64)
                 for r in range(ROW_TILES):
                     bank = psum.tile([P, PACK, P], F32, name="conv_bank", tag="turn", bufs=2)
                     for t in range(PACK):
                         nc.tensor.transpose(out=bank[:, t, :], in_=planes_t[r][:, t, :], identity=ident_f32[:])
-                    nc.scalar.activation(out=grouped[:, r * P:(r + 1) * P, :],
+                    nc.scalar.activation(out=grouped_c[g][:, r * P:(r + 1) * P, :],
                                          in_=bank[:].rearrange("p t b -> p b t"), func=ACT.Silu)
-                return grouped
 
-            grouped_c = {0: conv_head(0)}
-            nc.vector.tensor_copy(out=bias_t[:].rearrange("p s q c -> p (s q c)"), in_=bias_bank[:])
-            nc.vector.tensor_tensor(out=bias_cols[:], in0=bias_t[:, 0, :, :], in1=bias_t[:, 1, :, :], op=ALU.add)
-            for gate in ("f", "o"):
-                q = GATES.index(gate)
-                nc.vector.tensor_scalar_mul(out=bias_cols[:, q, :], in0=bias_cols[:, q, :],
-                                            scalar1=GATE_SCALE[gate])
-            nc.vector.tensor_scalar_mul(out=minus_ident[:], in0=ident_bf16[:], scalar1=-1.0)
             for g in range(HEADS):
-                quantise(grouped_h[g], "h", g)
-            for g in range(1, HEADS):
-                grouped_c[g] = conv_head(g)
-                quantise(grouped_c[g - 1], "c", g - 1)
-                if g - 1 < AHEAD:
-                    gates(g - 1, ("i", "f", "z", "o"))
-            quantise(grouped_c[HEADS - 1], "c", HEADS - 1)
+                centre(g)
+                if g >= 1:
+                    quantise(grouped_c[g - 1], "c", g - 1)
+                if g == 1:
+                    gates(0, ("i", "f"))
+                    gates(2, ("z", "o"))
+                if g == 2:
+                    gates(1, ("i", "f"))
+                    difference(0)
+                    difference(1)
+                if g == 3:
+                    gate_exps(0)
+                    gate_exps(1)
+                    nc.scalar.activation(out=warm_out[:, 2, 0:1], in_=warm_in[:], func=ACT.Silu)
+                conv_head(g)
 
         with tc.tile_pool(name="late", bufs=1, reuse_waits="tile") as late:
             n_all = late.tile([P, CHUNKS, HEAD], F32, name="n_all")
             oc_all = late.tile([P, CHUNKS, HEAD], F32, name="oc_all")
             recip_all = late.tile([P, CHUNKS, HEAD], F32, name="recip_all")
-            relus = {}
-            exps = {}
-
-            def back_to_rows(bank, gate, g, r, start, stop):
-                for j in range(BLOCKS):
-                    nc.tensor.matmul(
-                        out=bank[:, j * P:(j + 1) * P], lhsT=gate_t[(gate, g)][:, j, r * P:(r + 1) * P],
-                        rhs=ident_f32[:], is_transpose=True, start=start, stop=stop and j == BLOCKS - 1,
-                    )
-
-            def difference(c):
-                g, r, rows, cols = chunk_rows_cols(c)
-                d_bank = psum.tile([P, HEAD], F32, name="d_bank", tag="d")
-                nc.tensor.matmul(out=d_bank[:], lhsT=minus_ident[:], rhs=m_sb[:, r, cols], start=True, stop=False)
-                back_to_rows(d_bank, "i", g, r, False, False)
-                back_to_rows(d_bank, "f", g, r, False, True)
-                relus[c] = ring.tile([P, 2, HEAD], F32, name="relus", tag="relus")
-                nc.scalar.activation(out=relus[c][:, 0, :], in_=d_bank[:], func=ACT.Relu, scale=-1.0)
-                nc.scalar.activation(out=relus[c][:, 1, :], in_=d_bank[:], func=ACT.Relu, scale=1.0)
-
-            def gate_exps(c):
-                exps[c] = ring.tile([P, 2, HEAD], F32, name="exps", tag="exps")
-                nc.scalar.activation(out=exps[c][:], in_=relus[c][:], func=ACT.Exp, scale=-1.0)
 
             def update(c):
                 g, r, rows, cols = chunk_rows_cols(c)
                 banks = {}
-                for gate, tag in (("i", "a"), ("z", "z"), ("o", "o")):
+                for gate, tag in (("z", "z"), ("i", "a"), ("o", "o")):
                     banks[gate] = psum.tile([P, HEAD], F32, name="bank_" + gate, tag=tag)
                     for j in range(BLOCKS):
                         nc.tensor.transpose(out=banks[gate][:, j * P:(j + 1) * P],
-                                            in_=gate_t[(gate, g)][:, j, r * P:(r + 1) * P],
+                                            in_=gate_t[gate][:, g, j, r * P:(r + 1) * P],
                                             identity=ident_f32[:])
                 ig = exps[c][:, 0, :]
                 kept = ring.tile([P, 2, HEAD], F32, name="kept", tag="kept", bufs=1)
@@ -370,20 +386,17 @@ def tile_slstmblock_pa_e_kernel(
                 nc.vector.scalar_tensor_tensor(out=oc_all[:, c, :], in0=banks["o"][:], scalar=1.0, in1=c_t[:],
                                                op0=ALU.add, op1=ALU.mult)
 
-            difference(0)
-            difference(1)
-            gate_exps(0)
+            late_gates = [("i", 2), ("f", 2), ("i", 3), ("f", 3), ("z", 3), ("o", 3)]
             for c in range(CHUNKS):
-                g, r = divmod(c, ROW_TILES)
-                if c + 1 < CHUNKS:
-                    gate_exps(c + 1)
                 update(c)
-                if r == 1 and g + AHEAD < HEADS:
-                    gates(g + AHEAD, ("i", "f"))
-                if r == 0 and AHEAD <= g + 1 < HEADS:
-                    gates(g + 1, ("z", "o"))
+                if c == 0:
+                    quantise(grouped_c[HEADS - 1], "c", HEADS - 1)
+                if c < len(late_gates):
+                    gate, g = late_gates[c]
+                    gates(g, (gate,))
                 if c + 2 < CHUNKS:
                     difference(c + 2)
+                    gate_exps(c + 2)
 
             for c in range(CHUNKS):
                 nc.scalar.activation(out=recip_all[:, c, :], in_=n_all[:, c, :], func=ACT.Ln,

@@ -51,7 +51,6 @@ def tile_slstmblock_pa_e_kernel(
     with ExitStack() as ctx:
         ctx.enter_context(tc.manual_schedule())
         keep = ctx.enter_context(tc.tile_pool(name="keep", bufs=1))
-        stream = ctx.enter_context(tc.tile_pool(name="stream", bufs=2))
         ring = ctx.enter_context(tc.tile_pool(name="ring", bufs=2))
         psum = ctx.enter_context(tc.psum_pool(name="psum", bufs=1))
 
@@ -62,10 +61,11 @@ def tile_slstmblock_pa_e_kernel(
             codes[name] = keep.tile([P, HEADS * ROWS], U32, name="codes_" + name, align_bytes=64)
             scales[name] = keep.tile([P, HEADS * ROWS], U8, name="scales_" + name, align_bytes=64)
         gate_t = {}
-        for gate in GATES:
-            gate_t[gate] = keep.tile([P, HEADS, BLOCKS, ROWS], F32, name="gate_t_" + gate)
+        words_sb = {}
+        for name in WEIGHTS:
+            words_sb[name] = keep.tile([P, HEADS, HEAD], U32, name="words_" + name, align_bytes=64)
         m_sb = keep.tile([P, ROW_TILES, FEATURES], BF16, name="m_sb")
-        cn_sb = keep.tile([P, ROW_TILES, HEADS, 2, HEAD], BF16, name="cn_sb")
+        cn_sb = keep.tile([P, 2, ROW_TILES, FEATURES], BF16, name="cn_sb")
         ident_f32 = keep.tile([P, P], F32, name="ident_f32")
         ident_bf16 = keep.tile([P, P], BF16, name="ident_bf16")
         minus_ident = keep.tile([P, P], BF16, name="minus_ident")
@@ -74,6 +74,7 @@ def tile_slstmblock_pa_e_kernel(
         bias_cols = keep.tile([P, len(GATES), HEADS * BLOCKS], F32, name="bias_cols")
         tap_coef = keep.tile([P, 1], BF16, name="tap_coef")
         gain_pick = keep.tile([P, 1], BF16, name="gain_pick")
+        coef_wide = keep.tile([P, P], BF16, name="coef_wide")
         taps_bf16 = keep.tile([P, TAPS], BF16, name="taps_bf16")
         stats = keep.tile([P, ROW_TILES, HEADS, 6], F32, name="stats")
         mean_var = keep.tile([P, ROW_TILES, 2], F32, name="mean_var")
@@ -83,19 +84,15 @@ def tile_slstmblock_pa_e_kernel(
         taps_rstd = keep.tile([P, ROW_TILES, TAPS], F32, name="taps_rstd")
         two_eps = keep.tile([P, 1], F32, name="two_eps")
         warm_in = keep.tile([P, 1], F32, name="warm_in")
-        warm_out = keep.tile([P, 3, 8], F32, name="warm_out")
+        warm_out = keep.tile([P, 2, 8], F32, name="warm_out")
 
         def chunk_rows_cols(c):
             g, r = divmod(c, ROW_TILES)
             return g, r, slice(r * P, (r + 1) * P), slice(g * HEAD, (g + 1) * HEAD)
 
-        words_sb = {}
-
         def load_words(name, g):
-            words_sb[(name, g)] = stream.tile([P, HEAD], U32, name="words_" + name, tag="words_" + name,
-                                              align_bytes=64)
             nc.sync.dma_start(
-                out=words_sb[(name, g)][:].bitcast(I32),
+                out=words_sb[name][:, g, :].bitcast(I32),
                 in_=word_bytes[name][g].rearrange("p n t -> p (n t)").bitcast(I32),
             )
 
@@ -112,7 +109,7 @@ def tile_slstmblock_pa_e_kernel(
             batch = slice(g * ROWS, (g + 1) * ROWS)
             nc.tensor.matmul_mx(
                 out=acc,
-                lhsT=words_sb[(name, g)][:, cols].bitcast(FP8X4),
+                lhsT=words_sb[name][:, g, cols].bitcast(FP8X4),
                 lhsT_scale=planes[PACK * g:P, WEIGHTS.index(name), cols],
                 rhs=codes[operand][:, batch].bitcast(FP8X4),
                 rhs_scale=scales[operand][:, batch],
@@ -123,6 +120,8 @@ def tile_slstmblock_pa_e_kernel(
         def gates(g, names):
             for gate in names:
                 operand = "x" if gate in ("z", "o") else "c"
+                gate_t[(gate, g)] = ring.tile([P, BLOCKS, ROWS], F32, name="gate_t_" + gate,
+                                              tag="gate_t_" + gate, bufs=3 if gate == "z" else 2)
                 for pair in range(BLOCKS // 2):
                     acc = psum.tile([P, 2, ROWS], F32, name="acc", tag="acc", bufs=2)
                     for s in range(2):
@@ -133,12 +132,9 @@ def tile_slstmblock_pa_e_kernel(
                         j = 2 * pair + s
                         col = g * BLOCKS + j
                         nc.scalar.activation(
-                            out=gate_t[gate][:, g, j, :], in_=acc[:, s, :], func=GATE_FUNC[gate],
+                            out=gate_t[(gate, g)][:, j, :], in_=acc[:, s, :], func=GATE_FUNC[gate],
                             bias=bias_cols[:, GATES.index(gate), col:col + 1], scale=GATE_SCALE[gate],
                         )
-                if g + 2 < HEADS:
-                    load_words("w" + gate, g + 2)
-                    load_words("r" + gate, g + 2)
 
         def quantise(grouped, name, g):
             batch = slice(g * ROWS, (g + 1) * ROWS)
@@ -154,7 +150,7 @@ def tile_slstmblock_pa_e_kernel(
         def add_back_to_rows(bank, gate, g, r, stop):
             for j in range(BLOCKS):
                 nc.tensor.matmul(
-                    out=bank[:, j * P:(j + 1) * P], lhsT=gate_t[gate][:, g, j, r * P:(r + 1) * P],
+                    out=bank[:, j * P:(j + 1) * P], lhsT=gate_t[(gate, g)][:, j, r * P:(r + 1) * P],
                     rhs=ident_f32[:], is_transpose=True, start=False, stop=stop and j == BLOCKS - 1,
                 )
 
@@ -173,206 +169,225 @@ def tile_slstmblock_pa_e_kernel(
             nc.scalar.activation(out=exps[c][:], in_=relus[c][:], func=ACT.Exp, scale=-1.0)
 
         grouped_c = {}
+        conv_bank = {}
+
+        def silu_head(g):
+            grouped_c[g] = ring.tile([P, ROWS, PACK], BF16, name="grouped_c", tag="grouped_c", align_bytes=64)
+            for r in range(ROW_TILES):
+                nc.scalar.activation(out=grouped_c[g][:, r * P:(r + 1) * P, :],
+                                     in_=conv_bank[(g, r)][:].rearrange("p t b -> p b t"), func=ACT.Silu)
 
         with tc.tile_pool(name="pre", bufs=1) as pre:
             x_sb = pre.tile([P, ROW_TILES, FEATURES], BF16, name="x_sb")
-            h_sb = pre.tile([P, ROW_TILES, FEATURES], BF16, name="h_sb")
             vec_rows = pre.tile([P, FEATURES], BF16, name="vec_rows")
-            centred = pre.tile([P, ROW_TILES, PAD + FEATURES], F32, name="centred")
 
-            nc.vector.memset(vec_rows[:].bitcast(I32), 0)
-            nc.vector.memset(vec_rows[32:33, :], 1.0)
-            nc.vector.memset(tap_coef[:], 0.0)
-            nc.vector.memset(gain_pick[:], 0.0)
-            nc.vector.memset(gain_pick[64:65, :], 1.0)
-            nc.vector.memset(warm_in[:], 1.0)
-            nc.vector.memset(planes[:].rearrange("p w n -> p (w n)").bitcast(I32), 0)
-            nc.vector.memset(centred[:, :, 0:PAD], 0.0)
-            nc.vector.memset(two_eps[:], 2.0e-6)
+            with tc.tile_pool(name="early", bufs=1) as early:
+                h_sb = early.tile([P, ROW_TILES, FEATURES], BF16, name="h_sb")
 
-            make_identity(nc, ident_f32[:])
-            make_identity(nc, ident_bf16[:])
+                nc.vector.memset(vec_rows[:].bitcast(I32), 0)
+                nc.vector.memset(vec_rows[32:33, :], 1.0)
+                nc.vector.memset(tap_coef[:], 0.0)
+                nc.vector.memset(gain_pick[:], 0.0)
+                nc.vector.memset(gain_pick[64:65, :], 1.0)
+                nc.vector.memset(warm_in[:], 1.0)
+                nc.vector.memset(planes[:].rearrange("p w n -> p (w n)").bitcast(I32), 0)
+                nc.vector.memset(two_eps[:], 2.0e-6)
 
-            for r in range(ROW_TILES):
-                nc.sync.dma_start(out=x_sb[:, r, :], in_=x[r * P:(r + 1) * P, :])
-            nc.sync.dma_start(out=vec_rows[64:65, :], in_=ln_g.rearrange("(o d) -> o d", o=1))
-            nc.sync.dma_start(out=tap_coef[0:TAPS, :], in_=conv_w.rearrange("(k o) -> k o", o=1))
-            for j in range(TAPS):
-                shift = TAPS - 1 - j
-                nc.sync.dma_start(
-                    out=vec_rows[j:j + 1, shift:FEATURES],
-                    in_=ln_b.rearrange("(o d) -> o d", o=1)[:, 0:FEATURES - shift],
-                )
-            nc.sync.dma_start(out=tap_coef[32:33, :], in_=conv_b.rearrange("(k o) -> k o", o=1))
-            nc.sync.dma_start(out=taps_bf16[:], in_=conv_w.partition_broadcast(P))
-            for r in range(ROW_TILES):
-                nc.sync.dma_start(out=h_sb[:, r, :], in_=h_prev[r * P:(r + 1) * P, :])
-            for i, name in enumerate(WEIGHTS):
-                nc.sync.dma_start(
-                    out=bias_rows[16 * i:16 * (i + 1), :],
-                    in_=biases[name].rearrange("(c f) -> c f", f=P),
-                )
-            for name in ("wz", "rz", "wo", "ro"):
-                load_planes(name)
-            for g in range(2):
-                for name in ("wz", "rz", "wo", "ro"):
-                    load_words(name, g)
-            for name in ("wi", "ri", "wf", "rf"):
-                load_planes(name)
-            for name in ("wi", "ri", "wf", "rf"):
-                load_words(name, 0)
+                make_identity(nc, ident_f32[:])
+                make_identity(nc, ident_bf16[:])
 
-            nc.scalar.activation(out=warm_out[:, 0, 0:1], in_=warm_in[:], func=ACT.Sqrt)
-
-            gain_bank = {}
-            shift_bank = {}
-
-            def spread_vectors(g):
-                cols = slice(g * HEAD, (g + 1) * HEAD)
-                gain_bank[g] = psum.tile([P, HEAD], F32, name="gain_bank", tag="d" if g % 2 == 0 else "z")
-                shift_bank[g] = psum.tile([P, HEAD], F32, name="shift_bank", tag="a" if g % 2 == 0 else "o")
-                nc.tensor.matmul(out=gain_bank[g][:], lhsT=gain_pick[:].to_broadcast([P, P]),
-                                 rhs=vec_rows[:, cols], start=True, stop=True)
-                nc.tensor.matmul(out=shift_bank[g][:], lhsT=tap_coef[:].to_broadcast([P, P]),
-                                 rhs=vec_rows[:, cols], start=True, stop=True)
-
-            def words_to_partitions(src, g):
-                bank = psum.tile([P, 2, ROWS], F32, name="word_bank", tag="turn", bufs=2)
                 for r in range(ROW_TILES):
-                    src_words = src[:, r, :].bitcast(F32)
-                    for u in range(2):
-                        nc.tensor.transpose(
-                            out=bank[:, u, r * P:(r + 1) * P],
-                            in_=src_words[:, (HEAD // 2) * g + u:(HEAD // 2) * (g + 1):2],
-                            identity=ident_f32[:],
-                        )
-                grouped = pre.tile([P, ROWS, PACK], BF16, name="grouped", tag="grouped", bufs=4,
-                                   align_bytes=64)
-                nc.scalar.copy(out=grouped[:].bitcast(F32), in_=bank[:].rearrange("p u b -> p b u"))
-                return grouped
-
-            def row_stats(r):
-                for g in range(HEADS):
-                    nc.vector.bn_stats(out=stats[:, r, g, :], in_=x_sb[:, r, g * HEAD:(g + 1) * HEAD])
-                nc.vector.bn_aggr(out=mean_var[:, r, :], in_=stats[:, r, :, :].rearrange("p g s -> p (g s)"))
-
-            grouped_x = [words_to_partitions(x_sb, g) for g in range(HEADS)]
-            row_stats(0)
-            for g in range(HEADS):
-                quantise(grouped_x[g], "x", g)
-            grouped_h = [words_to_partitions(h_sb, g) for g in range(HEADS)]
-            spread_vectors(0)
-            spread_vectors(1)
-            bias_bank = psum.tile([P, P], BF16, name="bias_bank", tag="turn", bufs=2)
-            nc.tensor.transpose(out=bias_bank[:], in_=bias_rows[:], identity=ident_bf16[:])
-            row_stats(1)
-            nc.vector.tensor_scalar_add(out=var_eps[:], in0=mean_var[:, :, 1], scalar1=1.0e-5)
-            nc.scalar.activation(out=std[:], in_=var_eps[:], func=ACT.Sqrt)
-            nc.scalar.activation(out=warm_out[:, 1, 0:1], in_=warm_in[:], func=ACT.Silu)
-            for g in range(HEADS):
-                quantise(grouped_h[g], "h", g)
-            nc.vector.reciprocal(out=rstd[:], in_=std[:])
-            for r in range(ROW_TILES):
-                nc.vector.tensor_scalar_mul(out=taps_rstd[:, r, :], in0=taps_bf16[:], scalar1=rstd[:, r:r + 1])
-            nc.vector.tensor_copy(out=bias_t[:].rearrange("p s q c -> p (s q c)"), in_=bias_bank[:])
-            nc.vector.tensor_tensor(out=bias_cols[:], in0=bias_t[:, 0, :, :], in1=bias_t[:, 1, :, :], op=ALU.add)
-            for gate in ("f", "o"):
-                q = GATES.index(gate)
-                nc.vector.tensor_scalar_mul(out=bias_cols[:, q, :], in0=bias_cols[:, q, :],
-                                            scalar1=GATE_SCALE[gate])
-            nc.vector.tensor_scalar_mul(out=minus_ident[:], in0=ident_bf16[:], scalar1=-1.0)
-
-            gates(0, ("z", "o"))
-            for r in range(ROW_TILES):
-                nc.sync.dma_start(out=m_sb[:, r, :], in_=m_prev[r * P:(r + 1) * P, :])
-            for name in ("wi", "ri", "wf", "rf"):
-                load_words(name, 1)
-            for r in range(ROW_TILES):
-                for s, state in enumerate((c_prev, n_prev)):
-                    nc.sync.dma_start(
-                        out=cn_sb[:, r, :, s, :],
-                        in_=state[r * P:(r + 1) * P, :].rearrange("p (g f) -> p g f", g=HEADS),
-                    )
-            gates(1, ("z", "o"))
-
-            def centre(g):
-                for r in range(ROW_TILES):
-                    nc.vector.scalar_tensor_tensor(
-                        out=centred[:, r, PAD + g * HEAD:PAD + (g + 1) * HEAD],
-                        in0=x_sb[:, r, g * HEAD:(g + 1) * HEAD], scalar=mean_var[:, r, 0:1],
-                        in1=gain_bank[g][:], op0=ALU.subtract, op1=ALU.mult,
-                    )
-
-            def conv_head(g):
-                sums = [pre.tile([P, HEAD], F32, name="conv_sum", tag="conv_sum", bufs=2)
-                        for r in range(ROW_TILES)]
-                planes_t = [pre.tile([P, PACK, P], F32, name="conv_planes", tag="conv_planes", bufs=2)
-                            for r in range(ROW_TILES)]
+                    nc.sync.dma_start(out=x_sb[:, r, :], in_=x[r * P:(r + 1) * P, :])
+                nc.sync.dma_start(out=vec_rows[64:65, :], in_=ln_g.rearrange("(o d) -> o d", o=1))
+                nc.sync.dma_start(out=tap_coef[0:TAPS, :], in_=conv_w.rearrange("(k o) -> k o", o=1))
                 for j in range(TAPS):
+                    shift = TAPS - 1 - j
+                    nc.sync.dma_start(
+                        out=vec_rows[j:j + 1, shift:FEATURES],
+                        in_=ln_b.rearrange("(o d) -> o d", o=1)[:, 0:FEATURES - shift],
+                    )
+                nc.sync.dma_start(out=tap_coef[32:33, :], in_=conv_b.rearrange("(k o) -> k o", o=1))
+                nc.sync.dma_start(out=taps_bf16[:], in_=conv_w.partition_broadcast(P))
+                for r in range(ROW_TILES):
+                    nc.sync.dma_start(out=h_sb[:, r, :], in_=h_prev[r * P:(r + 1) * P, :])
+                for i, name in enumerate(WEIGHTS):
+                    nc.sync.dma_start(
+                        out=bias_rows[16 * i:16 * (i + 1), :],
+                        in_=biases[name].rearrange("(c f) -> c f", f=P),
+                    )
+                for name in ("wz", "rz", "wo", "ro"):
+                    load_words(name, 0)
+                for name in ("wz", "rz", "wo", "ro"):
+                    load_planes(name)
+                for name in ("wz", "rz", "wo", "ro"):
+                    load_words(name, 1)
+                for name in ("wi", "ri", "wf", "rf"):
+                    load_planes(name)
+                for name in ("wi", "ri", "wf", "rf"):
+                    load_words(name, 0)
+                for r in range(ROW_TILES):
+                    nc.sync.dma_start(out=m_sb[:, r, :], in_=m_prev[r * P:(r + 1) * P, :])
+                for r in range(ROW_TILES):
+                    for s, state in enumerate((c_prev, n_prev)):
+                        nc.sync.dma_start(out=cn_sb[:, s, r, :], in_=state[r * P:(r + 1) * P, :])
+                for name in ("wi", "ri", "wf", "rf"):
+                    load_words(name, 1)
+                for g in range(2, HEADS):
+                    for name in WEIGHTS:
+                        load_words(name, g)
+
+                nc.scalar.activation(out=warm_out[:, 0, 0:1], in_=warm_in[:], func=ACT.Sqrt)
+
+                gain_bank = {}
+
+                def spread_vectors(g):
+                    cols = slice(g * HEAD, (g + 1) * HEAD)
+                    gain_bank[g] = psum.tile([P, HEAD], F32, name="gain_bank", tag=("z", "a", "o")[g % 3])
+                    nc.tensor.matmul(out=gain_bank[g][:], lhsT=gain_pick[:].to_broadcast([P, P]),
+                                     rhs=vec_rows[:, cols], start=True, stop=True)
+
+
+                def words_to_partitions(src, g):
+                    bank = psum.tile([P, 2, ROWS], F32, name="word_bank", tag="turn", bufs=2)
+                    for r in range(ROW_TILES):
+                        src_words = src[:, r, :].bitcast(F32)
+                        for u in range(2):
+                            nc.tensor.transpose(
+                                out=bank[:, u, r * P:(r + 1) * P],
+                                in_=src_words[:, (HEAD // 2) * g + u:(HEAD // 2) * (g + 1):2],
+                                identity=ident_f32[:],
+                            )
+                    grouped = early.tile([P, ROWS, PACK], BF16, name="grouped", tag="grouped", bufs=4,
+                                       align_bytes=64)
+                    nc.scalar.copy(out=grouped[:].bitcast(F32), in_=bank[:].rearrange("p u b -> p b u"))
+                    return grouped
+
+                def row_stats(r):
+                    for g in range(HEADS):
+                        nc.vector.bn_stats(out=stats[:, r, g, :], in_=x_sb[:, r, g * HEAD:(g + 1) * HEAD])
+                    nc.vector.bn_aggr(out=mean_var[:, r, :], in_=stats[:, r, :, :].rearrange("p g s -> p (g s)"))
+
+                grouped_x = [words_to_partitions(x_sb, g) for g in range(HEADS)]
+                row_stats(0)
+                for g in range(HEADS):
+                    quantise(grouped_x[g], "x", g)
+                grouped_h = [words_to_partitions(h_sb, g) for g in range(HEADS)]
+                spread_vectors(0)
+                spread_vectors(1)
+                spread_vectors(2)
+                bias_bank = psum.tile([P, P], BF16, name="bias_bank", tag="turn", bufs=2)
+                nc.tensor.transpose(out=bias_bank[:], in_=bias_rows[:], identity=ident_bf16[:])
+                row_stats(1)
+                nc.vector.tensor_scalar_add(out=var_eps[:], in0=mean_var[:, :, 1], scalar1=1.0e-5)
+                nc.scalar.activation(out=std[:], in_=var_eps[:], func=ACT.Sqrt)
+                nc.scalar.activation(out=warm_out[:, 1, 0:1], in_=warm_in[:], func=ACT.Silu)
+                for g in range(HEADS):
+                    quantise(grouped_h[g], "h", g)
+
+            with tc.tile_pool(name="conv", bufs=1, reuse_waits="tile") as conv:
+                centred = conv.tile([P, ROW_TILES, PAD + FEATURES], F32, name="centred")
+                nc.vector.memset(centred[:, :, 0:PAD], 0.0)
+                nc.vector.reciprocal(out=rstd[:], in_=std[:])
+                for r in range(ROW_TILES):
+                    nc.vector.tensor_scalar_mul(out=taps_rstd[:, r, :], in0=taps_bf16[:], scalar1=rstd[:, r:r + 1])
+                nc.vector.tensor_copy(out=bias_t[:].rearrange("p s q c -> p (s q c)"), in_=bias_bank[:])
+                nc.vector.tensor_tensor(out=bias_cols[:], in0=bias_t[:, 0, :, :], in1=bias_t[:, 1, :, :], op=ALU.add)
+                for gate in ("f", "o"):
+                    q = GATES.index(gate)
+                    nc.vector.tensor_scalar_mul(out=bias_cols[:, q, :], in0=bias_cols[:, q, :],
+                                                scalar1=GATE_SCALE[gate])
+                nc.vector.tensor_scalar_mul(out=minus_ident[:], in0=ident_bf16[:], scalar1=-1.0)
+                nc.vector.tensor_copy(out=coef_wide[:], in_=tap_coef[:].to_broadcast([P, P]))
+
+                def centre(g):
+                    for r in range(ROW_TILES):
+                        nc.vector.scalar_tensor_tensor(
+                            out=centred[:, r, PAD + g * HEAD:PAD + (g + 1) * HEAD],
+                            in0=x_sb[:, r, g * HEAD:(g + 1) * HEAD], scalar=mean_var[:, r, 0:1],
+                            in1=gain_bank[g][:], op0=ALU.subtract, op1=ALU.mult,
+                        )
+
+                conv_sum = {}
+                conv_planes = {}
+
+                def tap(g, j):
                     first = PAD + g * HEAD + j - (TAPS - 1)
                     for r in range(ROW_TILES):
                         moved = centred[:, r, first:first + HEAD]
                         coef = taps_rstd[:, r, j:j + 1]
                         if j == 0:
-                            nc.vector.scalar_tensor_tensor(
-                                out=sums[r][:], in0=moved, scalar=coef, in1=shift_bank[g][:],
-                                op0=ALU.mult, op1=ALU.add)
+                            conv_sum[r] = conv.tile([P, HEAD], F32, name="conv_sum", tag="conv_sum", bufs=2)
+                            nc.vector.tensor_scalar_mul(out=conv_sum[r][:], in0=moved, scalar1=coef)
                         elif j < TAPS - 1:
                             nc.vector.scalar_tensor_tensor(
-                                out=sums[r][:], in0=moved, scalar=coef, in1=sums[r][:],
+                                out=conv_sum[r][:], in0=moved, scalar=coef, in1=conv_sum[r][:],
                                 op0=ALU.mult, op1=ALU.add)
                         else:
+                            conv_planes[r] = conv.tile([P, PACK, P], F32, name="conv_planes", tag="conv_planes", bufs=4)
                             nc.vector.scalar_tensor_tensor(
-                                out=planes_t[r][:].rearrange("p t q -> p q t"),
+                                out=conv_planes[r][:].rearrange("p t q -> p q t"),
                                 in0=moved.rearrange("p (q t) -> p q t", t=PACK), scalar=coef,
-                                in1=sums[r][:].rearrange("p (q t) -> p q t", t=PACK),
+                                in1=conv_sum[r][:].rearrange("p (q t) -> p q t", t=PACK),
                                 op0=ALU.mult, op1=ALU.add)
-                    if j == 0 and g + 2 < HEADS:
-                        spread_vectors(g + 2)
-                grouped_c[g] = ring.tile([P, ROWS, PACK], BF16, name="grouped_c", tag="grouped_c",
-                                         align_bytes=64)
-                for r in range(ROW_TILES):
-                    bank = psum.tile([P, PACK, P], F32, name="conv_bank", tag="turn", bufs=2)
-                    for t in range(PACK):
-                        nc.tensor.transpose(out=bank[:, t, :], in_=planes_t[r][:, t, :], identity=ident_f32[:])
-                    nc.scalar.activation(out=grouped_c[g][:, r * P:(r + 1) * P, :],
-                                         in_=bank[:].rearrange("p t b -> p b t"), func=ACT.Silu)
 
-            for g in range(HEADS):
-                centre(g)
-                if g >= 1:
-                    quantise(grouped_c[g - 1], "c", g - 1)
-                if g == 1:
-                    gates(0, ("i", "f"))
-                    gates(2, ("z", "o"))
-                if g == 2:
-                    gates(1, ("i", "f"))
-                    difference(0)
-                    difference(1)
-                if g == 3:
-                    gate_exps(0)
-                    gate_exps(1)
-                    nc.scalar.activation(out=warm_out[:, 2, 0:1], in_=warm_in[:], func=ACT.Silu)
-                conv_head(g)
+                def turn_conv(g):
+                    for r in range(ROW_TILES):
+                        conv_bank[(g, r)] = psum.tile([P, PACK, P], F32, name="conv_bank", tag="turn", bufs=2)
+                        for t in range(PACK):
+                            nc.tensor.matmul(out=conv_bank[(g, r)][:, t, :],
+                                             lhsT=vec_rows[:, g * HEAD + t:(g + 1) * HEAD:PACK], rhs=coef_wide[:],
+                                             start=True, stop=False)
+                            nc.tensor.matmul(out=conv_bank[(g, r)][:, t, :], lhsT=conv_planes[r][:, t, :],
+                                             rhs=ident_f32[:], is_transpose=True, start=False, stop=True)
+
+                for g in range(HEADS):
+                    if g >= 2:
+                        quantise(grouped_c[g - 2], "c", g - 2)
+                    centre(g)
+                    tap(g, 0)
+                    if g + 3 < HEADS:
+                        spread_vectors(g + 3)
+                    if g >= 1:
+                        silu_head(g - 1)
+                    if g == 0:
+                        gates(0, ("z", "o"))
+                    if g == 1:
+                        gates(1, ("z", "o"))
+                    if g == 2:
+                        gates(0, ("i", "f"))
+                        difference(0)
+                    if g == 3:
+                        gate_exps(0)
+                        difference(1)
+                        gate_exps(1)
+                    for j in range(1, TAPS):
+                        tap(g, j)
+                    turn_conv(g)
 
         with tc.tile_pool(name="late", bufs=1, reuse_waits="tile") as late:
             n_all = late.tile([P, CHUNKS, HEAD], F32, name="n_all")
             oc_all = late.tile([P, CHUNKS, HEAD], F32, name="oc_all")
             recip_all = late.tile([P, CHUNKS, HEAD], F32, name="recip_all")
 
+            all_banks = {}
+
+            def to_rows(c):
+                g, r, rows, cols = chunk_rows_cols(c)
+                all_banks[c] = {}
+                for gate, tag in (("z", "z"), ("i", "a"), ("o", "o")):
+                    all_banks[c][gate] = psum.tile([P, HEAD], F32, name="bank_" + gate, tag=tag)
+                    for j in range(BLOCKS):
+                        nc.tensor.transpose(out=all_banks[c][gate][:, j * P:(j + 1) * P],
+                                            in_=gate_t[(gate, g)][:, j, r * P:(r + 1) * P],
+                                            identity=ident_f32[:])
+
             def update(c):
                 g, r, rows, cols = chunk_rows_cols(c)
-                banks = {}
-                for gate, tag in (("z", "z"), ("i", "a"), ("o", "o")):
-                    banks[gate] = psum.tile([P, HEAD], F32, name="bank_" + gate, tag=tag)
-                    for j in range(BLOCKS):
-                        nc.tensor.transpose(out=banks[gate][:, j * P:(j + 1) * P],
-                                            in_=gate_t[gate][:, g, j, r * P:(r + 1) * P],
-                                            identity=ident_f32[:])
+                banks = all_banks[c]
                 ig = exps[c][:, 0, :]
                 kept = ring.tile([P, 2, HEAD], F32, name="kept", tag="kept", bufs=1)
                 nc.vector.tensor_tensor(out=kept[:], in0=exps[c][:, 1:2, :].to_broadcast([P, 2, HEAD]),
-                                        in1=cn_sb[:, r, g, :, :], op=ALU.mult)
+                                        in1=cn_sb[:, :, r, cols], op=ALU.mult)
                 fresh = ring.tile([P, HEAD], F32, name="fresh", tag="fresh", bufs=1)
                 nc.vector.tensor_tensor(out=fresh[:], in0=banks["z"][:], in1=ig, op=ALU.mult)
                 nc.vector.tensor_tensor(out=n_all[:, c, :], in0=kept[:, 1, :], in1=ig, op=ALU.add)
@@ -386,17 +401,24 @@ def tile_slstmblock_pa_e_kernel(
                 nc.vector.scalar_tensor_tensor(out=oc_all[:, c, :], in0=banks["o"][:], scalar=1.0, in1=c_t[:],
                                                op0=ALU.add, op1=ALU.mult)
 
-            late_gates = [("i", 2), ("f", 2), ("i", 3), ("f", 3), ("z", 3), ("o", 3)]
+            quantise(grouped_c[2], "c", 2)
+            to_rows(0)
+            gates(1, ("i", "f"))
             for c in range(CHUNKS):
                 update(c)
                 if c == 0:
-                    quantise(grouped_c[HEADS - 1], "c", HEADS - 1)
-                if c < len(late_gates):
-                    gate, g = late_gates[c]
-                    gates(g, (gate,))
+                    silu_head(3)
+                if c == 1:
+                    quantise(grouped_c[3], "c", 3)
+                for g in (2, 3):
+                    k = c - (ROW_TILES * g - len(GATES))
+                    if 0 <= k < len(GATES):
+                        gates(g, (GATES[k],))
                 if c + 2 < CHUNKS:
                     difference(c + 2)
                     gate_exps(c + 2)
+                if c + 1 < CHUNKS:
+                    to_rows(c + 1)
 
             for c in range(CHUNKS):
                 nc.scalar.activation(out=recip_all[:, c, :], in_=n_all[:, c, :], func=ACT.Ln,

@@ -22,7 +22,8 @@ HEAD = FEATURES // HEADS
 BLOCKS = HEAD // P
 CHUNKS = HEADS * ROW_TILES
 TAPS = 4
-PAD = 4
+SCALAR_TAPS = ((0, 2), (0, 2), (0,), ())
+PAD = 8
 
 WEIGHTS = ("wz", "wi", "wf", "wo", "rz", "ri", "rf", "ro")
 GATES = ("z", "i", "f", "o")
@@ -70,7 +71,7 @@ def tile_slstmblock_pa_e_kernel(
         ident_bf16 = keep.tile([P, P], BF16, name="ident_bf16")
         minus_ident = keep.tile([P, P], BF16, name="minus_ident")
         bias_rows = keep.tile([P, P], BF16, name="bias_rows")
-        bias_t = keep.tile([P, 2, len(GATES), HEADS * BLOCKS], F32, name="bias_t")
+        bias_pick = keep.tile([P, len(GATES), HEADS * BLOCKS], BF16, name="bias_pick")
         bias_cols = keep.tile([P, len(GATES), HEADS * BLOCKS], F32, name="bias_cols")
         tap_coef = keep.tile([P, 1], BF16, name="tap_coef")
         gain_pick = keep.tile([P, 1], BF16, name="gain_pick")
@@ -79,12 +80,12 @@ def tile_slstmblock_pa_e_kernel(
         stats = keep.tile([P, ROW_TILES, HEADS, 6], F32, name="stats")
         mean_var = keep.tile([P, ROW_TILES, 2], F32, name="mean_var")
         var_eps = keep.tile([P, ROW_TILES], F32, name="var_eps")
-        std = keep.tile([P, ROW_TILES], F32, name="std")
+        minus_half = keep.tile([P, ROW_TILES], F32, name="minus_half")
         rstd = keep.tile([P, ROW_TILES], F32, name="rstd")
         taps_rstd = keep.tile([P, ROW_TILES, TAPS], F32, name="taps_rstd")
         two_eps = keep.tile([P, 1], F32, name="two_eps")
         warm_in = keep.tile([P, 1], F32, name="warm_in")
-        warm_out = keep.tile([P, 2, 8], F32, name="warm_out")
+        warm_out = keep.tile([P, 1], F32, name="warm_out")
 
         def chunk_rows_cols(c):
             g, r = divmod(c, ROW_TILES)
@@ -117,7 +118,15 @@ def tile_slstmblock_pa_e_kernel(
                 stop=stop,
             )
 
-        def gates(g, names):
+        def leave_psum(out, acc, gate, col, on_vector):
+            bias = bias_cols[:, GATES.index(gate), col:col + 1]
+            if on_vector:
+                nc.vector.tensor_scalar(out=out, in0=acc, scalar1=GATE_SCALE[gate], scalar2=bias,
+                                        op0=ALU.mult, op1=ALU.add)
+            else:
+                nc.scalar.activation(out=out, in_=acc, func=GATE_FUNC[gate], bias=bias, scale=GATE_SCALE[gate])
+
+        def gates(g, names, on_vector=False):
             for gate in names:
                 operand = "x" if gate in ("z", "o") else "c"
                 gate_t[(gate, g)] = ring.tile([P, BLOCKS, ROWS], F32, name="gate_t_" + gate,
@@ -130,11 +139,7 @@ def tile_slstmblock_pa_e_kernel(
                         mx_pass(acc[:, s, :], "r" + gate, "h", g, j, False, True)
                     for s in range(2):
                         j = 2 * pair + s
-                        col = g * BLOCKS + j
-                        nc.scalar.activation(
-                            out=gate_t[(gate, g)][:, j, :], in_=acc[:, s, :], func=GATE_FUNC[gate],
-                            bias=bias_cols[:, GATES.index(gate), col:col + 1], scale=GATE_SCALE[gate],
-                        )
+                        leave_psum(gate_t[(gate, g)][:, j, :], acc[:, s, :], gate, g * BLOCKS + j, on_vector)
 
         def quantise(grouped, name, g):
             batch = slice(g * ROWS, (g + 1) * ROWS)
@@ -144,8 +149,9 @@ def tile_slstmblock_pa_e_kernel(
                 in_=grouped[:].rearrange("p b t -> p (b t)"),
             )
 
-        relus = {}
-        exps = {}
+        low = {}
+        keep_gate = {}
+        fresh = {}
 
         def add_back_to_rows(bank, gate, g, r, stop):
             for j in range(BLOCKS):
@@ -154,19 +160,22 @@ def tile_slstmblock_pa_e_kernel(
                     rhs=ident_f32[:], is_transpose=True, start=False, stop=stop and j == BLOCKS - 1,
                 )
 
+        d_banks = {}
+
         def difference(c):
             g, r, rows, cols = chunk_rows_cols(c)
-            d_bank = psum.tile([P, HEAD], F32, name="d_bank", tag="d")
-            nc.tensor.matmul(out=d_bank[:], lhsT=minus_ident[:], rhs=m_sb[:, r, cols], start=True, stop=False)
-            add_back_to_rows(d_bank, "i", g, r, False)
-            add_back_to_rows(d_bank, "f", g, r, True)
-            relus[c] = ring.tile([P, 2, HEAD], F32, name="relus", tag="relus")
-            nc.scalar.activation(out=relus[c][:, 0, :], in_=d_bank[:], func=ACT.Relu, scale=-1.0)
-            nc.scalar.activation(out=relus[c][:, 1, :], in_=d_bank[:], func=ACT.Relu, scale=1.0)
+            d_banks[c] = psum.tile([P, HEAD], F32, name="d_bank", tag="turn", bufs=3)
+            nc.tensor.matmul(out=d_banks[c][:], lhsT=minus_ident[:], rhs=m_sb[:, r, cols], start=True, stop=False)
+            add_back_to_rows(d_banks[c], "i", g, r, False)
+            add_back_to_rows(d_banks[c], "f", g, r, True)
 
         def gate_exps(c):
-            exps[c] = ring.tile([P, 2, HEAD], F32, name="exps", tag="exps")
-            nc.scalar.activation(out=exps[c][:], in_=relus[c][:], func=ACT.Exp, scale=-1.0)
+            low[c] = ring.tile([P, HEAD], F32, name="low", tag="low", bufs=3)
+            nc.scalar.activation(out=low[c][:], in_=d_banks[c][:], func=ACT.Relu, scale=-1.0)
+            keep_gate[c] = ring.tile([P, 1, HEAD], F32, name="keep_gate", tag="keep_gate", bufs=3)
+            nc.scalar.activation(out=keep_gate[c][:, 0, :], in_=d_banks[c][:], func=ACT.Exp, scale=-1.0)
+            fresh[c] = ring.tile([P, 2, HEAD], F32, name="fresh", tag="fresh", bufs=3)
+            nc.scalar.activation(out=fresh[c][:, 1, :], in_=low[c][:], func=ACT.Exp, scale=-1.0)
 
         grouped_c = {}
         conv_bank = {}
@@ -177,28 +186,56 @@ def tile_slstmblock_pa_e_kernel(
                 nc.scalar.activation(out=grouped_c[g][:, r * P:(r + 1) * P, :],
                                      in_=conv_bank[(g, r)][:].rearrange("p t b -> p b t"), func=ACT.Silu)
 
+        all_banks = {}
+
+        def to_rows(c, names):
+            g, r, rows, cols = chunk_rows_cols(c)
+            all_banks.setdefault(c, {})
+            for gate in names:
+                all_banks[c][gate] = psum.tile([P, HEAD], F32, name="bank_" + gate, tag={"z": "z", "i": "a", "o": "o"}[gate])
+                for j in range(BLOCKS):
+                    nc.tensor.transpose(out=all_banks[c][gate][:, j * P:(j + 1) * P],
+                                        in_=gate_t[(gate, g)][:, j, r * P:(r + 1) * P],
+                                        identity=ident_f32[:])
+
         with tc.tile_pool(name="pre", bufs=1) as pre:
             x_sb = pre.tile([P, ROW_TILES, FEATURES], BF16, name="x_sb")
             vec_rows = pre.tile([P, FEATURES], BF16, name="vec_rows")
 
-            with tc.tile_pool(name="early", bufs=1) as early:
-                h_sb = early.tile([P, ROW_TILES, FEATURES], BF16, name="h_sb")
+            if True:
+                h_sb = pre.tile([P, ROW_TILES, FEATURES], BF16, name="h_sb")
+                centred = pre.tile([P, ROW_TILES, PAD + FEATURES], F32, name="centred")
 
+                nc.vector.memset(warm_in[:], 1.0)
                 nc.vector.memset(vec_rows[:].bitcast(I32), 0)
-                nc.vector.memset(vec_rows[32:33, :], 1.0)
                 nc.vector.memset(tap_coef[:], 0.0)
                 nc.vector.memset(gain_pick[:], 0.0)
                 nc.vector.memset(gain_pick[64:65, :], 1.0)
-                nc.vector.memset(warm_in[:], 1.0)
-                nc.vector.memset(planes[:].rearrange("p w n -> p (w n)").bitcast(I32), 0)
                 nc.vector.memset(two_eps[:], 2.0e-6)
+                nc.vector.memset(centred[:, :, 0:PAD], 0.0)
 
                 make_identity(nc, ident_f32[:])
+                nc.gpsimd.memset(planes[:].rearrange("p w n -> p (w n)").bitcast(I32), 0)
+                nc.gpsimd.memset(vec_rows[32:33, :], 1.0)
+                nc.gpsimd.memset(minus_half[:], -0.5)
                 make_identity(nc, ident_bf16[:])
+                nc.gpsimd.tensor_tensor(out=bias_pick[:].rearrange("p q c -> p (q c)"), in0=ident_bf16[:, 0:P // 2],
+                                        in1=ident_bf16[:, P // 2:P], op=ALU.add)
+                for gate in ("f", "o"):
+                    q = GATES.index(gate)
+                    nc.gpsimd.tensor_scalar(out=bias_pick[:, q, :], in0=bias_pick[:, q, :], scalar1=GATE_SCALE[gate],
+                                            scalar2=0.0, op0=ALU.mult, op1=ALU.add)
+                nc.gpsimd.tensor_scalar(out=minus_ident[:], in0=ident_bf16[:], scalar1=-1.0, scalar2=0.0,
+                                        op0=ALU.mult, op1=ALU.add)
 
                 for r in range(ROW_TILES):
-                    nc.sync.dma_start(out=x_sb[:, r, :], in_=x[r * P:(r + 1) * P, :])
+                    for half in range(2):
+                        cols = slice(half * FEATURES // 2, (half + 1) * FEATURES // 2)
+                        nc.sync.dma_start(out=x_sb[:, r, cols], in_=x[r * P:(r + 1) * P, cols])
                 nc.sync.dma_start(out=vec_rows[64:65, :], in_=ln_g.rearrange("(o d) -> o d", o=1))
+                nc.sync.dma_start(out=taps_bf16[:], in_=conv_w.partition_broadcast(P))
+                for r in range(ROW_TILES):
+                    nc.sync.dma_start(out=h_sb[:, r, :], in_=h_prev[r * P:(r + 1) * P, :])
                 nc.sync.dma_start(out=tap_coef[0:TAPS, :], in_=conv_w.rearrange("(k o) -> k o", o=1))
                 for j in range(TAPS):
                     shift = TAPS - 1 - j
@@ -207,9 +244,6 @@ def tile_slstmblock_pa_e_kernel(
                         in_=ln_b.rearrange("(o d) -> o d", o=1)[:, 0:FEATURES - shift],
                     )
                 nc.sync.dma_start(out=tap_coef[32:33, :], in_=conv_b.rearrange("(k o) -> k o", o=1))
-                nc.sync.dma_start(out=taps_bf16[:], in_=conv_w.partition_broadcast(P))
-                for r in range(ROW_TILES):
-                    nc.sync.dma_start(out=h_sb[:, r, :], in_=h_prev[r * P:(r + 1) * P, :])
                 for i, name in enumerate(WEIGHTS):
                     nc.sync.dma_start(
                         out=bias_rows[16 * i:16 * (i + 1), :],
@@ -219,36 +253,37 @@ def tile_slstmblock_pa_e_kernel(
                     load_words(name, 0)
                 for name in ("wz", "rz", "wo", "ro"):
                     load_planes(name)
-                for name in ("wz", "rz", "wo", "ro"):
-                    load_words(name, 1)
                 for name in ("wi", "ri", "wf", "rf"):
                     load_planes(name)
                 for name in ("wi", "ri", "wf", "rf"):
                     load_words(name, 0)
                 for r in range(ROW_TILES):
                     nc.sync.dma_start(out=m_sb[:, r, :], in_=m_prev[r * P:(r + 1) * P, :])
+                for name in ("wi", "ri", "wf", "rf"):
+                    load_words(name, 1)
                 for r in range(ROW_TILES):
                     for s, state in enumerate((c_prev, n_prev)):
                         nc.sync.dma_start(out=cn_sb[:, s, r, :], in_=state[r * P:(r + 1) * P, :])
-                for name in ("wi", "ri", "wf", "rf"):
+                for name in ("wz", "rz", "wo", "ro"):
                     load_words(name, 1)
                 for g in range(2, HEADS):
-                    for name in WEIGHTS:
+                    for name in ("wi", "ri", "wf", "rf", "wz", "rz", "wo", "ro"):
                         load_words(name, g)
 
-                nc.scalar.activation(out=warm_out[:, 0, 0:1], in_=warm_in[:], func=ACT.Sqrt)
+                nc.gpsimd.tensor_copy(out=coef_wide[:], in_=tap_coef[:].to_broadcast([P, P]))
+
+                nc.scalar.activation(out=warm_out[:], in_=warm_in[:], func=ACT.Silu)
 
                 gain_bank = {}
 
-                def spread_vectors(g):
+                def spread_gain(g):
                     cols = slice(g * HEAD, (g + 1) * HEAD)
                     gain_bank[g] = psum.tile([P, HEAD], F32, name="gain_bank", tag=("z", "a", "o")[g % 3])
                     nc.tensor.matmul(out=gain_bank[g][:], lhsT=gain_pick[:].to_broadcast([P, P]),
                                      rhs=vec_rows[:, cols], start=True, stop=True)
 
-
                 def words_to_partitions(src, g):
-                    bank = psum.tile([P, 2, ROWS], F32, name="word_bank", tag="turn", bufs=2)
+                    bank = psum.tile([P, 2, ROWS], F32, name="word_bank", tag="turn", bufs=3)
                     for r in range(ROW_TILES):
                         src_words = src[:, r, :].bitcast(F32)
                         for u in range(2):
@@ -257,8 +292,8 @@ def tile_slstmblock_pa_e_kernel(
                                 in_=src_words[:, (HEAD // 2) * g + u:(HEAD // 2) * (g + 1):2],
                                 identity=ident_f32[:],
                             )
-                    grouped = early.tile([P, ROWS, PACK], BF16, name="grouped", tag="grouped", bufs=4,
-                                       align_bytes=64)
+                    grouped = pre.tile([P, ROWS, PACK], BF16, name="grouped", tag="sorted", bufs=8,
+                                         align_bytes=64)
                     nc.scalar.copy(out=grouped[:].bitcast(F32), in_=bank[:].rearrange("p u b -> p b u"))
                     return grouped
 
@@ -266,38 +301,6 @@ def tile_slstmblock_pa_e_kernel(
                     for g in range(HEADS):
                         nc.vector.bn_stats(out=stats[:, r, g, :], in_=x_sb[:, r, g * HEAD:(g + 1) * HEAD])
                     nc.vector.bn_aggr(out=mean_var[:, r, :], in_=stats[:, r, :, :].rearrange("p g s -> p (g s)"))
-
-                grouped_x = [words_to_partitions(x_sb, g) for g in range(HEADS)]
-                row_stats(0)
-                for g in range(HEADS):
-                    quantise(grouped_x[g], "x", g)
-                grouped_h = [words_to_partitions(h_sb, g) for g in range(HEADS)]
-                spread_vectors(0)
-                spread_vectors(1)
-                spread_vectors(2)
-                bias_bank = psum.tile([P, P], BF16, name="bias_bank", tag="turn", bufs=2)
-                nc.tensor.transpose(out=bias_bank[:], in_=bias_rows[:], identity=ident_bf16[:])
-                row_stats(1)
-                nc.vector.tensor_scalar_add(out=var_eps[:], in0=mean_var[:, :, 1], scalar1=1.0e-5)
-                nc.scalar.activation(out=std[:], in_=var_eps[:], func=ACT.Sqrt)
-                nc.scalar.activation(out=warm_out[:, 1, 0:1], in_=warm_in[:], func=ACT.Silu)
-                for g in range(HEADS):
-                    quantise(grouped_h[g], "h", g)
-
-            with tc.tile_pool(name="conv", bufs=1, reuse_waits="tile") as conv:
-                centred = conv.tile([P, ROW_TILES, PAD + FEATURES], F32, name="centred")
-                nc.vector.memset(centred[:, :, 0:PAD], 0.0)
-                nc.vector.reciprocal(out=rstd[:], in_=std[:])
-                for r in range(ROW_TILES):
-                    nc.vector.tensor_scalar_mul(out=taps_rstd[:, r, :], in0=taps_bf16[:], scalar1=rstd[:, r:r + 1])
-                nc.vector.tensor_copy(out=bias_t[:].rearrange("p s q c -> p (s q c)"), in_=bias_bank[:])
-                nc.vector.tensor_tensor(out=bias_cols[:], in0=bias_t[:, 0, :, :], in1=bias_t[:, 1, :, :], op=ALU.add)
-                for gate in ("f", "o"):
-                    q = GATES.index(gate)
-                    nc.vector.tensor_scalar_mul(out=bias_cols[:, q, :], in0=bias_cols[:, q, :],
-                                                scalar1=GATE_SCALE[gate])
-                nc.vector.tensor_scalar_mul(out=minus_ident[:], in0=ident_bf16[:], scalar1=-1.0)
-                nc.vector.tensor_copy(out=coef_wide[:], in_=tap_coef[:].to_broadcast([P, P]))
 
                 def centre(g):
                     for r in range(ROW_TILES):
@@ -307,125 +310,145 @@ def tile_slstmblock_pa_e_kernel(
                             in1=gain_bank[g][:], op0=ALU.subtract, op1=ALU.mult,
                         )
 
-                conv_sum = {}
-                conv_planes = {}
+                even_taps = {}
+                tap_pairs = {}
 
-                def tap(g, j):
+                def moved(g, r, j):
                     first = PAD + g * HEAD + j - (TAPS - 1)
-                    for r in range(ROW_TILES):
-                        moved = centred[:, r, first:first + HEAD]
-                        coef = taps_rstd[:, r, j:j + 1]
-                        if j == 0:
-                            conv_sum[r] = conv.tile([P, HEAD], F32, name="conv_sum", tag="conv_sum", bufs=2)
-                            nc.vector.tensor_scalar_mul(out=conv_sum[r][:], in0=moved, scalar1=coef)
-                        elif j < TAPS - 1:
-                            nc.vector.scalar_tensor_tensor(
-                                out=conv_sum[r][:], in0=moved, scalar=coef, in1=conv_sum[r][:],
-                                op0=ALU.mult, op1=ALU.add)
+                    return centred[:, r, first:first + HEAD]
+
+                def taps_even(g, r):
+                    for j in (0, 2):
+                        even_taps[(r, j)] = pre.tile([P, HEAD], F32, name="even_taps", tag="even_taps", bufs=4)
+                        if j in SCALAR_TAPS[g]:
+                            nc.scalar.activation(out=even_taps[(r, j)][:], in_=moved(g, r, j), func=ACT.Copy,
+                                                 scale=taps_rstd[:, r, j:j + 1])
                         else:
-                            conv_planes[r] = conv.tile([P, PACK, P], F32, name="conv_planes", tag="conv_planes", bufs=4)
-                            nc.vector.scalar_tensor_tensor(
-                                out=conv_planes[r][:].rearrange("p t q -> p q t"),
-                                in0=moved.rearrange("p (q t) -> p q t", t=PACK), scalar=coef,
-                                in1=conv_sum[r][:].rearrange("p (q t) -> p q t", t=PACK),
-                                op0=ALU.mult, op1=ALU.add)
+                            nc.vector.tensor_scalar_mul(out=even_taps[(r, j)][:], in0=moved(g, r, j),
+                                                        scalar1=taps_rstd[:, r, j:j + 1])
 
-                def turn_conv(g):
-                    for r in range(ROW_TILES):
-                        conv_bank[(g, r)] = psum.tile([P, PACK, P], F32, name="conv_bank", tag="turn", bufs=2)
-                        for t in range(PACK):
-                            nc.tensor.matmul(out=conv_bank[(g, r)][:, t, :],
-                                             lhsT=vec_rows[:, g * HEAD + t:(g + 1) * HEAD:PACK], rhs=coef_wide[:],
-                                             start=True, stop=False)
-                            nc.tensor.matmul(out=conv_bank[(g, r)][:, t, :], lhsT=conv_planes[r][:, t, :],
-                                             rhs=ident_f32[:], is_transpose=True, start=False, stop=True)
+                def taps_odd(g, r):
+                    for j in (1, 3):
+                        tap_pairs[(r, j)] = pre.tile([P, PACK, P], F32, name="tap_pairs", tag="sorted", bufs=8, align_bytes=64)
+                        nc.vector.scalar_tensor_tensor(
+                            out=tap_pairs[(r, j)][:].rearrange("p t q -> p q t"),
+                            in0=moved(g, r, j).rearrange("p (q t) -> p q t", t=PACK),
+                            scalar=taps_rstd[:, r, j:j + 1],
+                            in1=even_taps[(r, j - 1)][:].rearrange("p (q t) -> p q t", t=PACK),
+                            op0=ALU.mult, op1=ALU.add)
 
+                def turn_conv(g, r):
+                    conv_bank[(g, r)] = psum.tile([P, PACK, P], F32, name="conv_bank", tag="turn", bufs=3)
+                    for t in range(PACK):
+                        nc.tensor.matmul(out=conv_bank[(g, r)][:, t, :],
+                                         lhsT=vec_rows[:, g * HEAD + t:(g + 1) * HEAD:PACK], rhs=coef_wide[:],
+                                         start=True, stop=False)
+                        for j in (1, 3):
+                            nc.tensor.matmul(out=conv_bank[(g, r)][:, t, :], lhsT=tap_pairs[(r, j)][:, t, :],
+                                             rhs=ident_f32[:], is_transpose=True, start=False, stop=j == 3)
+
+                row_stats(0)
+                row_stats(1)
+                nc.vector.tensor_scalar_add(out=var_eps[:], in0=mean_var[:, :, 1], scalar1=1.0e-5)
+                nc.gpsimd.tensor_tensor(out=rstd[:], in0=var_eps[:], in1=minus_half[:], op=ALU.pow)
+                grouped_x = [words_to_partitions(x_sb, g) for g in range(HEADS)]
+                for g in range(3):
+                    spread_gain(g)
+                grouped_h = [words_to_partitions(h_sb, g) for g in range(2)]
+                centre(0)
+                for r in range(ROW_TILES):
+                    nc.vector.tensor_scalar_mul(out=taps_rstd[:, r, :], in0=taps_bf16[:], scalar1=rstd[:, r:r + 1])
+                for r in range(ROW_TILES):
+                    taps_even(0, r)
+                grouped_h.extend([words_to_partitions(h_sb, g) for g in range(2, HEADS)])
+                bias_bank = psum.tile([P, HEAD], F32, name="bias_bank", tag="turn", bufs=3)
+                nc.tensor.matmul(out=bias_bank[:, 0:P // 2], lhsT=bias_rows[:],
+                                 rhs=bias_pick[:].rearrange("p q c -> p (q c)"), start=True, stop=True)
+                centre(1)
                 for g in range(HEADS):
-                    if g >= 2:
-                        quantise(grouped_c[g - 2], "c", g - 2)
-                    centre(g)
-                    tap(g, 0)
-                    if g + 3 < HEADS:
-                        spread_vectors(g + 3)
-                    if g >= 1:
-                        silu_head(g - 1)
-                    if g == 0:
-                        gates(0, ("z", "o"))
+                    quantise(grouped_x[g], "x", g)
+                for r in range(ROW_TILES):
+                    taps_odd(0, r)
+                    turn_conv(0, r)
+                for r in range(ROW_TILES):
+                    taps_even(1, r)
+                nc.vector.tensor_copy(out=bias_cols[:].rearrange("p q c -> p (q c)"), in_=bias_bank[:, 0:P // 2])
+                spread_gain(3)
+                for g in range(HEADS):
+                    quantise(grouped_h[g], "h", g)
+                silu_head(0)
+                gates(0, ("z", "o"))
+                for g in range(1, HEADS):
+                    if g + 1 < HEADS:
+                        centre(g + 1)
+                    for r in range(ROW_TILES):
+                        taps_odd(g, r)
+                        turn_conv(g, r)
+                        if g + 1 < HEADS:
+                            taps_even(g + 1, r)
+                    quantise(grouped_c[g - 1], "c", g - 1)
+                    silu_head(g)
                     if g == 1:
-                        gates(1, ("z", "o"))
-                    if g == 2:
                         gates(0, ("i", "f"))
+                    if g == 2:
                         difference(0)
-                    if g == 3:
-                        gate_exps(0)
-                        difference(1)
-                        gate_exps(1)
-                    for j in range(1, TAPS):
-                        tap(g, j)
-                    turn_conv(g)
+                gates(1, ("i", "f"), True)
+                gate_exps(0)
+                quantise(grouped_c[3], "c", 3)
+                to_rows(0, ("z", "i", "o"))
+                difference(1)
+                gate_exps(1)
+                difference(2)
+                gates(1, ("z",))
+                gates(1, ("o",))
 
         with tc.tile_pool(name="late", bufs=1, reuse_waits="tile") as late:
-            n_all = late.tile([P, CHUNKS, HEAD], F32, name="n_all")
+            state = {}
             oc_all = late.tile([P, CHUNKS, HEAD], F32, name="oc_all")
-            recip_all = late.tile([P, CHUNKS, HEAD], F32, name="recip_all")
-
-            all_banks = {}
-
-            def to_rows(c):
-                g, r, rows, cols = chunk_rows_cols(c)
-                all_banks[c] = {}
-                for gate, tag in (("z", "z"), ("i", "a"), ("o", "o")):
-                    all_banks[c][gate] = psum.tile([P, HEAD], F32, name="bank_" + gate, tag=tag)
-                    for j in range(BLOCKS):
-                        nc.tensor.transpose(out=all_banks[c][gate][:, j * P:(j + 1) * P],
-                                            in_=gate_t[(gate, g)][:, j, r * P:(r + 1) * P],
-                                            identity=ident_f32[:])
 
             def update(c):
                 g, r, rows, cols = chunk_rows_cols(c)
                 banks = all_banks[c]
-                ig = exps[c][:, 0, :]
-                kept = ring.tile([P, 2, HEAD], F32, name="kept", tag="kept", bufs=1)
-                nc.vector.tensor_tensor(out=kept[:], in0=exps[c][:, 1:2, :].to_broadcast([P, 2, HEAD]),
-                                        in1=cn_sb[:, :, r, cols], op=ALU.mult)
-                fresh = ring.tile([P, HEAD], F32, name="fresh", tag="fresh", bufs=1)
-                nc.vector.tensor_tensor(out=fresh[:], in0=banks["z"][:], in1=ig, op=ALU.mult)
-                nc.vector.tensor_tensor(out=n_all[:, c, :], in0=kept[:, 1, :], in1=ig, op=ALU.add)
-                nc.sync.dma_start(out=out_2[rows, cols], in_=n_all[:, c, :])
-                c_t = ring.tile([P, HEAD], F32, name="c_t", tag="c_t")
-                nc.vector.tensor_tensor(out=c_t[:], in0=kept[:, 0, :], in1=fresh[:], op=ALU.add)
-                nc.sync.dma_start(out=out_1[rows, cols], in_=c_t[:])
+                state[c] = late.tile([P, 2, HEAD], F32, name="state", tag="state", bufs=CHUNKS)
+                nc.vector.scalar_tensor_tensor(out=state[c][:], in0=keep_gate[c][:].to_broadcast([P, 2, HEAD]), scalar=1.0,
+                                               in1=cn_sb[:, :, r, cols], op0=ALU.min, op1=ALU.mult)
+                nc.vector.tensor_tensor(out=fresh[c][:, 0, :], in0=banks["z"][:], in1=fresh[c][:, 1, :], op=ALU.mult)
                 m_t = ring.tile([P, HEAD], F32, name="m_t", tag="m_t")
-                nc.vector.tensor_tensor(out=m_t[:], in0=banks["i"][:], in1=relus[c][:, 0, :], op=ALU.add)
+                nc.vector.tensor_tensor(out=m_t[:], in0=banks["i"][:], in1=low[c][:], op=ALU.add)
                 nc.sync.dma_start(out=out_3[rows, cols], in_=m_t[:])
-                nc.vector.scalar_tensor_tensor(out=oc_all[:, c, :], in0=banks["o"][:], scalar=1.0, in1=c_t[:],
+                nc.vector.tensor_tensor(out=state[c][:], in0=state[c][:], in1=fresh[c][:], op=ALU.add)
+                nc.sync.dma_start(out=out_1[rows, cols], in_=state[c][:, 0, :])
+                nc.sync.dma_start(out=out_2[rows, cols], in_=state[c][:, 1, :])
+                nc.vector.scalar_tensor_tensor(out=oc_all[:, c, :], in0=banks["o"][:], scalar=1.0, in1=state[c][:, 0, :],
                                                op0=ALU.add, op1=ALU.mult)
 
-            quantise(grouped_c[2], "c", 2)
-            to_rows(0)
-            gates(1, ("i", "f"))
+            def root(c):
+                recip = late.tile([P, HEAD], F32, name="recip", tag="recip", bufs=6)
+                nc.scalar.activation(out=recip[:], in_=state[c][:, 1, :], func=ACT.Abs_reciprocal_sqrt,
+                                     bias=two_eps[:, 0:1], scale=2.0)
+                nc.scalar.activation(out=recip[:], in_=recip[:], func=ACT.Square)
+                return recip
+
+            def finish(c, recip):
+                g, r, rows, cols = chunk_rows_cols(c)
+                nc.vector.tensor_tensor(out=oc_all[:, c, :], in0=oc_all[:, c, :], in1=recip[:], op=ALU.mult)
+                nc.sync.dma_start(out=out_0[rows, cols], in_=oc_all[:, c, :])
+
+            gates_at = {0: ((2, "f"), (2, "i")), 1: ((2, "z"), (2, "o")), 2: ((3, "f"), (3, "i")), 3: ((3, "z"),), 4: ((3, "o"),)}
             for c in range(CHUNKS):
                 update(c)
-                if c == 0:
-                    silu_head(3)
-                if c == 1:
-                    quantise(grouped_c[3], "c", 3)
-                for g in (2, 3):
-                    k = c - (ROW_TILES * g - len(GATES))
-                    if 0 <= k < len(GATES):
-                        gates(g, (GATES[k],))
-                if c + 2 < CHUNKS:
-                    difference(c + 2)
-                    gate_exps(c + 2)
+                coming = gates_at.get(c, ())
+                for g, gate in coming[:1]:
+                    gates(g, (gate,))
                 if c + 1 < CHUNKS:
-                    to_rows(c + 1)
-
+                    to_rows(c + 1, ("z", "i"))
+                if c + 2 < CHUNKS:
+                    gate_exps(c + 2)
+                if c + 3 < CHUNKS:
+                    difference(c + 3)
+                for g, gate in coming[1:]:
+                    gates(g, (gate,))
+                if c + 1 < CHUNKS:
+                    to_rows(c + 1, ("o",))
             for c in range(CHUNKS):
-                nc.scalar.activation(out=recip_all[:, c, :], in_=n_all[:, c, :], func=ACT.Ln,
-                                     bias=two_eps[:, 0:1], scale=2.0)
-            for c in range(CHUNKS):
-                g, r, rows, cols = chunk_rows_cols(c)
-                nc.scalar.activation(out=recip_all[:, c, :], in_=recip_all[:, c, :], func=ACT.Exp, scale=-1.0)
-                nc.vector.tensor_tensor(out=oc_all[:, c, :], in0=oc_all[:, c, :], in1=recip_all[:, c, :],
-                                        op=ALU.mult)
-                nc.sync.dma_start(out=out_0[rows, cols], in_=oc_all[:, c, :])
+                finish(c, root(c))

@@ -249,14 +249,9 @@ def tile_slstmblock_pa_e_kernel(
                         out=bias_rows[16 * i:16 * (i + 1), :],
                         in_=biases[name].rearrange("(c f) -> c f", f=P),
                     )
-                for name in ("wz", "rz", "wo", "ro"):
+                for name in ("wz", "rz", "wo", "ro", "wi", "ri", "wf", "rf"):
                     load_words(name, 0)
-                for name in ("wz", "rz", "wo", "ro"):
                     load_planes(name)
-                for name in ("wi", "ri", "wf", "rf"):
-                    load_planes(name)
-                for name in ("wi", "ri", "wf", "rf"):
-                    load_words(name, 0)
                 for r in range(ROW_TILES):
                     nc.sync.dma_start(out=m_sb[:, r, :], in_=m_prev[r * P:(r + 1) * P, :])
                 for name in ("wi", "ri", "wf", "rf"):

@@ -401,12 +401,18 @@ def tile_slstmblock_pa_e_kernel(
             state = {}
             oc_all = late.tile([P, CHUNKS, HEAD], F32, name="oc_all")
 
+            def gate_output(c):
+                nc.vector.scalar_tensor_tensor(out=oc_all[:, c, :], in0=all_banks[c]["o"][:], scalar=1.0,
+                                               in1=state[c][:, 0, :], op0=ALU.add, op1=ALU.mult)
+
             def update(c):
                 g, r, rows, cols = chunk_rows_cols(c)
                 banks = all_banks[c]
                 state[c] = late.tile([P, 2, HEAD], F32, name="state", tag="state", bufs=CHUNKS)
                 nc.vector.scalar_tensor_tensor(out=state[c][:], in0=keep_gate[c][:].to_broadcast([P, 2, HEAD]), scalar=1.0,
                                                in1=cn_sb[:, :, r, cols], op0=ALU.min, op1=ALU.mult)
+                if c > 0:
+                    gate_output(c - 1)
                 nc.vector.tensor_tensor(out=fresh[c][:, 0, :], in0=banks["z"][:], in1=fresh[c][:, 1, :], op=ALU.mult)
                 m_t = ring.tile([P, HEAD], F32, name="m_t", tag="m_t")
                 nc.vector.tensor_tensor(out=m_t[:], in0=banks["i"][:], in1=low[c][:], op=ALU.add)
@@ -414,27 +420,30 @@ def tile_slstmblock_pa_e_kernel(
                 nc.vector.tensor_tensor(out=state[c][:], in0=state[c][:], in1=fresh[c][:], op=ALU.add)
                 nc.sync.dma_start(out=out_1[rows, cols], in_=state[c][:, 0, :])
                 nc.sync.dma_start(out=out_2[rows, cols], in_=state[c][:, 1, :])
-                nc.vector.scalar_tensor_tensor(out=oc_all[:, c, :], in0=banks["o"][:], scalar=1.0, in1=state[c][:, 0, :],
-                                               op0=ALU.add, op1=ALU.mult)
 
-            def root(c):
-                recip = late.tile([P, HEAD], F32, name="recip", tag="recip", bufs=6)
-                nc.scalar.activation(out=recip[:], in_=state[c][:, 1, :], func=ACT.Abs_reciprocal_sqrt,
+            recip = {}
+
+            def inverse_root(c):
+                recip[c] = late.tile([P, HEAD], F32, name="recip", tag="recip", bufs=6)
+                nc.scalar.activation(out=recip[c][:], in_=state[c][:, 1, :], func=ACT.Abs_reciprocal_sqrt,
                                      bias=two_eps[:, 0:1], scale=2.0)
-                nc.scalar.activation(out=recip[:], in_=recip[:], func=ACT.Square)
-                return recip
 
-            def finish(c, recip):
+            def inverse(c):
+                nc.scalar.activation(out=recip[c][:], in_=recip[c][:], func=ACT.Square)
+
+            def finish(c):
                 g, r, rows, cols = chunk_rows_cols(c)
-                nc.vector.tensor_tensor(out=oc_all[:, c, :], in0=oc_all[:, c, :], in1=recip[:], op=ALU.mult)
+                nc.vector.tensor_tensor(out=oc_all[:, c, :], in0=oc_all[:, c, :], in1=recip[c][:], op=ALU.mult)
                 nc.sync.dma_start(out=out_0[rows, cols], in_=oc_all[:, c, :])
 
-            gates_at = {0: ((2, "f"), (2, "i")), 1: ((2, "z"), (2, "o")), 2: ((3, "f"), (3, "i")), 3: ((3, "z"),), 4: ((3, "o"),)}
+            gates_at = {0: ((2, "f"), (2, "i")), 1: ((2, "z"),), 2: ((2, "o"), (3, "i")), 3: ((3, "f"), (3, "z")), 4: ((3, "o"),)}
             for c in range(CHUNKS):
                 update(c)
                 coming = gates_at.get(c, ())
                 for g, gate in coming[:1]:
                     gates(g, (gate,))
+                if c > 0:
+                    to_rows(c, ("o",))
                 if c + 1 < CHUNKS:
                     to_rows(c + 1, ("z", "i"))
                 if c + 2 < CHUNKS:
@@ -443,7 +452,12 @@ def tile_slstmblock_pa_e_kernel(
                     difference(c + 3)
                 for g, gate in coming[1:]:
                     gates(g, (gate,))
-                if c + 1 < CHUNKS:
-                    to_rows(c + 1, ("o",))
             for c in range(CHUNKS):
-                finish(c, root(c))
+                inverse_root(c)
+                if c > 0:
+                    inverse(c - 1)
+                    finish(c - 1)
+                if c == 2:
+                    gate_output(CHUNKS - 1)
+            inverse(CHUNKS - 1)
+            finish(CHUNKS - 1)

@@ -342,11 +342,20 @@ def tile_slstmblock_pa_e_kernel(
                             nc.tensor.matmul(out=conv_bank[(g, r)][:, t, :], lhsT=tap_pairs[(r, j)][:, t, :],
                                              rhs=ident_f32[:], is_transpose=True, start=False, stop=j == 3)
 
+                def keep_clock(n):
+                    for i in range(n):
+                        clock_bank = psum.tile([P, 2, ROWS], F32, name="clock_bank", tag="acc", bufs=2)
+                        nc.tensor.matmul(out=clock_bank[:, 0, 0:P], lhsT=ident_f32[:], rhs=ident_f32[:], start=True, stop=True)
+
+                keep_clock(8)
                 row_stats(0)
                 row_stats(1)
                 nc.vector.tensor_scalar_add(out=var_eps[:], in0=mean_var[:, :, 1], scalar1=1.0e-5)
                 nc.gpsimd.tensor_tensor(out=rstd[:], in0=var_eps[:], in1=minus_half[:], op=ALU.pow)
-                grouped_x = [words_to_partitions(x_sb, g) for g in range(HEADS)]
+                grouped_x = []
+                for g in range(HEADS):
+                    grouped_x.append(words_to_partitions(x_sb, g))
+                    keep_clock(1)
                 for g in range(3):
                     spread_gain(g)
                 grouped_h = [words_to_partitions(h_sb, g) for g in range(2)]
@@ -355,13 +364,16 @@ def tile_slstmblock_pa_e_kernel(
                     nc.vector.tensor_scalar_mul(out=taps_rstd[:, r, :], in0=taps_bf16[:], scalar1=rstd[:, r:r + 1])
                 for r in range(ROW_TILES):
                     taps_even(0, r)
-                grouped_h.extend([words_to_partitions(h_sb, g) for g in range(2, HEADS)])
+                for g in range(2, HEADS):
+                    grouped_h.append(words_to_partitions(h_sb, g))
+                    keep_clock(1)
                 bias_bank = psum.tile([P, HEAD], F32, name="bias_bank", tag="turn", bufs=3)
                 nc.tensor.matmul(out=bias_bank[:, 0:P // 2], lhsT=bias_rows[:],
                                  rhs=bias_pick[:].rearrange("p q c -> p (q c)"), start=True, stop=True)
                 centre(1)
                 for g in range(HEADS):
                     quantise(grouped_x[g], "x", g)
+                keep_clock(2)
                 for r in range(ROW_TILES):
                     taps_odd(0, r)
                     turn_conv(0, r)

@@ -84,6 +84,7 @@ def tile_slstmblock_pa_e_kernel(
         rstd = keep.tile([P, ROW_TILES], F32, name="rstd")
         taps_rstd = keep.tile([P, ROW_TILES, TAPS], F32, name="taps_rstd")
         two_eps = keep.tile([P, 1], F32, name="two_eps")
+        clock_zeros = keep.tile([P, P], F32, name="clock_zeros")
         warm_in = keep.tile([P, 1], F32, name="warm_in")
         warm_out = keep.tile([P, 1], F32, name="warm_out")
 
@@ -206,6 +207,7 @@ def tile_slstmblock_pa_e_kernel(
                 h_sb = pre.tile([P, ROW_TILES, FEATURES], BF16, name="h_sb")
                 centred = pre.tile([P, ROW_TILES, PAD + FEATURES], F32, name="centred")
 
+                nc.vector.memset(clock_zeros[:], 0.0)
                 nc.vector.memset(warm_in[:], 1.0)
                 nc.vector.memset(vec_rows[:].bitcast(I32), 0)
                 nc.vector.memset(tap_coef[:], 0.0)
@@ -228,8 +230,8 @@ def tile_slstmblock_pa_e_kernel(
                 nc.gpsimd.tensor_scalar(out=minus_ident[:], in0=ident_bf16[:], scalar1=-1.0, scalar2=0.0,
                                         op0=ALU.mult, op1=ALU.add)
 
-                for r in range(ROW_TILES):
-                    for half in range(2):
+                for half in range(2):
+                    for r in range(ROW_TILES):
                         cols = slice(half * FEATURES // 2, (half + 1) * FEATURES // 2)
                         nc.sync.dma_start(out=x_sb[:, r, cols], in_=x[r * P:(r + 1) * P, cols])
                 nc.sync.dma_start(out=vec_rows[64:65, :], in_=ln_g.rearrange("(o d) -> o d", o=1))
@@ -292,10 +294,13 @@ def tile_slstmblock_pa_e_kernel(
                     nc.scalar.copy(out=grouped[:].bitcast(F32), in_=bank[:].rearrange("p u b -> p b u"))
                     return grouped
 
-                def row_stats(r):
-                    for g in range(HEADS):
-                        nc.vector.bn_stats(out=stats[:, r, g, :], in_=x_sb[:, r, g * HEAD:(g + 1) * HEAD])
-                    nc.vector.bn_aggr(out=mean_var[:, r, :], in_=stats[:, r, :, :].rearrange("p g s -> p (g s)"))
+                def row_stats():
+                    for half in range(2):
+                        for r in range(ROW_TILES):
+                            for g in range(half * HEADS // 2, (half + 1) * HEADS // 2):
+                                nc.vector.bn_stats(out=stats[:, r, g, :], in_=x_sb[:, r, g * HEAD:(g + 1) * HEAD])
+                    for r in range(ROW_TILES):
+                        nc.vector.bn_aggr(out=mean_var[:, r, :], in_=stats[:, r, :, :].rearrange("p g s -> p (g s)"))
 
                 def centre(g):
                     for r in range(ROW_TILES):
@@ -345,11 +350,10 @@ def tile_slstmblock_pa_e_kernel(
                 def keep_clock(n):
                     for i in range(n):
                         clock_bank = psum.tile([P, 2, ROWS], F32, name="clock_bank", tag="acc", bufs=2)
-                        nc.tensor.matmul(out=clock_bank[:, 0, 0:P], lhsT=ident_f32[:], rhs=ident_f32[:], start=True, stop=True)
+                        nc.tensor.matmul(out=clock_bank[:, 0, 0:P], lhsT=clock_zeros[:], rhs=clock_zeros[:], start=True, stop=True)
 
-                keep_clock(8)
-                row_stats(0)
-                row_stats(1)
+                keep_clock(4)
+                row_stats()
                 nc.vector.tensor_scalar_add(out=var_eps[:], in0=mean_var[:, :, 1], scalar1=1.0e-5)
                 nc.gpsimd.tensor_tensor(out=rstd[:], in0=var_eps[:], in1=minus_half[:], op=ALU.pow)
                 grouped_x = []
@@ -403,11 +407,11 @@ def tile_slstmblock_pa_e_kernel(
                 gate_exps(0)
                 quantise(grouped_c[3], "c", 3)
                 to_rows(0, ("z", "i", "o"))
+                gates(1, ("z",))
                 difference(1)
                 gate_exps(1)
-                difference(2)
-                gates(1, ("z",))
                 gates(1, ("o",))
+                difference(2)
 
         with tc.tile_pool(name="late", bufs=1, reuse_waits="tile") as late:
             state = {}
@@ -423,13 +427,14 @@ def tile_slstmblock_pa_e_kernel(
                 state[c] = late.tile([P, 2, HEAD], F32, name="state", tag="state", bufs=CHUNKS)
                 nc.vector.scalar_tensor_tensor(out=state[c][:], in0=keep_gate[c][:].to_broadcast([P, 2, HEAD]), scalar=1.0,
                                                in1=cn_sb[:, :, r, cols], op0=ALU.min, op1=ALU.mult)
+                nc.gpsimd.tensor_tensor(out=state[c][:, 1, :], in0=state[c][:, 1, :], in1=fresh[c][:, 1, :], op=ALU.add)
                 if c > 0:
                     gate_output(c - 1)
                 nc.vector.tensor_tensor(out=fresh[c][:, 0, :], in0=banks["z"][:], in1=fresh[c][:, 1, :], op=ALU.mult)
                 m_t = ring.tile([P, HEAD], F32, name="m_t", tag="m_t")
                 nc.vector.tensor_tensor(out=m_t[:], in0=banks["i"][:], in1=low[c][:], op=ALU.add)
                 nc.sync.dma_start(out=out_3[rows, cols], in_=m_t[:])
-                nc.vector.tensor_tensor(out=state[c][:], in0=state[c][:], in1=fresh[c][:], op=ALU.add)
+                nc.vector.tensor_tensor(out=state[c][:, 0, :], in0=state[c][:, 0, :], in1=fresh[c][:, 0, :], op=ALU.add)
                 nc.sync.dma_start(out=out_1[rows, cols], in_=state[c][:, 0, :])
                 nc.sync.dma_start(out=out_2[rows, cols], in_=state[c][:, 1, :])
 

@@ -76,7 +76,6 @@ def tile_slstmblock_pa_e_kernel(
         tap_coef = keep.tile([P, 1], BF16, name="tap_coef")
         gain_pick = keep.tile([P, 1], BF16, name="gain_pick")
         coef_wide = keep.tile([P, P], BF16, name="coef_wide")
-        taps_bf16 = keep.tile([P, TAPS], BF16, name="taps_bf16")
         stats = keep.tile([P, ROW_TILES, HEADS, 6], F32, name="stats")
         mean_var = keep.tile([P, ROW_TILES, 2], F32, name="mean_var")
         var_eps = keep.tile([P, ROW_TILES], F32, name="var_eps")
@@ -235,10 +234,9 @@ def tile_slstmblock_pa_e_kernel(
                         cols = slice(half * FEATURES // 2, (half + 1) * FEATURES // 2)
                         nc.sync.dma_start(out=x_sb[:, r, cols], in_=x[r * P:(r + 1) * P, cols])
                 nc.sync.dma_start(out=vec_rows[64:65, :], in_=ln_g.rearrange("(o d) -> o d", o=1))
-                nc.sync.dma_start(out=taps_bf16[:], in_=conv_w.partition_broadcast(P))
+                nc.sync.dma_start(out=tap_coef[0:TAPS, :], in_=conv_w.rearrange("(k o) -> k o", o=1))
                 for r in range(ROW_TILES):
                     nc.sync.dma_start(out=h_sb[:, r, :], in_=h_prev[r * P:(r + 1) * P, :])
-                nc.sync.dma_start(out=tap_coef[0:TAPS, :], in_=conv_w.rearrange("(k o) -> k o", o=1))
                 for j in range(TAPS):
                     shift = TAPS - 1 - j
                     nc.sync.dma_start(
@@ -362,10 +360,13 @@ def tile_slstmblock_pa_e_kernel(
                     keep_clock(1)
                 for g in range(3):
                     spread_gain(g)
+                taps_bank = psum.tile([P, 2, ROWS], F32, name="taps_bank", tag="acc", bufs=2)
+                nc.tensor.matmul(out=taps_bank[:, 0, 0:TAPS], lhsT=tap_coef[:].to_broadcast([P, P]),
+                                 rhs=ident_bf16[:, 0:TAPS], start=True, stop=True)
                 grouped_h = [words_to_partitions(h_sb, g) for g in range(2)]
                 centre(0)
                 for r in range(ROW_TILES):
-                    nc.vector.tensor_scalar_mul(out=taps_rstd[:, r, :], in0=taps_bf16[:], scalar1=rstd[:, r:r + 1])
+                    nc.vector.tensor_scalar_mul(out=taps_rstd[:, r, :], in0=taps_bank[:, 0, 0:TAPS], scalar1=rstd[:, r:r + 1])
                 for r in range(ROW_TILES):
                     taps_even(0, r)
                 for g in range(2, HEADS):

@@ -201,6 +201,7 @@ def tile_slstmblock_pa_e_kernel(
         with tc.tile_pool(name="pre", bufs=1) as pre:
             x_sb = pre.tile([P, ROW_TILES, FEATURES], BF16, name="x_sb")
             vec_rows = pre.tile([P, FEATURES], BF16, name="vec_rows")
+            gain_rows = pre.tile([P, FEATURES], BF16, name="gain_rows")
 
             if True:
                 h_sb = pre.tile([P, ROW_TILES, FEATURES], BF16, name="h_sb")
@@ -211,11 +212,12 @@ def tile_slstmblock_pa_e_kernel(
                 nc.vector.memset(vec_rows[:].bitcast(I32), 0)
                 nc.vector.memset(tap_coef[:], 0.0)
                 nc.vector.memset(gain_pick[:], 0.0)
-                nc.vector.memset(gain_pick[64:65, :], 1.0)
+                nc.vector.memset(gain_pick[0:1, :], 1.0)
                 nc.vector.memset(two_eps[:], 2.0e-6)
                 nc.vector.memset(centred[:, :, 0:PAD], 0.0)
 
                 make_identity(nc, ident_f32[:])
+                nc.gpsimd.memset(gain_rows[:].bitcast(I32), 0)
                 nc.gpsimd.memset(planes[:].rearrange("p w n -> p (w n)").bitcast(I32), 0)
                 nc.gpsimd.memset(vec_rows[32:33, :], 1.0)
                 nc.gpsimd.memset(minus_half[:], -0.5)
@@ -233,8 +235,9 @@ def tile_slstmblock_pa_e_kernel(
                     for r in range(ROW_TILES):
                         cols = slice(half * FEATURES // 2, (half + 1) * FEATURES // 2)
                         nc.sync.dma_start(out=x_sb[:, r, cols], in_=x[r * P:(r + 1) * P, cols])
-                nc.sync.dma_start(out=vec_rows[64:65, :], in_=ln_g.rearrange("(o d) -> o d", o=1))
+                nc.sync.dma_start(out=gain_rows[0:1, :], in_=ln_g.rearrange("(o d) -> o d", o=1))
                 nc.sync.dma_start(out=tap_coef[0:TAPS, :], in_=conv_w.rearrange("(k o) -> k o", o=1))
+                nc.sync.dma_start(out=tap_coef[32:33, :], in_=conv_b.rearrange("(k o) -> k o", o=1))
                 for r in range(ROW_TILES):
                     nc.sync.dma_start(out=h_sb[:, r, :], in_=h_prev[r * P:(r + 1) * P, :])
                 for j in range(TAPS):
@@ -243,7 +246,6 @@ def tile_slstmblock_pa_e_kernel(
                         out=vec_rows[j:j + 1, shift:FEATURES],
                         in_=ln_b.rearrange("(o d) -> o d", o=1)[:, 0:FEATURES - shift],
                     )
-                nc.sync.dma_start(out=tap_coef[32:33, :], in_=conv_b.rearrange("(k o) -> k o", o=1))
                 for i, name in enumerate(WEIGHTS):
                     nc.sync.dma_start(
                         out=bias_rows[16 * i:16 * (i + 1), :],
@@ -275,7 +277,7 @@ def tile_slstmblock_pa_e_kernel(
                     cols = slice(g * HEAD, (g + 1) * HEAD)
                     gain_bank[g] = psum.tile([P, HEAD], F32, name="gain_bank", tag=("z", "a", "o")[g % 3])
                     nc.tensor.matmul(out=gain_bank[g][:], lhsT=gain_pick[:].to_broadcast([P, P]),
-                                     rhs=vec_rows[:, cols], start=True, stop=True)
+                                     rhs=gain_rows[:, cols], start=True, stop=True)
 
                 def words_to_partitions(src, g):
                     bank = psum.tile([P, 2, ROWS], F32, name="word_bank", tag="turn", bufs=3)
@@ -432,7 +434,7 @@ def tile_slstmblock_pa_e_kernel(
                 if c > 0:
                     gate_output(c - 1)
                 nc.vector.tensor_tensor(out=fresh[c][:, 0, :], in0=banks["z"][:], in1=fresh[c][:, 1, :], op=ALU.mult)
-                m_t = ring.tile([P, HEAD], F32, name="m_t", tag="m_t")
+                m_t = late.tile([P, HEAD], F32, name="m_t", tag="m_t", bufs=2)
                 nc.vector.tensor_tensor(out=m_t[:], in0=banks["i"][:], in1=low[c][:], op=ALU.add)
                 nc.sync.dma_start(out=out_3[rows, cols], in_=m_t[:])
                 nc.vector.tensor_tensor(out=state[c][:, 0, :], in0=state[c][:, 0, :], in1=fresh[c][:, 0, :], op=ALU.add)
@@ -449,33 +451,41 @@ def tile_slstmblock_pa_e_kernel(
             def inverse(c):
                 nc.scalar.activation(out=recip[c][:], in_=recip[c][:], func=ACT.Square)
 
-            def finish(c):
-                g, r, rows, cols = chunk_rows_cols(c)
+            def times_recip(c):
                 nc.vector.tensor_tensor(out=oc_all[:, c, :], in0=oc_all[:, c, :], in1=recip[c][:], op=ALU.mult)
+
+            def store_h(c):
+                g, r, rows, cols = chunk_rows_cols(c)
                 nc.sync.dma_start(out=out_0[rows, cols], in_=oc_all[:, c, :])
 
-            gates_at = {0: ((2, "f"), (2, "i")), 1: ((2, "z"),), 2: ((2, "o"), (3, "i")), 3: ((3, "f"), (3, "z")), 4: ((3, "o"),)}
+            gates_at = {0: ((2, "f"), (2, "i")), 1: ((2, "z"),), 2: ((2, "o"), (3, "i")), 3: ((3, "f"),), 4: ((3, "z"),), 5: ((3, "o"),)}
             for c in range(CHUNKS):
                 update(c)
                 coming = gates_at.get(c, ())
-                for g, gate in coming[:1]:
-                    gates(g, (gate,))
                 if c > 0:
                     to_rows(c, ("o",))
                 if c + 1 < CHUNKS:
                     to_rows(c + 1, ("z", "i"))
                 if c + 2 < CHUNKS:
                     gate_exps(c + 2)
+                for g, gate in coming[:1]:
+                    gates(g, (gate,))
                 if c + 3 < CHUNKS:
                     difference(c + 3)
                 for g, gate in coming[1:]:
                     gates(g, (gate,))
-            for c in range(CHUNKS):
+            for c in range(ROW_TILES):
                 inverse_root(c)
-                if c > 0:
-                    inverse(c - 1)
-                    finish(c - 1)
+            for c in (0, 1, 0, 1):
+                times_recip(c)
+            for c in range(ROW_TILES):
+                store_h(c)
+            inverse_root(2)
+            for c in range(2, CHUNKS):
+                if c + 1 < CHUNKS:
+                    inverse_root(c + 1)
+                inverse(c)
+                times_recip(c)
+                store_h(c)
                 if c == 2:
                     gate_output(CHUNKS - 1)
-            inverse(CHUNKS - 1)
-            finish(CHUNKS - 1)

@@ -171,7 +171,10 @@ def tile_slstmblock_pa_e_kernel(
 
         def gate_exps(c):
             low[c] = ring.tile([P, HEAD], F32, name="low", tag="low", bufs=3)
-            nc.scalar.activation(out=low[c][:], in_=d_banks[c][:], func=ACT.Relu, scale=-1.0)
+            if c >= ROW_TILES:
+                nc.vector.tensor_scalar(out=low[c][:], in0=d_banks[c][:], scalar1=-1.0, scalar2=0.0, op0=ALU.mult, op1=ALU.max)
+            else:
+                nc.scalar.activation(out=low[c][:], in_=d_banks[c][:], func=ACT.Relu, scale=-1.0)
             keep_gate[c] = ring.tile([P, 1, HEAD], F32, name="keep_gate", tag="keep_gate", bufs=3)
             nc.scalar.activation(out=keep_gate[c][:, 0, :], in_=d_banks[c][:], func=ACT.Exp, scale=-1.0)
             fresh[c] = ring.tile([P, 2, HEAD], F32, name="fresh", tag="fresh", bufs=3)

@@ -23,6 +23,7 @@ BLOCKS = HEAD // P
 CHUNKS = HEADS * ROW_TILES
 TAPS = 4
 SCALAR_TAPS = ((0, 2), (0, 2), (0,), ())
+CHAINED = (2, 3)
 PAD = 8
 
 WEIGHTS = ("wz", "wi", "wf", "wo", "rz", "ri", "rf", "ro")
@@ -314,14 +315,14 @@ def tile_slstmblock_pa_e_kernel(
                         )
 
                 even_taps = {}
-                tap_pairs = {}
+                tap_sums = {}
 
                 def moved(g, r, j):
                     first = PAD + g * HEAD + j - (TAPS - 1)
                     return centred[:, r, first:first + HEAD]
 
                 def taps_even(g, r):
-                    for j in (0, 2):
+                    for j in (0,) if g in CHAINED else (0, 2):
                         even_taps[(r, j)] = pre.tile([P, HEAD], F32, name="even_taps", tag="even_taps", bufs=4)
                         if j in SCALAR_TAPS[g]:
                             nc.scalar.activation(out=even_taps[(r, j)][:], in_=moved(g, r, j), func=ACT.Copy,
@@ -330,24 +331,43 @@ def tile_slstmblock_pa_e_kernel(
                             nc.vector.tensor_scalar_mul(out=even_taps[(r, j)][:], in0=moved(g, r, j),
                                                         scalar1=taps_rstd[:, r, j:j + 1])
 
-                def taps_odd(g, r):
-                    for j in (1, 3):
-                        tap_pairs[(r, j)] = pre.tile([P, PACK, P], F32, name="tap_pairs", tag="sorted", bufs=8, align_bytes=64)
-                        nc.vector.scalar_tensor_tensor(
-                            out=tap_pairs[(r, j)][:].rearrange("p t q -> p q t"),
-                            in0=moved(g, r, j).rearrange("p (q t) -> p q t", t=PACK),
-                            scalar=taps_rstd[:, r, j:j + 1],
-                            in1=even_taps[(r, j - 1)][:].rearrange("p (q t) -> p q t", t=PACK),
-                            op0=ALU.mult, op1=ALU.add)
+                def add_tap(g, r, j, base):
+                    nc.vector.scalar_tensor_tensor(out=even_taps[(r, base)][:], in0=moved(g, r, j), scalar=taps_rstd[:, r, j:j + 1],
+                                                   in1=even_taps[(r, base)][:], op0=ALU.mult, op1=ALU.add)
+
+                def last_tap(g, r, j, base):
+                    tap_sums[(r, j)] = pre.tile([P, PACK, P], F32, name="tap_sums", tag="sorted", bufs=8, align_bytes=64)
+                    nc.vector.scalar_tensor_tensor(
+                        out=tap_sums[(r, j)][:].rearrange("p t q -> p q t"),
+                        in0=moved(g, r, j).rearrange("p (q t) -> p q t", t=PACK),
+                        scalar=taps_rstd[:, r, j:j + 1],
+                        in1=even_taps[(r, base)][:].rearrange("p (q t) -> p q t", t=PACK),
+                        op0=ALU.mult, op1=ALU.add)
+
+                def conv_head(g):
+                    if g in CHAINED:
+                        for j in (1, 2):
+                            for r in range(ROW_TILES):
+                                add_tap(g, r, j, 0)
+                    for r in range(ROW_TILES):
+                        if g in CHAINED:
+                            last_tap(g, r, 3, 0)
+                        else:
+                            for j in (1, 3):
+                                last_tap(g, r, j, j - 1)
+                        turn_conv(g, r)
+                        if 0 < g < HEADS - 1:
+                            taps_even(g + 1, r)
 
                 def turn_conv(g, r):
+                    sums = (3,) if g in CHAINED else (1, 3)
                     conv_bank[(g, r)] = psum.tile([P, PACK, P], F32, name="conv_bank", tag="turn", bufs=3)
                     for t in range(PACK):
                         nc.tensor.matmul(out=conv_bank[(g, r)][:, t, :],
                                          lhsT=vec_rows[:, g * HEAD + t:(g + 1) * HEAD:PACK], rhs=coef_wide[:],
                                          start=True, stop=False)
-                        for j in (1, 3):
-                            nc.tensor.matmul(out=conv_bank[(g, r)][:, t, :], lhsT=tap_pairs[(r, j)][:, t, :],
+                        for j in sums:
+                            nc.tensor.matmul(out=conv_bank[(g, r)][:, t, :], lhsT=tap_sums[(r, j)][:, t, :],
                                              rhs=ident_f32[:], is_transpose=True, start=False, stop=j == 3)
 
                 def keep_clock(n):
@@ -384,9 +404,7 @@ def tile_slstmblock_pa_e_kernel(
                 for g in range(HEADS):
                     quantise(grouped_x[g], "x", g)
                 keep_clock(2)
-                for r in range(ROW_TILES):
-                    taps_odd(0, r)
-                    turn_conv(0, r)
+                conv_head(0)
                 for r in range(ROW_TILES):
                     taps_even(1, r)
                 nc.vector.tensor_copy(out=bias_cols[:].rearrange("p q c -> p (q c)"), in_=bias_bank[:, 0:P // 2])
@@ -398,11 +416,7 @@ def tile_slstmblock_pa_e_kernel(
                 for g in range(1, HEADS):
                     if g + 1 < HEADS:
                         centre(g + 1)
-                    for r in range(ROW_TILES):
-                        taps_odd(g, r)
-                        turn_conv(g, r)
-                        if g + 1 < HEADS:
-                            taps_even(g + 1, r)
+                    conv_head(g)
                     quantise(grouped_c[g - 1], "c", g - 1)
                     silu_head(g)
                     if g == 1:

@@ -22,14 +22,14 @@ HEAD = FEATURES // HEADS
 BLOCKS = HEAD // P
 CHUNKS = HEADS * ROW_TILES
 TAPS = 4
-SCALAR_TAPS = ((0, 2), (0, 2), (0,), ())
-CHAINED = (2, 3)
+SCALAR_TAPS = ((0, 2), (0, 2), (0, 2), ())
+CHAINED = (3,)
 PAD = 8
 
 WEIGHTS = ("wz", "wi", "wf", "wo", "rz", "ri", "rf", "ro")
 GATES = ("z", "i", "f", "o")
-GATE_FUNC = {"z": ACT.Tanh, "i": ACT.Identity, "f": ACT.Identity, "o": ACT.Tanh}
-GATE_SCALE = {"z": 1.0, "i": 1.0, "f": -1.0, "o": 0.5}
+GATE_FUNC = {"z": ACT.Tanh, "i": ACT.Identity, "o": ACT.Tanh}
+GATE_SCALE = {"z": 1.0, "i": 1.0, "o": 0.5}
 
 FLOPS = 2 * len(WEIGHTS) * ROWS * FEATURES * HEAD
 
@@ -70,7 +70,6 @@ def tile_slstmblock_pa_e_kernel(
         cn_sb = keep.tile([P, 2, ROW_TILES, FEATURES], BF16, name="cn_sb")
         ident_f32 = keep.tile([P, P], F32, name="ident_f32")
         ident_bf16 = keep.tile([P, P], BF16, name="ident_bf16")
-        minus_ident = keep.tile([P, P], BF16, name="minus_ident")
         bias_rows = keep.tile([P, P], BF16, name="bias_rows")
         bias_pick = keep.tile([P, len(GATES), HEADS * BLOCKS], BF16, name="bias_pick")
         bias_cols = keep.tile([P, len(GATES), HEADS * BLOCKS], F32, name="bias_cols")
@@ -127,20 +126,39 @@ def tile_slstmblock_pa_e_kernel(
             else:
                 nc.scalar.activation(out=out, in_=acc, func=GATE_FUNC[gate], bias=bias, scale=GATE_SCALE[gate])
 
+        def products(acc, gate, g, pair):
+            operand = "x" if gate in ("z", "o") else "c"
+            for s in range(2):
+                j = 2 * pair + s
+                mx_pass(acc[:, s, :], "w" + gate, operand, g, j, True, False)
+                mx_pass(acc[:, s, :], "r" + gate, "h", g, j, False, True)
+
         def gates(g, names, on_vector=False):
             for gate in names:
-                operand = "x" if gate in ("z", "o") else "c"
-                gate_t[(gate, g)] = ring.tile([P, BLOCKS, ROWS], F32, name="gate_t_" + gate,
-                                              tag="gate_t_" + gate, bufs=3 if gate == "z" else 2)
+                gate_t[(gate, g)] = ring.tile([P, BLOCKS, ROWS], F32, name="gate_t_" + gate, tag="gate_t_" + gate, bufs=2)
                 for pair in range(BLOCKS // 2):
                     acc = psum.tile([P, 2, ROWS], F32, name="acc", tag="acc", bufs=2)
-                    for s in range(2):
-                        j = 2 * pair + s
-                        mx_pass(acc[:, s, :], "w" + gate, operand, g, j, True, False)
-                        mx_pass(acc[:, s, :], "r" + gate, "h", g, j, False, True)
+                    products(acc, gate, g, pair)
                     for s in range(2):
                         j = 2 * pair + s
                         leave_psum(gate_t[(gate, g)][:, j, :], acc[:, s, :], gate, g * BLOCKS + j, on_vector)
+
+        f_acc = {}
+
+        def forget_products(g, pair, tag, bufs=1):
+            f_acc[(g, pair)] = psum.tile([P, 2, ROWS], F32, name="f_acc", tag=tag, bufs=bufs)
+            products(f_acc[(g, pair)], "f", g, pair)
+
+        def forget_minus_input(g, pair):
+            if pair == 0:
+                gate_t[("f", g)] = ring.tile([P, BLOCKS, ROWS], F32, name="gate_t_f", tag="gate_t_f", bufs=2)
+            for s in range(2):
+                j = 2 * pair + s
+                col = g * BLOCKS + j
+                nc.vector.scalar_tensor_tensor(
+                    out=gate_t[("f", g)][:, j, :], in0=f_acc[(g, pair)][:, s, :],
+                    scalar=bias_cols[:, GATES.index("f"), col:col + 1], in1=gate_t[("i", g)][:, j, :],
+                    op0=ALU.add, op1=ALU.subtract)
 
         def quantise(grouped, name, g):
             batch = slice(g * ROWS, (g + 1) * ROWS)
@@ -154,30 +172,23 @@ def tile_slstmblock_pa_e_kernel(
         keep_gate = {}
         fresh = {}
 
-        def add_back_to_rows(bank, gate, g, r, stop):
-            for j in range(BLOCKS):
-                nc.tensor.matmul(
-                    out=bank[:, j * P:(j + 1) * P], lhsT=gate_t[(gate, g)][:, j, r * P:(r + 1) * P],
-                    rhs=ident_f32[:], is_transpose=True, start=False, stop=stop and j == BLOCKS - 1,
-                )
-
         d_banks = {}
 
         def difference(c):
             g, r, rows, cols = chunk_rows_cols(c)
             d_banks[c] = psum.tile([P, HEAD], F32, name="d_bank", tag="turn", bufs=3)
-            nc.tensor.matmul(out=d_banks[c][:], lhsT=minus_ident[:], rhs=m_sb[:, r, cols], start=True, stop=False)
-            add_back_to_rows(d_banks[c], "i", g, r, False)
-            add_back_to_rows(d_banks[c], "f", g, r, True)
+            nc.tensor.matmul(out=d_banks[c][:], lhsT=ident_bf16[:], rhs=m_sb[:, r, cols], start=True, stop=False)
+            for j in range(BLOCKS):
+                nc.tensor.matmul(
+                    out=d_banks[c][:, j * P:(j + 1) * P], lhsT=gate_t[("f", g)][:, j, r * P:(r + 1) * P],
+                    rhs=ident_f32[:], is_transpose=True, start=False, stop=j == BLOCKS - 1,
+                )
 
         def gate_exps(c):
             low[c] = ring.tile([P, HEAD], F32, name="low", tag="low", bufs=3)
-            if c >= ROW_TILES:
-                nc.vector.tensor_scalar(out=low[c][:], in0=d_banks[c][:], scalar1=-1.0, scalar2=0.0, op0=ALU.mult, op1=ALU.max)
-            else:
-                nc.scalar.activation(out=low[c][:], in_=d_banks[c][:], func=ACT.Relu, scale=-1.0)
+            nc.scalar.activation(out=low[c][:], in_=d_banks[c][:], func=ACT.Relu)
             keep_gate[c] = ring.tile([P, 1, HEAD], F32, name="keep_gate", tag="keep_gate", bufs=3)
-            nc.scalar.activation(out=keep_gate[c][:, 0, :], in_=d_banks[c][:], func=ACT.Exp, scale=-1.0)
+            nc.scalar.activation(out=keep_gate[c][:, 0, :], in_=d_banks[c][:], func=ACT.Exp)
             fresh[c] = ring.tile([P, 2, HEAD], F32, name="fresh", tag="fresh", bufs=3)
             nc.scalar.activation(out=fresh[c][:, 1, :], in_=low[c][:], func=ACT.Exp, scale=-1.0)
 
@@ -228,12 +239,9 @@ def tile_slstmblock_pa_e_kernel(
                 make_identity(nc, ident_bf16[:])
                 nc.gpsimd.tensor_tensor(out=bias_pick[:].rearrange("p q c -> p (q c)"), in0=ident_bf16[:, 0:P // 2],
                                         in1=ident_bf16[:, P // 2:P], op=ALU.add)
-                for gate in ("f", "o"):
-                    q = GATES.index(gate)
-                    nc.gpsimd.tensor_scalar(out=bias_pick[:, q, :], in0=bias_pick[:, q, :], scalar1=GATE_SCALE[gate],
-                                            scalar2=0.0, op0=ALU.mult, op1=ALU.add)
-                nc.gpsimd.tensor_scalar(out=minus_ident[:], in0=ident_bf16[:], scalar1=-1.0, scalar2=0.0,
-                                        op0=ALU.mult, op1=ALU.add)
+                q = GATES.index("o")
+                nc.gpsimd.tensor_scalar(out=bias_pick[:, q, :], in0=bias_pick[:, q, :], scalar1=GATE_SCALE["o"],
+                                        scalar2=0.0, op0=ALU.mult, op1=ALU.add)
 
                 for half in range(2):
                     for r in range(ROW_TILES):
@@ -417,13 +425,20 @@ def tile_slstmblock_pa_e_kernel(
                     if g + 1 < HEADS:
                         centre(g + 1)
                     conv_head(g)
+                    if g == 3:
+                        for pair in range(BLOCKS // 2):
+                            forget_minus_input(0, pair)
                     quantise(grouped_c[g - 1], "c", g - 1)
                     silu_head(g)
                     if g == 1:
-                        gates(0, ("i", "f"))
-                    if g == 2:
-                        difference(0)
-                gates(1, ("i", "f"), True)
+                        gates(0, ("i",))
+                        forget_products(0, 0, "a")
+                        forget_products(0, 1, "o")
+                difference(0)
+                gates(1, ("i",), True)
+                for pair in range(BLOCKS // 2):
+                    forget_products(1, pair, "acc", 2)
+                    forget_minus_input(1, pair)
                 gate_exps(0)
                 quantise(grouped_c[3], "c", 3)
                 to_rows(0, ("z", "i", "o"))
@@ -454,11 +469,15 @@ def tile_slstmblock_pa_e_kernel(
                 m_t = late.tile([P, HEAD], F32, name="m_t", tag="m_t", bufs=2)
                 nc.vector.tensor_tensor(out=m_t[:], in0=banks["i"][:], in1=low[c][:], op=ALU.add)
                 nc.sync.dma_start(out=out_3[rows, cols], in_=m_t[:])
+                if c in forget_at:
+                    for pair in range(BLOCKS // 2):
+                        forget_minus_input(forget_at[c], pair)
                 nc.vector.tensor_tensor(out=state[c][:, 0, :], in0=state[c][:, 0, :], in1=fresh[c][:, 0, :], op=ALU.add)
                 nc.sync.dma_start(out=out_1[rows, cols], in_=state[c][:, 0, :])
                 nc.sync.dma_start(out=out_2[rows, cols], in_=state[c][:, 1, :])
 
             recip = {}
+            forget_at = {1: 2, 3: 3}
 
             def inverse_root(c):
                 recip[c] = late.tile([P, HEAD], F32, name="recip", tag="recip", bufs=6)
@@ -475,7 +494,7 @@ def tile_slstmblock_pa_e_kernel(
                 g, r, rows, cols = chunk_rows_cols(c)
                 nc.sync.dma_start(out=out_0[rows, cols], in_=oc_all[:, c, :])
 
-            gates_at = {0: ((2, "f"), (2, "i")), 1: ((2, "z"),), 2: ((2, "o"), (3, "i")), 3: ((3, "f"),), 4: ((3, "z"),), 5: ((3, "o"),)}
+            gates_at = {0: ((2, "i"), (2, "f")), 1: ((2, "z"),), 2: ((3, "i"), (3, "f")), 3: ((2, "o"),), 4: ((3, "z"),), 5: ((3, "o"),)}
             for c in range(CHUNKS):
                 update(c)
                 coming = gates_at.get(c, ())
@@ -490,7 +509,8 @@ def tile_slstmblock_pa_e_kernel(
                 if c + 3 < CHUNKS:
                     difference(c + 3)
                 for g, gate in coming[1:]:
-                    gates(g, (gate,))
+                    for pair in range(BLOCKS // 2):
+                        forget_products(g, pair, "turn", 3)
             for c in range(ROW_TILES):
                 inverse_root(c)
             for c in (0, 1, 0, 1):

@@ -91,10 +91,10 @@ def tile_slstmblock_pa_e_kernel(
             g, r = divmod(c, ROW_TILES)
             return g, r, slice(r * P, (r + 1) * P), slice(g * HEAD, (g + 1) * HEAD)
 
-        def load_words(name, g):
+        def load_words(name, first, last):
             nc.sync.dma_start(
-                out=words_sb[name][:, g, :].bitcast(I32),
-                in_=word_bytes[name][g].rearrange("p n t -> p (n t)").bitcast(I32),
+                out=words_sb[name][:, first:last, :].bitcast(I32),
+                in_=word_bytes[name][first:last].rearrange("g p n t -> p g (n t)").bitcast(I32),
             )
 
         def load_planes(name):
@@ -250,8 +250,7 @@ def tile_slstmblock_pa_e_kernel(
                 nc.sync.dma_start(out=gain_rows[0:1, :], in_=ln_g.rearrange("(o d) -> o d", o=1))
                 nc.sync.dma_start(out=tap_coef[0:TAPS, :], in_=conv_w.rearrange("(k o) -> k o", o=1))
                 nc.sync.dma_start(out=tap_coef[32:33, :], in_=conv_b.rearrange("(k o) -> k o", o=1))
-                for r in range(ROW_TILES):
-                    nc.sync.dma_start(out=h_sb[:, r, :], in_=h_prev[r * P:(r + 1) * P, :])
+                nc.sync.dma_start(out=h_sb[:], in_=h_prev.rearrange("(r p) d -> p r d", p=P))
                 for j in range(TAPS):
                     shift = TAPS - 1 - j
                     nc.sync.dma_start(
@@ -263,21 +262,20 @@ def tile_slstmblock_pa_e_kernel(
                         out=bias_rows[16 * i:16 * (i + 1), :],
                         in_=biases[name].rearrange("(c f) -> c f", f=P),
                     )
-                for name in ("wz", "rz", "wo", "ro", "wi", "ri", "wf", "rf"):
-                    load_words(name, 0)
+                for name in ("wz", "rz", "wi", "ri", "wf", "rf", "wo", "ro"):
+                    load_words(name, 0, 1)
                     load_planes(name)
-                for r in range(ROW_TILES):
-                    nc.sync.dma_start(out=m_sb[:, r, :], in_=m_prev[r * P:(r + 1) * P, :])
+                nc.sync.dma_start(out=m_sb[:], in_=m_prev.rearrange("(r p) d -> p r d", p=P))
                 for name in ("wi", "ri", "wf", "rf"):
-                    load_words(name, 1)
-                for r in range(ROW_TILES):
-                    for s, state in enumerate((c_prev, n_prev)):
-                        nc.sync.dma_start(out=cn_sb[:, s, r, :], in_=state[r * P:(r + 1) * P, :])
-                for name in ("wz", "rz", "wo", "ro"):
-                    load_words(name, 1)
-                for g in range(2, HEADS):
-                    for name in ("wi", "ri", "wf", "rf", "wz", "rz", "wo", "ro"):
-                        load_words(name, g)
+                    load_words(name, 1, 2)
+                for name in ("wz", "rz"):
+                    load_words(name, 1, 2)
+                for s, state in enumerate((c_prev, n_prev)):
+                    nc.sync.dma_start(out=cn_sb[:, s, :, :], in_=state.rearrange("(r p) d -> p r d", p=P))
+                for name in ("wo", "ro"):
+                    load_words(name, 1, 2)
+                for name in ("wi", "ri", "wf", "rf", "wz", "rz", "wo", "ro"):
+                    load_words(name, 2, HEADS)
 
                 nc.gpsimd.tensor_copy(out=coef_wide[:], in_=tap_coef[:].to_broadcast([P, P]))
 
@@ -420,7 +418,7 @@ def tile_slstmblock_pa_e_kernel(
                 for g in range(HEADS):
                     quantise(grouped_h[g], "h", g)
                 silu_head(0)
-                gates(0, ("z", "o"))
+                gates(0, ("z",))
                 for g in range(1, HEADS):
                     if g + 1 < HEADS:
                         centre(g + 1)
@@ -430,6 +428,8 @@ def tile_slstmblock_pa_e_kernel(
                             forget_minus_input(0, pair)
                     quantise(grouped_c[g - 1], "c", g - 1)
                     silu_head(g)
+                    if g == 2:
+                        gates(0, ("o",))
                     if g == 1:
                         gates(0, ("i",))
                         forget_products(0, 0, "a")
@@ -469,12 +469,12 @@ def tile_slstmblock_pa_e_kernel(
                 m_t = late.tile([P, HEAD], F32, name="m_t", tag="m_t", bufs=2)
                 nc.vector.tensor_tensor(out=m_t[:], in0=banks["i"][:], in1=low[c][:], op=ALU.add)
                 nc.sync.dma_start(out=out_3[rows, cols], in_=m_t[:])
-                if c in forget_at:
-                    for pair in range(BLOCKS // 2):
-                        forget_minus_input(forget_at[c], pair)
                 nc.vector.tensor_tensor(out=state[c][:, 0, :], in0=state[c][:, 0, :], in1=fresh[c][:, 0, :], op=ALU.add)
                 nc.sync.dma_start(out=out_1[rows, cols], in_=state[c][:, 0, :])
                 nc.sync.dma_start(out=out_2[rows, cols], in_=state[c][:, 1, :])
+                if c in forget_at:
+                    for pair in range(BLOCKS // 2):
+                        forget_minus_input(forget_at[c], pair)
 
             recip = {}
             forget_at = {1: 2, 3: 3}

@@ -22,7 +22,7 @@ HEAD = FEATURES // HEADS
 BLOCKS = HEAD // P
 CHUNKS = HEADS * ROW_TILES
 TAPS = 4
-SCALAR_TAPS = ((0, 2), (0, 2), (0, 2), ())
+SCALAR_TAPS = ((0, 2), (0, 2), (0, 2), (0,))
 CHAINED = (3,)
 PAD = 8
 
@@ -263,17 +263,11 @@ def tile_slstmblock_pa_e_kernel(
                         in_=biases[name].rearrange("(c f) -> c f", f=P),
                     )
                 for name in ("wz", "rz", "wi", "ri", "wf", "rf", "wo", "ro"):
-                    load_words(name, 0, 1)
+                    load_words(name, 0, 2)
                     load_planes(name)
                 nc.sync.dma_start(out=m_sb[:], in_=m_prev.rearrange("(r p) d -> p r d", p=P))
-                for name in ("wi", "ri", "wf", "rf"):
-                    load_words(name, 1, 2)
-                for name in ("wz", "rz"):
-                    load_words(name, 1, 2)
                 for s, state in enumerate((c_prev, n_prev)):
                     nc.sync.dma_start(out=cn_sb[:, s, :, :], in_=state.rearrange("(r p) d -> p r d", p=P))
-                for name in ("wo", "ro"):
-                    load_words(name, 1, 2)
                 for name in ("wi", "ri", "wf", "rf", "wz", "rz", "wo", "ro"):
                     load_words(name, 2, HEADS)
 

@@ -22,8 +22,8 @@ HEAD = FEATURES // HEADS
 BLOCKS = HEAD // P
 CHUNKS = HEADS * ROW_TILES
 TAPS = 4
-SCALAR_TAPS = ((0, 2), (0, 2), (0, 2), (0,))
-CHAINED = (3,)
+SCALAR_TAPS = ((0, 2), (0, 2), (0,), (0,))
+CHAINED = (2, 3)
 PAD = 8
 
 WEIGHTS = ("wz", "wi", "wf", "wo", "rz", "ri", "rf", "ro")

@@ -27,6 +27,7 @@ CHAINED = (2, 3)
 PAD = 8
 
 WEIGHTS = ("wz", "wi", "wf", "wo", "rz", "ri", "rf", "ro")
+BIAS_GROUPS = (("wz", "wi", "rz", "ri"), ("wf", "wo", "rf", "ro"))
 GATES = ("z", "i", "f", "o")
 GATE_FUNC = {"z": ACT.Tanh, "i": ACT.Identity, "o": ACT.Tanh}
 GATE_SCALE = {"z": 1.0, "i": 1.0, "o": 0.5}
@@ -69,13 +70,14 @@ def tile_slstmblock_pa_e_kernel(
         m_sb = keep.tile([P, ROW_TILES, FEATURES], BF16, name="m_sb")
         cn_sb = keep.tile([P, 2, ROW_TILES, FEATURES], BF16, name="cn_sb")
         ident_f32 = keep.tile([P, P], F32, name="ident_f32")
-        ident_bf16 = keep.tile([P, P], BF16, name="ident_bf16")
-        bias_rows = keep.tile([P, P], BF16, name="bias_rows")
-        bias_pick = keep.tile([P, len(GATES), HEADS * BLOCKS], BF16, name="bias_pick")
+        ident_wide = keep.tile([P, PACK + P], BF16, name="ident_wide")
+        ident_bf16 = ident_wide[:, PACK:PACK + P]
+        bias_rows = keep.tile([P, 2, P], BF16, name="bias_rows")
+        bias_pick = keep.tile([P, 2, 2, HEADS * BLOCKS], BF16, name="bias_pick")
         bias_cols = keep.tile([P, len(GATES), HEADS * BLOCKS], F32, name="bias_cols")
         tap_coef = keep.tile([P, 1], BF16, name="tap_coef")
         gain_pick = keep.tile([P, 1], BF16, name="gain_pick")
-        coef_wide = keep.tile([P, P], BF16, name="coef_wide")
+        tap_shift = keep.tile([P, PACK, P], BF16, name="tap_shift")
         stats = keep.tile([P, ROW_TILES, HEADS, 6], F32, name="stats")
         mean_var = keep.tile([P, ROW_TILES, 2], F32, name="mean_var")
         var_eps = keep.tile([P, ROW_TILES], F32, name="var_eps")
@@ -177,7 +179,7 @@ def tile_slstmblock_pa_e_kernel(
         def difference(c):
             g, r, rows, cols = chunk_rows_cols(c)
             d_banks[c] = psum.tile([P, HEAD], F32, name="d_bank", tag="turn", bufs=3)
-            nc.tensor.matmul(out=d_banks[c][:], lhsT=ident_bf16[:], rhs=m_sb[:, r, cols], start=True, stop=False)
+            nc.tensor.matmul(out=d_banks[c][:], lhsT=ident_bf16, rhs=m_sb[:, r, cols], start=True, stop=False)
             for j in range(BLOCKS):
                 nc.tensor.matmul(
                     out=d_banks[c][:, j * P:(j + 1) * P], lhsT=gate_t[("f", g)][:, j, r * P:(r + 1) * P],
@@ -222,6 +224,7 @@ def tile_slstmblock_pa_e_kernel(
                 h_sb = pre.tile([P, ROW_TILES, FEATURES], BF16, name="h_sb")
                 centred = pre.tile([P, ROW_TILES, PAD + FEATURES], F32, name="centred")
 
+                nc.vector.memset(bias_rows[:].rearrange("p a f -> p (a f)").bitcast(I32), 0)
                 nc.vector.memset(clock_zeros[:], 0.0)
                 nc.vector.memset(warm_in[:], 1.0)
                 nc.vector.memset(vec_rows[:].bitcast(I32), 0)
@@ -231,38 +234,44 @@ def tile_slstmblock_pa_e_kernel(
                 nc.vector.memset(two_eps[:], 2.0e-6)
                 nc.vector.memset(centred[:, :, 0:PAD], 0.0)
 
-                make_identity(nc, ident_f32[:])
                 nc.gpsimd.memset(gain_rows[:].bitcast(I32), 0)
+                make_identity(nc, ident_f32[:])
                 nc.gpsimd.memset(planes[:].rearrange("p w n -> p (w n)").bitcast(I32), 0)
-                nc.gpsimd.memset(vec_rows[32:33, :], 1.0)
+                nc.gpsimd.memset(vec_rows[32:32 + PACK, :], 1.0)
                 nc.gpsimd.memset(minus_half[:], -0.5)
-                make_identity(nc, ident_bf16[:])
-                nc.gpsimd.tensor_tensor(out=bias_pick[:].rearrange("p q c -> p (q c)"), in0=ident_bf16[:, 0:P // 2],
-                                        in1=ident_bf16[:, P // 2:P], op=ALU.add)
-                q = GATES.index("o")
-                nc.gpsimd.tensor_scalar(out=bias_pick[:, q, :], in0=bias_pick[:, q, :], scalar1=GATE_SCALE["o"],
+                nc.gpsimd.memset(ident_wide[:, 0:PACK], 0.0)
+                make_identity(nc, ident_bf16)
+                for a in range(2):
+                    nc.gpsimd.tensor_tensor(out=bias_pick[:, a, :, :].rearrange("p q c -> p (q c)"), in0=ident_bf16[:, 0:P // 4],
+                                            in1=ident_bf16[:, P // 4:P // 2], op=ALU.add)
+                nc.gpsimd.tensor_scalar(out=bias_pick[:, 1, 1, :], in0=bias_pick[:, 1, 1, :], scalar1=GATE_SCALE["o"],
                                         scalar2=0.0, op0=ALU.mult, op1=ALU.add)
 
-                for half in range(2):
-                    for r in range(ROW_TILES):
-                        cols = slice(half * FEATURES // 2, (half + 1) * FEATURES // 2)
-                        nc.sync.dma_start(out=x_sb[:, r, cols], in_=x[r * P:(r + 1) * P, cols])
+                half = FEATURES // 2
+                for r in range(ROW_TILES):
+                    nc.sync.dma_start(out=x_sb[:, r, 0:half], in_=x[r * P:(r + 1) * P, 0:half])
+                nc.sync.dma_start(out=x_sb[:, :, half:FEATURES], in_=x[:, half:FEATURES].rearrange("(r p) d -> p r d", p=P))
+
+                def load_biases(group):
+                    for i, name in enumerate(BIAS_GROUPS[group]):
+                        nc.sync.dma_start(out=bias_rows[16 * i:16 * (i + 1), group, :], in_=biases[name].rearrange("(c f) -> c f", f=P))
+
+                load_biases(0)
                 nc.sync.dma_start(out=gain_rows[0:1, :], in_=ln_g.rearrange("(o d) -> o d", o=1))
+                nc.sync.dma_start(out=h_sb[:], in_=h_prev.rearrange("(r p) d -> p r d", p=P))
                 nc.sync.dma_start(out=tap_coef[0:TAPS, :], in_=conv_w.rearrange("(k o) -> k o", o=1))
                 nc.sync.dma_start(out=tap_coef[32:33, :], in_=conv_b.rearrange("(k o) -> k o", o=1))
-                nc.sync.dma_start(out=h_sb[:], in_=h_prev.rearrange("(r p) d -> p r d", p=P))
-                for j in range(TAPS):
-                    shift = TAPS - 1 - j
+                for s in range(TAPS + PACK - 1):
+                    shift = s - (TAPS - 1)
                     nc.sync.dma_start(
-                        out=vec_rows[j:j + 1, shift:FEATURES],
-                        in_=ln_b.rearrange("(o d) -> o d", o=1)[:, 0:FEATURES - shift],
+                        out=vec_rows[s:s + 1, max(0, -shift):FEATURES - max(0, shift)],
+                        in_=ln_b.rearrange("(o d) -> o d", o=1)[:, max(0, shift):FEATURES - max(0, -shift)],
                     )
-                for i, name in enumerate(WEIGHTS):
-                    nc.sync.dma_start(
-                        out=bias_rows[16 * i:16 * (i + 1), :],
-                        in_=biases[name].rearrange("(c f) -> c f", f=P),
-                    )
-                for name in ("wz", "rz", "wi", "ri", "wf", "rf", "wo", "ro"):
+                for name in ("wz", "rz", "wi", "ri", "wf", "rf"):
+                    load_words(name, 0, 2)
+                    load_planes(name)
+                load_biases(1)
+                for name in ("wo", "ro"):
                     load_words(name, 0, 2)
                     load_planes(name)
                 nc.sync.dma_start(out=m_sb[:], in_=m_prev.rearrange("(r p) d -> p r d", p=P))
@@ -270,8 +279,6 @@ def tile_slstmblock_pa_e_kernel(
                     nc.sync.dma_start(out=cn_sb[:, s, :, :], in_=state.rearrange("(r p) d -> p r d", p=P))
                 for name in ("wi", "ri", "wf", "rf", "wz", "rz", "wo", "ro"):
                     load_words(name, 2, HEADS)
-
-                nc.gpsimd.tensor_copy(out=coef_wide[:], in_=tap_coef[:].to_broadcast([P, P]))
 
                 nc.scalar.activation(out=warm_out[:], in_=warm_in[:], func=ACT.Silu)
 
@@ -362,13 +369,12 @@ def tile_slstmblock_pa_e_kernel(
                 def turn_conv(g, r):
                     sums = (3,) if g in CHAINED else (1, 3)
                     conv_bank[(g, r)] = psum.tile([P, PACK, P], F32, name="conv_bank", tag="turn", bufs=3)
-                    for t in range(PACK):
-                        nc.tensor.matmul(out=conv_bank[(g, r)][:, t, :],
-                                         lhsT=vec_rows[:, g * HEAD + t:(g + 1) * HEAD:PACK], rhs=coef_wide[:],
-                                         start=True, stop=False)
-                        for j in sums:
-                            nc.tensor.matmul(out=conv_bank[(g, r)][:, t, :], lhsT=tap_sums[(r, j)][:, t, :],
-                                             rhs=ident_f32[:], is_transpose=True, start=False, stop=j == 3)
+                    nc.tensor.matmul(out=conv_bank[(g, r)][:].rearrange("p t b -> p (t b)"), lhsT=vec_rows[:, g * HEAD:(g + 1) * HEAD:PACK],
+                                     rhs=tap_shift[:].rearrange("p t b -> p (t b)"), start=True, stop=False)
+                    for j in sums:
+                        for t in range(PACK):
+                            nc.tensor.matmul(out=conv_bank[(g, r)][:, t, :], lhsT=tap_sums[(r, j)][:, t, :], rhs=ident_f32[:],
+                                             is_transpose=True, start=False, stop=j == 3 and t == PACK - 1)
 
                 def keep_clock(n):
                     for i in range(n):
@@ -388,6 +394,10 @@ def tile_slstmblock_pa_e_kernel(
                 taps_bank = psum.tile([P, 2, ROWS], F32, name="taps_bank", tag="acc", bufs=2)
                 nc.tensor.matmul(out=taps_bank[:, 0, 0:TAPS], lhsT=tap_coef[:].to_broadcast([P, P]),
                                  rhs=ident_bf16[:, 0:TAPS], start=True, stop=True)
+                for t in range(PACK):
+                    nc.tensor.matmul(out=taps_bank[:, 1, t:t + 1], lhsT=ident_wide[:, PACK - t:PACK - t + P], rhs=tap_coef[:],
+                                     start=True, stop=True)
+                nc.scalar.copy(out=tap_shift[:], in_=taps_bank[:, 1, 0:PACK].unsqueeze(2).to_broadcast([P, PACK, P]))
                 grouped_h = [words_to_partitions(h_sb, g) for g in range(2)]
                 centre(0)
                 for r in range(ROW_TILES):
@@ -397,9 +407,17 @@ def tile_slstmblock_pa_e_kernel(
                 for g in range(2, HEADS):
                     grouped_h.append(words_to_partitions(h_sb, g))
                     keep_clock(1)
-                bias_bank = psum.tile([P, HEAD], F32, name="bias_bank", tag="turn", bufs=3)
-                nc.tensor.matmul(out=bias_bank[:, 0:P // 2], lhsT=bias_rows[:],
-                                 rhs=bias_pick[:].rearrange("p q c -> p (q c)"), start=True, stop=True)
+                bias_bank = {}
+
+                def sum_biases(a, tag, bufs):
+                    bias_bank[a] = psum.tile([P, HEAD], F32, name="bias_bank", tag=tag, bufs=bufs)
+                    nc.tensor.matmul(out=bias_bank[a][:, 0:P // 4], lhsT=bias_rows[:, a, :],
+                                     rhs=bias_pick[:, a, :, :].rearrange("p q c -> p (q c)"), start=True, stop=True)
+
+                def keep_biases(a):
+                    nc.vector.tensor_copy(out=bias_cols[:, 2 * a:2 * a + 2, :].rearrange("p q c -> p (q c)"), in_=bias_bank[a][:, 0:P // 4])
+
+                sum_biases(0, "turn", 3)
                 centre(1)
                 for g in range(HEADS):
                     quantise(grouped_x[g], "x", g)
@@ -407,7 +425,7 @@ def tile_slstmblock_pa_e_kernel(
                 conv_head(0)
                 for r in range(ROW_TILES):
                     taps_even(1, r)
-                nc.vector.tensor_copy(out=bias_cols[:].rearrange("p q c -> p (q c)"), in_=bias_bank[:, 0:P // 2])
+                keep_biases(0)
                 spread_gain(3)
                 for g in range(HEADS):
                     quantise(grouped_h[g], "h", g)
@@ -421,6 +439,8 @@ def tile_slstmblock_pa_e_kernel(
                         for pair in range(BLOCKS // 2):
                             forget_minus_input(0, pair)
                     quantise(grouped_c[g - 1], "c", g - 1)
+                    if g == 2:
+                        keep_biases(1)
                     silu_head(g)
                     if g == 2:
                         gates(0, ("o",))
@@ -428,6 +448,7 @@ def tile_slstmblock_pa_e_kernel(
                         gates(0, ("i",))
                         forget_products(0, 0, "a")
                         forget_products(0, 1, "o")
+                        sum_biases(1, "z", 1)
                 difference(0)
                 gates(1, ("i",), True)
                 for pair in range(BLOCKS // 2):
@@ -460,7 +481,7 @@ def tile_slstmblock_pa_e_kernel(
                 if c > 0:
                     gate_output(c - 1)
                 nc.vector.tensor_tensor(out=fresh[c][:, 0, :], in0=banks["z"][:], in1=fresh[c][:, 1, :], op=ALU.mult)
-                m_t = late.tile([P, HEAD], F32, name="m_t", tag="m_t", bufs=2)
+                m_t = late.tile([P, HEAD], F32, name="m_t", tag="m_t", bufs=4)
                 nc.vector.tensor_tensor(out=m_t[:], in0=banks["i"][:], in1=low[c][:], op=ALU.add)
                 nc.sync.dma_start(out=out_3[rows, cols], in_=m_t[:])
                 nc.vector.tensor_tensor(out=state[c][:, 0, :], in0=state[c][:, 0, :], in1=fresh[c][:, 0, :], op=ALU.add)
@@ -498,9 +519,11 @@ def tile_slstmblock_pa_e_kernel(
                     to_rows(c + 1, ("z", "i"))
                 if c + 2 < CHUNKS:
                     gate_exps(c + 2)
+                if c + 3 < CHUNKS and len(coming) > 1:
+                    difference(c + 3)
                 for g, gate in coming[:1]:
                     gates(g, (gate,))
-                if c + 3 < CHUNKS:
+                if c + 3 < CHUNKS and len(coming) < 2:
                     difference(c + 3)
                 for g, gate in coming[1:]:
                     for pair in range(BLOCKS // 2):

from contextlib import ExitStack

import concourse.mybir as mybir
from concourse.masks import make_identity

F32 = mybir.dt.float32
BF16 = mybir.dt.bfloat16
I32 = mybir.dt.int32
U32 = mybir.dt.uint32
U8 = mybir.dt.uint8
FP8X4 = mybir.dt.float8_e4m3fn_x4
ACT = mybir.ActivationFunctionType
ALU = mybir.AluOpType

P = 128
PACK = 4
ROWS = 256
ROW_TILES = ROWS // P
FEATURES = 2048
HEADS = 4
HEAD = FEATURES // HEADS
BLOCKS = HEAD // P
CHUNKS = HEADS * ROW_TILES
TAPS = 4
SCALAR_TAPS = ((0, 2), (0, 2), (0,), (0,))
CHAINED = (2, 3)
PAD = 8

WEIGHTS = ("wz", "wi", "wf", "wo", "rz", "ri", "rf", "ro")
BIAS_GROUPS = (("wz", "wi", "rz", "ri"), ("wf", "wo", "rf", "ro"))
GATES = ("z", "i", "f", "o")
GATE_FUNC = {"z": ACT.Tanh, "i": ACT.Identity, "o": ACT.Tanh}
GATE_SCALE = {"z": 1.0, "i": 1.0, "o": 0.5}

FLOPS = 2 * len(WEIGHTS) * ROWS * FEATURES * HEAD


def tile_slstmblock_pa_e_kernel(
    tc, x, h_prev, c_prev, n_prev, m_prev, ln_g, ln_b, conv_w, conv_b,
    wz_w_words, wz_w_scales, wz_b, wi_w_words, wi_w_scales, wi_b,
    wf_w_words, wf_w_scales, wf_b, wo_w_words, wo_w_scales, wo_b,
    rz_w_words, rz_w_scales, rz_b, ri_w_words, ri_w_scales, ri_b,
    rf_w_words, rf_w_scales, rf_b, ro_w_words, ro_w_scales, ro_b,
    out_0, out_1, out_2, out_3,
):
    nc = tc.nc
    word_bytes = {"wz": wz_w_words, "wi": wi_w_words, "wf": wf_w_words, "wo": wo_w_words,
                  "rz": rz_w_words, "ri": ri_w_words, "rf": rf_w_words, "ro": ro_w_words}
    scale_bytes = {"wz": wz_w_scales, "wi": wi_w_scales, "wf": wf_w_scales, "wo": wo_w_scales,
                   "rz": rz_w_scales, "ri": ri_w_scales, "rf": rf_w_scales, "ro": ro_w_scales}
    biases = {"wz": wz_b, "wi": wi_b, "wf": wf_b, "wo": wo_b,
              "rz": rz_b, "ri": ri_b, "rf": rf_b, "ro": ro_b}

    with ExitStack() as ctx:
        ctx.enter_context(tc.manual_schedule())
        keep = ctx.enter_context(tc.tile_pool(name="keep", bufs=1))
        ring = ctx.enter_context(tc.tile_pool(name="ring", bufs=2))
        psum = ctx.enter_context(tc.psum_pool(name="psum", bufs=1))

        planes = keep.tile([P, len(WEIGHTS), HEAD], U8, name="planes", align_bytes=64)
        codes = {}
        scales = {}
        for name in ("x", "h", "c"):
            codes[name] = keep.tile([P, HEADS * ROWS], U32, name="codes_" + name, align_bytes=64)
            scales[name] = keep.tile([P, HEADS * ROWS], U8, name="scales_" + name, align_bytes=64)
        gate_t = {}
        words_sb = {}
        for name in WEIGHTS:
            words_sb[name] = keep.tile([P, HEADS, HEAD], U32, name="words_" + name, align_bytes=64)
        m_sb = keep.tile([P, ROW_TILES, FEATURES], BF16, name="m_sb")
        cn_sb = keep.tile([P, 2, ROW_TILES, FEATURES], BF16, name="cn_sb")
        ident_f32 = keep.tile([P, P], F32, name="ident_f32")
        ident_wide = keep.tile([P, PACK + P], BF16, name="ident_wide")
        ident_bf16 = ident_wide[:, PACK:PACK + P]
        bias_rows = keep.tile([P, 2, P], BF16, name="bias_rows")
        bias_pick = keep.tile([P, 2, 2, HEADS * BLOCKS], BF16, name="bias_pick")
        bias_cols = keep.tile([P, len(GATES), HEADS * BLOCKS], F32, name="bias_cols")
        tap_coef = keep.tile([P, 1], BF16, name="tap_coef")
        gain_pick = keep.tile([P, 1], BF16, name="gain_pick")
        tap_shift = keep.tile([P, PACK, P], BF16, name="tap_shift")
        stats = keep.tile([P, ROW_TILES, HEADS, 6], F32, name="stats")
        mean_var = keep.tile([P, ROW_TILES, 2], F32, name="mean_var")
        var_eps = keep.tile([P, ROW_TILES], F32, name="var_eps")
        minus_half = keep.tile([P, ROW_TILES], F32, name="minus_half")
        rstd = keep.tile([P, ROW_TILES], F32, name="rstd")
        taps_rstd = keep.tile([P, ROW_TILES, TAPS], F32, name="taps_rstd")
        two_eps = keep.tile([P, 1], F32, name="two_eps")
        clock_zeros = keep.tile([P, P], F32, name="clock_zeros")
        warm_in = keep.tile([P, 1], F32, name="warm_in")
        warm_out = keep.tile([P, 1], F32, name="warm_out")

        def chunk_rows_cols(c):
            g, r = divmod(c, ROW_TILES)
            return g, r, slice(r * P, (r + 1) * P), slice(g * HEAD, (g + 1) * HEAD)

        def load_words(name, first, last):
            nc.sync.dma_start(
                out=words_sb[name][:, first:last, :].bitcast(I32),
                in_=word_bytes[name][first:last].rearrange("g p n t -> p g (n t)").bitcast(I32),
            )

        def load_planes(name):
            w = WEIGHTS.index(name)
            for quad in range(4):
                nc.sync.dma_start(
                    out=planes[32 * quad:32 * quad + 16, w, :].bitcast(I32),
                    in_=scale_bytes[name][:, PACK * quad:PACK * (quad + 1), :].bitcast(I32),
                )

        def mx_pass(acc, name, operand, g, j, start, stop):
            cols = slice(j * P, (j + 1) * P)
            batch = slice(g * ROWS, (g + 1) * ROWS)
            nc.tensor.matmul_mx(
                out=acc,
                lhsT=words_sb[name][:, g, cols].bitcast(FP8X4),
                lhsT_scale=planes[PACK * g:P, WEIGHTS.index(name), cols],
                rhs=codes[operand][:, batch].bitcast(FP8X4),
                rhs_scale=scales[operand][:, batch],
                start=start,
                stop=stop,
            )

        def leave_psum(out, acc, gate, col, on_vector):
            bias = bias_cols[:, GATES.index(gate), col:col + 1]
            if on_vector:
                nc.vector.tensor_scalar(out=out, in0=acc, scalar1=GATE_SCALE[gate], scalar2=bias,
                                        op0=ALU.mult, op1=ALU.add)
            else:
                nc.scalar.activation(out=out, in_=acc, func=GATE_FUNC[gate], bias=bias, scale=GATE_SCALE[gate])

        def products(acc, gate, g, pair):
            operand = "x" if gate in ("z", "o") else "c"
            for s in range(2):
                j = 2 * pair + s
                mx_pass(acc[:, s, :], "w" + gate, operand, g, j, True, False)
                mx_pass(acc[:, s, :], "r" + gate, "h", g, j, False, True)

        def gates(g, names, on_vector=False):
            for gate in names:
                gate_t[(gate, g)] = ring.tile([P, BLOCKS, ROWS], F32, name="gate_t_" + gate, tag="gate_t_" + gate, bufs=2)
                for pair in range(BLOCKS // 2):
                    acc = psum.tile([P, 2, ROWS], F32, name="acc", tag="acc", bufs=2)
                    products(acc, gate, g, pair)
                    for s in range(2):
                        j = 2 * pair + s
                        leave_psum(gate_t[(gate, g)][:, j, :], acc[:, s, :], gate, g * BLOCKS + j, on_vector)

        f_acc = {}

        def forget_products(g, pair, tag, bufs=1):
            f_acc[(g, pair)] = psum.tile([P, 2, ROWS], F32, name="f_acc", tag=tag, bufs=bufs)
            products(f_acc[(g, pair)], "f", g, pair)

        def forget_minus_input(g, pair):
            if pair == 0:
                gate_t[("f", g)] = ring.tile([P, BLOCKS, ROWS], F32, name="gate_t_f", tag="gate_t_f", bufs=2)
            for s in range(2):
                j = 2 * pair + s
                col = g * BLOCKS + j
                nc.vector.scalar_tensor_tensor(
                    out=gate_t[("f", g)][:, j, :], in0=f_acc[(g, pair)][:, s, :],
                    scalar=bias_cols[:, GATES.index("f"), col:col + 1], in1=gate_t[("i", g)][:, j, :],
                    op0=ALU.add, op1=ALU.subtract)

        def quantise(grouped, name, g):
            batch = slice(g * ROWS, (g + 1) * ROWS)
            nc.vector.quantize_mx(
                out=codes[name][:, batch].bitcast(FP8X4),
                scales=scales[name][:, batch],
                in_=grouped[:].rearrange("p b t -> p (b t)"),
            )

        low = {}
        keep_gate = {}
        fresh = {}

        d_banks = {}

        def difference(c):
            g, r, rows, cols = chunk_rows_cols(c)
            d_banks[c] = psum.tile([P, HEAD], F32, name="d_bank", tag="turn", bufs=3)
            nc.tensor.matmul(out=d_banks[c][:], lhsT=ident_bf16, rhs=m_sb[:, r, cols], start=True, stop=False)
            for j in range(BLOCKS):
                nc.tensor.matmul(
                    out=d_banks[c][:, j * P:(j + 1) * P], lhsT=gate_t[("f", g)][:, j, r * P:(r + 1) * P],
                    rhs=ident_f32[:], is_transpose=True, start=False, stop=j == BLOCKS - 1,
                )

        def gate_exps(c):
            low[c] = ring.tile([P, HEAD], F32, name="low", tag="low", bufs=3)
            nc.scalar.activation(out=low[c][:], in_=d_banks[c][:], func=ACT.Relu)
            keep_gate[c] = ring.tile([P, 1, HEAD], F32, name="keep_gate", tag="keep_gate", bufs=3)
            nc.scalar.activation(out=keep_gate[c][:, 0, :], in_=d_banks[c][:], func=ACT.Exp)
            fresh[c] = ring.tile([P, 2, HEAD], F32, name="fresh", tag="fresh", bufs=3)
            nc.scalar.activation(out=fresh[c][:, 1, :], in_=low[c][:], func=ACT.Exp, scale=-1.0)

        grouped_c = {}
        conv_bank = {}

        def silu_head(g):
            grouped_c[g] = ring.tile([P, ROWS, PACK], BF16, name="grouped_c", tag="grouped_c", align_bytes=64)
            for r in range(ROW_TILES):
                nc.scalar.activation(out=grouped_c[g][:, r * P:(r + 1) * P, :],
                                     in_=conv_bank[(g, r)][:].rearrange("p t b -> p b t"), func=ACT.Silu)

        all_banks = {}

        def to_rows(c, names):
            g, r, rows, cols = chunk_rows_cols(c)
            all_banks.setdefault(c, {})
            for gate in names:
                all_banks[c][gate] = psum.tile([P, HEAD], F32, name="bank_" + gate, tag={"z": "z", "i": "a", "o": "o"}[gate])
                for j in range(BLOCKS):
                    nc.tensor.transpose(out=all_banks[c][gate][:, j * P:(j + 1) * P],
                                        in_=gate_t[(gate, g)][:, j, r * P:(r + 1) * P],
                                        identity=ident_f32[:])

        with tc.tile_pool(name="pre", bufs=1) as pre:
            x_sb = pre.tile([P, ROW_TILES, FEATURES], BF16, name="x_sb")
            vec_rows = pre.tile([P, FEATURES], BF16, name="vec_rows")
            gain_rows = pre.tile([P, FEATURES], BF16, name="gain_rows")

            if True:
                h_sb = pre.tile([P, ROW_TILES, FEATURES], BF16, name="h_sb")
                centred = pre.tile([P, ROW_TILES, PAD + FEATURES], F32, name="centred")

                nc.vector.memset(bias_rows[:].rearrange("p a f -> p (a f)").bitcast(I32), 0)
                nc.vector.memset(clock_zeros[:], 0.0)
                nc.vector.memset(warm_in[:], 1.0)
                nc.vector.memset(vec_rows[:].bitcast(I32), 0)
                nc.vector.memset(tap_coef[:], 0.0)
                nc.vector.memset(gain_pick[:], 0.0)
                nc.vector.memset(gain_pick[0:1, :], 1.0)
                nc.vector.memset(two_eps[:], 2.0e-6)
                nc.vector.memset(centred[:, :, 0:PAD], 0.0)

                nc.gpsimd.memset(gain_rows[:].bitcast(I32), 0)
                make_identity(nc, ident_f32[:])
                nc.gpsimd.memset(planes[:].rearrange("p w n -> p (w n)").bitcast(I32), 0)
                nc.gpsimd.memset(vec_rows[32:32 + PACK, :], 1.0)
                nc.gpsimd.memset(minus_half[:], -0.5)
                nc.gpsimd.memset(ident_wide[:, 0:PACK], 0.0)
                make_identity(nc, ident_bf16)
                for a in range(2):
                    nc.gpsimd.tensor_tensor(out=bias_pick[:, a, :, :].rearrange("p q c -> p (q c)"), in0=ident_bf16[:, 0:P // 4],
                                            in1=ident_bf16[:, P // 4:P // 2], op=ALU.add)
                nc.gpsimd.tensor_scalar(out=bias_pick[:, 1, 1, :], in0=bias_pick[:, 1, 1, :], scalar1=GATE_SCALE["o"],
                                        scalar2=0.0, op0=ALU.mult, op1=ALU.add)

                half = FEATURES // 2
                for r in range(ROW_TILES):
                    nc.sync.dma_start(out=x_sb[:, r, 0:half], in_=x[r * P:(r + 1) * P, 0:half])
                nc.sync.dma_start(out=x_sb[:, :, half:FEATURES], in_=x[:, half:FEATURES].rearrange("(r p) d -> p r d", p=P))

                def load_biases(group):
                    for i, name in enumerate(BIAS_GROUPS[group]):
                        nc.sync.dma_start(out=bias_rows[16 * i:16 * (i + 1), group, :], in_=biases[name].rearrange("(c f) -> c f", f=P))

                load_biases(0)
                nc.sync.dma_start(out=gain_rows[0:1, :], in_=ln_g.rearrange("(o d) -> o d", o=1))
                nc.sync.dma_start(out=h_sb[:], in_=h_prev.rearrange("(r p) d -> p r d", p=P))
                nc.sync.dma_start(out=tap_coef[0:TAPS, :], in_=conv_w.rearrange("(k o) -> k o", o=1))
                nc.sync.dma_start(out=tap_coef[32:33, :], in_=conv_b.rearrange("(k o) -> k o", o=1))
                for s in range(TAPS + PACK - 1):
                    shift = s - (TAPS - 1)
                    nc.sync.dma_start(
                        out=vec_rows[s:s + 1, max(0, -shift):FEATURES - max(0, shift)],
                        in_=ln_b.rearrange("(o d) -> o d", o=1)[:, max(0, shift):FEATURES - max(0, -shift)],
                    )
                for name in ("wz", "rz", "wi", "ri", "wf", "rf"):
                    load_words(name, 0, 2)
                    load_planes(name)
                load_biases(1)
                for name in ("wo", "ro"):
                    load_words(name, 0, 2)
                    load_planes(name)
                nc.sync.dma_start(out=m_sb[:], in_=m_prev.rearrange("(r p) d -> p r d", p=P))
                for s, state in enumerate((c_prev, n_prev)):
                    nc.sync.dma_start(out=cn_sb[:, s, :, :], in_=state.rearrange("(r p) d -> p r d", p=P))
                for name in ("wi", "ri", "wf", "rf", "wz", "rz", "wo", "ro"):
                    load_words(name, 2, HEADS)

                nc.scalar.activation(out=warm_out[:], in_=warm_in[:], func=ACT.Silu)

                gain_bank = {}

                def spread_gain(g):
                    cols = slice(g * HEAD, (g + 1) * HEAD)
                    gain_bank[g] = psum.tile([P, HEAD], F32, name="gain_bank", tag=("z", "a", "o")[g % 3])
                    nc.tensor.matmul(out=gain_bank[g][:], lhsT=gain_pick[:].to_broadcast([P, P]),
                                     rhs=gain_rows[:, cols], start=True, stop=True)

                def words_to_partitions(src, g):
                    bank = psum.tile([P, 2, ROWS], F32, name="word_bank", tag="turn", bufs=3)
                    for r in range(ROW_TILES):
                        src_words = src[:, r, :].bitcast(F32)
                        for u in range(2):
                            nc.tensor.transpose(
                                out=bank[:, u, r * P:(r + 1) * P],
                                in_=src_words[:, (HEAD // 2) * g + u:(HEAD // 2) * (g + 1):2],
                                identity=ident_f32[:],
                            )
                    grouped = pre.tile([P, ROWS, PACK], BF16, name="grouped", tag="sorted", bufs=8,
                                         align_bytes=64)
                    nc.scalar.copy(out=grouped[:].bitcast(F32), in_=bank[:].rearrange("p u b -> p b u"))
                    return grouped

                def row_stats():
                    for half in range(2):
                        for r in range(ROW_TILES):
                            for g in range(half * HEADS // 2, (half + 1) * HEADS // 2):
                                nc.vector.bn_stats(out=stats[:, r, g, :], in_=x_sb[:, r, g * HEAD:(g + 1) * HEAD])
                    for r in range(ROW_TILES):
                        nc.vector.bn_aggr(out=mean_var[:, r, :], in_=stats[:, r, :, :].rearrange("p g s -> p (g s)"))

                def centre(g):
                    for r in range(ROW_TILES):
                        nc.vector.scalar_tensor_tensor(
                            out=centred[:, r, PAD + g * HEAD:PAD + (g + 1) * HEAD],
                            in0=x_sb[:, r, g * HEAD:(g + 1) * HEAD], scalar=mean_var[:, r, 0:1],
                            in1=gain_bank[g][:], op0=ALU.subtract, op1=ALU.mult,
                        )

                even_taps = {}
                tap_sums = {}

                def moved(g, r, j):
                    first = PAD + g * HEAD + j - (TAPS - 1)
                    return centred[:, r, first:first + HEAD]

                def taps_even(g, r):
                    for j in (0,) if g in CHAINED else (0, 2):
                        even_taps[(r, j)] = pre.tile([P, HEAD], F32, name="even_taps", tag="even_taps", bufs=4)
                        if j in SCALAR_TAPS[g]:
                            nc.scalar.activation(out=even_taps[(r, j)][:], in_=moved(g, r, j), func=ACT.Copy,
                                                 scale=taps_rstd[:, r, j:j + 1])
                        else:
                            nc.vector.tensor_scalar_mul(out=even_taps[(r, j)][:], in0=moved(g, r, j),
                                                        scalar1=taps_rstd[:, r, j:j + 1])

                def add_tap(g, r, j, base):
                    nc.vector.scalar_tensor_tensor(out=even_taps[(r, base)][:], in0=moved(g, r, j), scalar=taps_rstd[:, r, j:j + 1],
                                                   in1=even_taps[(r, base)][:], op0=ALU.mult, op1=ALU.add)

                def last_tap(g, r, j, base):
                    tap_sums[(r, j)] = pre.tile([P, PACK, P], F32, name="tap_sums", tag="sorted", bufs=8, align_bytes=64)
                    nc.vector.scalar_tensor_tensor(
                        out=tap_sums[(r, j)][:].rearrange("p t q -> p q t"),
                        in0=moved(g, r, j).rearrange("p (q t) -> p q t", t=PACK),
                        scalar=taps_rstd[:, r, j:j + 1],
                        in1=even_taps[(r, base)][:].rearrange("p (q t) -> p q t", t=PACK),
                        op0=ALU.mult, op1=ALU.add)

                def conv_head(g):
                    if g in CHAINED:
                        for j in (1, 2):
                            for r in range(ROW_TILES):
                                add_tap(g, r, j, 0)
                    for r in range(ROW_TILES):
                        if g in CHAINED:
                            last_tap(g, r, 3, 0)
                        else:
                            for j in (1, 3):
                                last_tap(g, r, j, j - 1)
                        turn_conv(g, r)
                        if 0 < g < HEADS - 1:
                            taps_even(g + 1, r)

                def turn_conv(g, r):
                    sums = (3,) if g in CHAINED else (1, 3)
                    conv_bank[(g, r)] = psum.tile([P, PACK, P], F32, name="conv_bank", tag="turn", bufs=3)
                    nc.tensor.matmul(out=conv_bank[(g, r)][:].rearrange("p t b -> p (t b)"), lhsT=vec_rows[:, g * HEAD:(g + 1) * HEAD:PACK],
                                     rhs=tap_shift[:].rearrange("p t b -> p (t b)"), start=True, stop=False)
                    for j in sums:
                        for t in range(PACK):
                            nc.tensor.matmul(out=conv_bank[(g, r)][:, t, :], lhsT=tap_sums[(r, j)][:, t, :], rhs=ident_f32[:],
                                             is_transpose=True, start=False, stop=j == 3 and t == PACK - 1)

                def keep_clock(n):
                    for i in range(n):
                        clock_bank = psum.tile([P, 2, ROWS], F32, name="clock_bank", tag="acc", bufs=2)
                        nc.tensor.matmul(out=clock_bank[:, 0, 0:P], lhsT=clock_zeros[:], rhs=clock_zeros[:], start=True, stop=True)

                keep_clock(4)
                row_stats()
                nc.vector.tensor_scalar_add(out=var_eps[:], in0=mean_var[:, :, 1], scalar1=1.0e-5)
                nc.gpsimd.tensor_tensor(out=rstd[:], in0=var_eps[:], in1=minus_half[:], op=ALU.pow)
                grouped_x = []
                for g in range(HEADS):
                    grouped_x.append(words_to_partitions(x_sb, g))
                    keep_clock(1)
                for g in range(3):
                    spread_gain(g)
                taps_bank = psum.tile([P, 2, ROWS], F32, name="taps_bank", tag="acc", bufs=2)
                nc.tensor.matmul(out=taps_bank[:, 0, 0:TAPS], lhsT=tap_coef[:].to_broadcast([P, P]),
                                 rhs=ident_bf16[:, 0:TAPS], start=True, stop=True)
                for t in range(PACK):
                    nc.tensor.matmul(out=taps_bank[:, 1, t:t + 1], lhsT=ident_wide[:, PACK - t:PACK - t + P], rhs=tap_coef[:],
                                     start=True, stop=True)
                nc.scalar.copy(out=tap_shift[:], in_=taps_bank[:, 1, 0:PACK].unsqueeze(2).to_broadcast([P, PACK, P]))
                grouped_h = [words_to_partitions(h_sb, g) for g in range(2)]
                centre(0)
                for r in range(ROW_TILES):
                    nc.vector.tensor_scalar_mul(out=taps_rstd[:, r, :], in0=taps_bank[:, 0, 0:TAPS], scalar1=rstd[:, r:r + 1])
                for r in range(ROW_TILES):
                    taps_even(0, r)
                for g in range(2, HEADS):
                    grouped_h.append(words_to_partitions(h_sb, g))
                    keep_clock(1)
                bias_bank = {}

                def sum_biases(a, tag, bufs):
                    bias_bank[a] = psum.tile([P, HEAD], F32, name="bias_bank", tag=tag, bufs=bufs)
                    nc.tensor.matmul(out=bias_bank[a][:, 0:P // 4], lhsT=bias_rows[:, a, :],
                                     rhs=bias_pick[:, a, :, :].rearrange("p q c -> p (q c)"), start=True, stop=True)

                def keep_biases(a):
                    nc.vector.tensor_copy(out=bias_cols[:, 2 * a:2 * a + 2, :].rearrange("p q c -> p (q c)"), in_=bias_bank[a][:, 0:P // 4])

                sum_biases(0, "turn", 3)
                centre(1)
                for g in range(HEADS):
                    quantise(grouped_x[g], "x", g)
                keep_clock(2)
                conv_head(0)
                for r in range(ROW_TILES):
                    taps_even(1, r)
                keep_biases(0)
                spread_gain(3)
                for g in range(HEADS):
                    quantise(grouped_h[g], "h", g)
                silu_head(0)
                gates(0, ("z",))
                for g in range(1, HEADS):
                    if g + 1 < HEADS:
                        centre(g + 1)
                    conv_head(g)
                    if g == 3:
                        for pair in range(BLOCKS // 2):
                            forget_minus_input(0, pair)
                    quantise(grouped_c[g - 1], "c", g - 1)
                    if g == 2:
                        keep_biases(1)
                    silu_head(g)
                    if g == 2:
                        gates(0, ("o",))
                    if g == 1:
                        gates(0, ("i",))
                        forget_products(0, 0, "a")
                        forget_products(0, 1, "o")
                        sum_biases(1, "z", 1)
                difference(0)
                gates(1, ("i",), True)
                for pair in range(BLOCKS // 2):
                    forget_products(1, pair, "acc", 2)
                    forget_minus_input(1, pair)
                gate_exps(0)
                quantise(grouped_c[3], "c", 3)
                to_rows(0, ("z", "i", "o"))
                gates(1, ("z",))
                difference(1)
                gate_exps(1)
                gates(1, ("o",))
                difference(2)

        with tc.tile_pool(name="late", bufs=1, reuse_waits="tile") as late:
            state = {}
            oc_all = late.tile([P, CHUNKS, HEAD], F32, name="oc_all")

            def gate_output(c):
                nc.vector.scalar_tensor_tensor(out=oc_all[:, c, :], in0=all_banks[c]["o"][:], scalar=1.0,
                                               in1=state[c][:, 0, :], op0=ALU.add, op1=ALU.mult)

            def update(c):
                g, r, rows, cols = chunk_rows_cols(c)
                banks = all_banks[c]
                state[c] = late.tile([P, 2, HEAD], F32, name="state", tag="state", bufs=CHUNKS)
                nc.vector.scalar_tensor_tensor(out=state[c][:], in0=keep_gate[c][:].to_broadcast([P, 2, HEAD]), scalar=1.0,
                                               in1=cn_sb[:, :, r, cols], op0=ALU.min, op1=ALU.mult)
                nc.gpsimd.tensor_tensor(out=state[c][:, 1, :], in0=state[c][:, 1, :], in1=fresh[c][:, 1, :], op=ALU.add)
                if c > 0:
                    gate_output(c - 1)
                nc.vector.tensor_tensor(out=fresh[c][:, 0, :], in0=banks["z"][:], in1=fresh[c][:, 1, :], op=ALU.mult)
                m_t = late.tile([P, HEAD], F32, name="m_t", tag="m_t", bufs=4)
                nc.vector.tensor_tensor(out=m_t[:], in0=banks["i"][:], in1=low[c][:], op=ALU.add)
                nc.sync.dma_start(out=out_3[rows, cols], in_=m_t[:])
                nc.vector.tensor_tensor(out=state[c][:, 0, :], in0=state[c][:, 0, :], in1=fresh[c][:, 0, :], op=ALU.add)
                nc.sync.dma_start(out=out_1[rows, cols], in_=state[c][:, 0, :])
                nc.sync.dma_start(out=out_2[rows, cols], in_=state[c][:, 1, :])
                if c in forget_at:
                    for pair in range(BLOCKS // 2):
                        forget_minus_input(forget_at[c], pair)

            recip = {}
            forget_at = {1: 2, 3: 3}

            def inverse_root(c):
                recip[c] = late.tile([P, HEAD], F32, name="recip", tag="recip", bufs=6)
                nc.scalar.activation(out=recip[c][:], in_=state[c][:, 1, :], func=ACT.Abs_reciprocal_sqrt,
                                     bias=two_eps[:, 0:1], scale=2.0)

            def inverse(c):
                nc.scalar.activation(out=recip[c][:], in_=recip[c][:], func=ACT.Square)

            def times_recip(c):
                nc.vector.tensor_tensor(out=oc_all[:, c, :], in0=oc_all[:, c, :], in1=recip[c][:], op=ALU.mult)

            def store_h(c):
                g, r, rows, cols = chunk_rows_cols(c)
                nc.sync.dma_start(out=out_0[rows, cols], in_=oc_all[:, c, :])

            gates_at = {0: ((2, "i"), (2, "f")), 1: ((2, "z"),), 2: ((3, "i"), (3, "f")), 3: ((2, "o"),), 4: ((3, "z"),), 5: ((3, "o"),)}
            for c in range(CHUNKS):
                update(c)
                coming = gates_at.get(c, ())
                if c > 0:
                    to_rows(c, ("o",))
                if c + 1 < CHUNKS:
                    to_rows(c + 1, ("z", "i"))
                if c + 2 < CHUNKS:
                    gate_exps(c + 2)
                if c + 3 < CHUNKS and len(coming) > 1:
                    difference(c + 3)
                for g, gate in coming[:1]:
                    gates(g, (gate,))
                if c + 3 < CHUNKS and len(coming) < 2:
                    difference(c + 3)
                for g, gate in coming[1:]:
                    for pair in range(BLOCKS // 2):
                        forget_products(g, pair, "turn", 3)
            for c in range(ROW_TILES):
                inverse_root(c)
            for c in (0, 1, 0, 1):
                times_recip(c)
            for c in range(ROW_TILES):
                store_h(c)
            inverse_root(2)
            for c in range(2, CHUNKS):
                if c + 1 < CHUNKS:
                    inverse_root(c + 1)
                inverse(c)
                times_recip(c)
                store_h(c)
                if c == 2:
                    gate_output(CHUNKS - 1)
